import numpy as np
import ml_dtypes


def mxq(x, axis, fmt="e4m3"):
    dtype, down = {"e4m3": (ml_dtypes.float8_e4m3fn, 7), "e5m2": (ml_dtypes.float8_e5m2, 14)}[fmt]
    v = np.moveaxis(np.asarray(x, np.float32).astype(ml_dtypes.bfloat16).astype(np.float64), axis, -1)
    blocks = v.reshape(v.shape[:-1] + (-1, 32))
    amax = np.abs(blocks).max(-1, keepdims=True)
    byte = np.maximum(np.where(amax > 0, np.frexp(amax)[1] - 1 + 127, 0) - down, 1)
    scale = np.exp2(byte - 127.0)
    codes = (blocks / scale).astype(np.float32).astype(dtype).astype(np.float64)
    return np.moveaxis((codes * scale).reshape(v.shape), -1, axis)


WIDE = False


def mx_kscale(k):
    if not WIDE:
        return np.ones(k)
    levels = np.array([10, -10, 5, -5, 0])
    a = np.random.permutation(np.resize(levels, k // 512 * 4)).reshape(k // 512, 4)
    idx = np.arange(k)
    return np.exp2(a[idx // 512, idx % 128 // 32])


BF16 = ml_dtypes.bfloat16


def bf(x):
    return np.asarray(x, np.float32).astype(BF16)


def f64(x):
    return np.asarray(x).astype(np.float64)


B, CIN, CO, H, W, G, KT, KF = 1, 512, 128, 128, 128, 8, 3, 3
CG = CO // G
HALF = CO // 2
WIN = KT * KF
A = np.sqrt(1.5) / (2.0 * CG) ** 0.25


def unfold(t):
    wins = [t[:, :, i:i + H, j:j + W] for i in range(KT) for j in range(KF)]
    return np.stack(wins, axis=-1).reshape(B, CO, H, W, KT, KF)


def setup_inputs():
    s = mx_kscale(CIN)
    return {
        "x": bf(np.random.standard_normal((B, CIN, H, W)) * s[None, :, None, None]),
        "Wq": bf(np.random.standard_normal((CO, CIN)) * A / np.sqrt(CIN) / s[None, :]),
        "Wk": bf(np.random.standard_normal((CO, CIN)) * A / np.sqrt(CIN) / s[None, :]),
        "Wv": bf(np.random.standard_normal((CO, CIN)) / np.sqrt(CIN) / s[None, :]),
        "rel_t": bf(np.random.standard_normal((HALF, KT)) * A),
        "rel_f": bf(np.random.standard_normal((HALF, KF)) * A),
    }


def reference(x, Wq, Wk, Wv, rel_t, rel_f):
    pt, pf = (KT - 1) // 2, (KF - 1) // 2
    xq = mxq(f64(x).reshape(B, CIN, H * W), 1, "e4m3")
    q = (mxq(f64(Wq), 1, "e4m3") @ xq).reshape(B, CO, H, W)
    k = (mxq(f64(Wk), 1, "e4m3") @ xq).reshape(B, CO, H, W)
    v = (mxq(f64(Wv), 1, "e4m3") @ xq).reshape(B, CO, H, W)
    pad = ((0, 0), (0, 0), (pt, pt), (pf, pf))
    kw = unfold(np.pad(k, pad))
    vw = unfold(np.pad(v, pad))
    kw = np.concatenate([
        kw[:, :HALF] + f64(rel_t)[None, :, None, None, :, None],
        kw[:, HALF:] + f64(rel_f)[None, :, None, None, None, :],
    ], axis=1)
    kw = kw.reshape(B, G, CG, H, W, WIN)
    vw = vw.reshape(B, G, CG, H, W, WIN)
    qg = q.reshape(B, G, CG, H, W, 1)
    energy = np.sum(qg * kw, axis=2)
    e = np.exp(energy - energy.max(-1, keepdims=True))
    attn = e / e.sum(-1, keepdims=True)
    out = np.sum(attn[:, :, None] * vw, axis=-1)
    return out.reshape(B, CO, H, W), attn

@@ -1,0 +1,322 @@
+from contextlib import ExitStack
+
+import concourse.masks as masks
+import concourse.mybir as mybir
+
+F32 = mybir.dt.float32
+BF16 = mybir.dt.bfloat16
+U32 = mybir.dt.uint32
+U8 = mybir.dt.uint8
+FP8X4 = mybir.dt.float8_e4m3fn_x4
+ALU = mybir.AluOpType
+ACT = mybir.ActivationFunctionType
+AX = mybir.AxisListType
+
+P = 128
+H = 128
+W = 128
+NG = 8
+CG = 16
+WIN = 9
+R = 4
+NB = H // R
+PIX = R * W
+RK = 16
+RV = 32
+MAC = 16
+CHUNK = 2
+NCHUNK = NB // CHUNK
+RAW_BUFS = 4
+NGROUPS = ((0, 4), (4, 4), (8, 1))
+QN = 8
+
+FLOPS = 2 * 3 * 128 * 512 * H * W + 2 * 2 * WIN * 128 * H * W
+
+
+def ring_runs(first, count, ring):
+    runs = []
+    done = 0
+    while done < count:
+        slot = (first + done) % ring
+        n = min(count - done, ring - slot)
+        runs.append((done, slot, n))
+        done += n
+    return runs
+
+
+def tile_mutliheadattention2d_kernel(tc, x, Wq, Wk, Wv, rel_t, rel_f, out_0, out_1):
+    nc = tc.nc
+    with ExitStack() as ctx:
+        const = ctx.enter_context(tc.tile_pool(name="const", bufs=1))
+        rawp = ctx.enter_context(tc.tile_pool(name="rawp", bufs=RAW_BUFS))
+        grpp = ctx.enter_context(tc.tile_pool(name="grpp", bufs=3))
+        codp = ctx.enter_context(tc.tile_pool(name="codp", bufs=3))
+        prodp = ctx.enter_context(tc.tile_pool(name="prodp", bufs=2))
+        smallp = ctx.enter_context(tc.tile_pool(name="smallp", bufs=3))
+        outp = ctx.enter_context(tc.tile_pool(name="outp", bufs=2))
+        psum = ctx.enter_context(tc.psum_pool(name="psum", bufs=1))
+
+        xv = x.rearrange("b (p j) h w -> p (b j) (h w)", j=4)
+        o0 = out_0.rearrange("b o h w -> (b o) (h w)")
+        o1 = out_1.rearrange("b g h w n -> (b g) h (w n)")
+
+        raw = {}
+
+        def load(c):
+            t_raw = rawp.tile([P, 4, CHUNK * PIX], BF16, name="raw")
+            nc.sync.dma_start(out=t_raw[:], in_=xv[:, :, c * CHUNK * PIX:(c + 1) * CHUNK * PIX])
+            raw[c] = t_raw
+
+        w_raw = []
+        for idx, wsrc in enumerate((Wq, Wk, Wv)):
+            t_w = const.tile([P, 512], BF16, name="w_raw%d" % idx)
+            nc.sync.dma_start(out=t_w[:], in_=wsrc)
+            w_raw.append(t_w)
+        load(0)
+        rel_sb = const.tile([P, 3], BF16, name="rel_sb")
+        nc.sync.dma_start(out=rel_sb[0:64, :], in_=rel_t)
+        nc.sync.dma_start(out=rel_sb[64:128, :], in_=rel_f)
+        for c in range(1, RAW_BUFS):
+            load(c)
+
+        ident_f = const.tile([P, P], F32, name="ident_f")
+        masks.make_identity(nc, ident_f[:])
+        ident_b = const.tile([P, P], BF16, name="ident_b")
+        masks.make_identity(nc, ident_b[:])
+        perm0 = const.tile([P, P], F32, name="perm0")
+        perm2 = const.tile([P, P], F32, name="perm2")
+        shl0 = const.tile([P, P], F32, name="shl0")
+        shl2 = const.tile([P, P], F32, name="shl2")
+        nc.vector.tensor_copy(out=perm0[:, 1:P], in_=ident_f[:, 0:P - 1])
+        nc.vector.tensor_copy(out=perm0[:, 0:1], in_=ident_f[:, P - 1:P])
+        nc.vector.tensor_copy(out=perm2[:, 0:P - 1], in_=ident_f[:, 1:P])
+        nc.vector.tensor_copy(out=perm2[:, P - 1:P], in_=ident_f[:, 0:1])
+        nc.vector.tensor_copy(out=shl0[:, 0:P - 1], in_=ident_f[:, 1:P])
+        nc.vector.memset(shl0[:, P - 1:P], 0.0)
+        nc.vector.tensor_copy(out=shl2[:, 1:P], in_=ident_f[:, 0:P - 1])
+        nc.vector.memset(shl2[:, 0:1], 0.0)
+        perms = (perm0, ident_f, perm2)
+        gsum = const.tile([P, NG], F32, name="gsum")
+        nc.vector.tensor_reduce(out=gsum[:], in_=ident_f[:].rearrange("p (g c) -> p g c", c=CG), axis=AX.X, op=ALU.add)
+        r9 = const.tile([P, WIN], F32, name="r9")
+        nc.vector.tensor_copy(out=r9[0:64, :].rearrange("p (i j) -> p i j", j=3),
+                              in_=rel_sb[0:64, :].unsqueeze(2).to_broadcast([64, 3, 3]))
+        nc.vector.tensor_copy(out=r9[64:128, :].rearrange("p (i j) -> p i j", j=3),
+                              in_=rel_sb[64:128, :].unsqueeze(1).to_broadcast([64, 3, 3]))
+        k_ring = const.tile([P, RK, W + 2], F32, name="k_ring")
+        nc.gpsimd.memset(k_ring[:], 0.0)
+        v_ring = const.tile([P, RV, P], F32, name="v_ring")
+
+        w_codes = []
+        w_scales = []
+        for idx in range(3):
+            w_de = const.tile([P, 4, P], BF16, name="w_de%d" % idx)
+            nc.vector.tensor_copy(out=w_de[:], in_=w_raw[idx][:].rearrange("o (p t) -> o t p", t=4))
+            w_ps = psum.tile([P, 4, P], BF16, name="w_ps", tag="tps")
+            for t in range(4):
+                nc.tensor.transpose(w_ps[:, t, :], w_de[:, t, :], ident_b[:])
+            w_grp = const.tile([P, P, 4], BF16, name="w_grp%d" % idx, align_bytes=64)
+            nc.vector.tensor_copy(out=w_grp[:], in_=w_ps[:].rearrange("p t o -> p o t"))
+            w_c = const.tile([P, P], U32, name="w_c%d" % idx, align_bytes=64)
+            w_s = const.tile([P, P], U8, name="w_s%d" % idx, align_bytes=64)
+            nc.vector.quantize_mx(out=w_c[:].bitcast(FP8X4), scales=w_s[:], in_=w_grp[:].rearrange("p o t -> p (o t)"))
+            w_codes.append(w_c)
+            w_scales.append(w_s)
+
+        grp = {}
+        xc = {}
+        xs = {}
+        q_ps = {}
+        prod = {}
+        e_ps = {}
+        dif = {}
+        a16 = {}
+        sh_ps = {}
+        sh_sb = {}
+        avp = {}
+
+        def regroup(b):
+            t_g = grpp.tile([P, PIX, 4], BF16, name="grp", align_bytes=64)
+            src = raw[b // CHUNK][:, :, (b % CHUNK) * PIX:(b % CHUNK + 1) * PIX]
+            nc.scalar.copy(out=t_g[:].rearrange("p (c i) t -> p c t i", i=4),
+                           in_=src.rearrange("p t (c i) -> p c t i", i=4))
+            grp[b] = t_g
+            if b % CHUNK == CHUNK - 1 and b // CHUNK + RAW_BUFS < NCHUNK:
+                load(b // CHUNK + RAW_BUFS)
+
+        def quant(b):
+            t_c = codp.tile([P, PIX], U32, name="xc", align_bytes=64)
+            t_s = codp.tile([P, PIX], U8, name="xs", align_bytes=64)
+            nc.vector.quantize_mx(out=t_c[:].bitcast(FP8X4), scales=t_s[:], in_=grp[b][:].rearrange("p c t -> p (c t)"))
+            xc[b] = t_c
+            xs[b] = t_s
+
+        def mx_w_stationary(dst, widx, b):
+            nc.tensor.matmul_mx(out=dst, lhsT=w_codes[widx][:].bitcast(FP8X4), lhsT_scale=w_scales[widx][:],
+                                rhs=xc[b][:].bitcast(FP8X4), rhs_scale=xs[b][:], start=True, stop=True)
+
+        def mx_kv(b):
+            k_ps = psum.tile([P, R, W], F32, name="k_ps", tag="kps")
+            mx_w_stationary(k_ps[:].rearrange("p r w -> p (r w)"), 1, b)
+            v_ps = psum.tile([P, R, P], F32, name="v_ps", tag="vps")
+            for r in range(R):
+                cols = slice(r * W, (r + 1) * W)
+                nc.tensor.matmul_mx(out=v_ps[:, r, :], lhsT=xc[b][:, cols].bitcast(FP8X4), lhsT_scale=xs[b][:, cols],
+                                    rhs=w_codes[2][:].bitcast(FP8X4), rhs_scale=w_scales[2][:], start=True, stop=True)
+            ks = (b * R) % RK
+            nc.scalar.copy(out=k_ring[:, ks:ks + R, 1:W + 1], in_=k_ps[:])
+            vs = (b * R) % RV
+            nc.scalar.copy(out=v_ring[:, vs:vs + R, :], in_=v_ps[:])
+
+        def mx_q(b):
+            t_q = psum.tile([P, R, W], F32, name="q_ps", tag="qps", bufs=2)
+            mx_w_stationary(t_q[:].rearrange("p r w -> p (r w)"), 0, b)
+            q_ps[b] = t_q
+
+        def qk(b, filler):
+            h0 = b * R
+            if b == NB - 1:
+                nc.vector.memset(k_ring[:, H % RK, :], 0.0)
+            t_p = prodp.tile([P, WIN, R, W], F32, name="prod")
+            t_e = psum.tile([P, WIN, NG, R], F32, name="e_ps", tag="eps")
+            for i in range(3):
+                runs = ring_runs(h0 + i - 1, R, RK)
+                for j in range(3):
+                    n = 3 * i + j
+                    for off, slot, cnt in runs:
+                        nc.vector.scalar_tensor_tensor(
+                            out=t_p[:, n, off:off + cnt, :], in0=k_ring[:, slot:slot + cnt, j:j + W],
+                            scalar=r9[:, n:n + 1], in1=q_ps[b][:, off:off + cnt, :], op0=ALU.add, op1=ALU.mult)
+                    for r in range(R):
+                        nc.tensor.matmul(out=t_e[:, n, :, r], lhsT=t_p[:, n, r, :], rhs=gsum[:, 0:QN], start=True, stop=True)
+                    filler(R)
+            e_ps[b] = t_e
+
+        def softmax_a(b):
+            t_m = smallp.tile([P, NG * R], F32, name="mx")
+            nc.vector.tensor_reduce(out=t_m[:], in_=e_ps[b][:].rearrange("p n g r -> p (g r) n"), axis=AX.X, op=ALU.max)
+            t_d = smallp.tile([P, WIN, NG * R], F32, name="dif")
+            nc.vector.tensor_tensor(out=t_d[:], in0=e_ps[b][:].rearrange("p n g r -> p n (g r)"),
+                                    in1=t_m[:].unsqueeze(1).to_broadcast([P, WIN, NG * R]), op=ALU.subtract)
+            nc.scalar.activation(out=t_d[:], in_=t_d[:], func=ACT.Exp)
+            dif[b] = t_d
+
+        def softmax_b(b):
+            t_s = smallp.tile([P, NG * R], F32, name="ssum")
+            nc.vector.tensor_reduce(out=t_s[:], in_=dif[b][:].rearrange("p n m -> p m n"), axis=AX.X, op=ALU.add)
+            t_r = smallp.tile([P, NG * R], F32, name="rsum")
+            nc.vector.reciprocal(out=t_r[:], in_=t_s[:])
+            m = b // (MAC // R)
+            if b % (MAC // R) == 0:
+                t_a = outp.tile([P, WIN, NG, MAC], F32, name="a16")
+                a16[m] = t_a
+            hs = (b * R) % MAC
+            nc.gpsimd.tensor_tensor(out=a16[m][:, :, :, hs:hs + R], in0=dif[b][:].rearrange("p n (g r) -> p n g r", r=R),
+                                    in1=t_r[:].rearrange("p (g r) -> p g r", r=R).unsqueeze(1).to_broadcast([P, WIN, NG, R]),
+                                    op=ALU.mult)
+
+        def shift(b):
+            m = b // (MAC // R)
+            hs = (b * R) % MAC
+            t_sh = psum.tile([P, 2, 3, NG, R], F32, name="sh_ps", tag="shps")
+            av = a16[m][:].rearrange("p (i j) g h -> p i j g h", j=3)
+            nc.tensor.matmul(out=t_sh[:, 0], lhsT=shl0[:], rhs=av[:, :, 0, :, hs:hs + R], start=True, stop=True)
+            nc.tensor.matmul(out=t_sh[:, 1], lhsT=shl2[:], rhs=av[:, :, 2, :, hs:hs + R], start=True, stop=True)
+            t_sb = smallp.tile([P, 3, NG, R], F32, name="sh_sb")
+            nc.scalar.copy(out=t_sb[:], in_=t_sh[:, 1])
+            sh_ps[b] = t_sh
+            sh_sb[b] = t_sb
+
+        def av_products(b):
+            h0 = b * R
+            m = b // (MAC // R)
+            hs = (b * R) % MAC
+            t_q = prodp.tile([P, WIN, R, P], F32, name="avp")
+            for j in (0, 1, 2):
+                for i in range(3):
+                    n = 3 * i + j
+                    lo = max(0, 1 - i - h0)
+                    hi = min(R, H + 1 - i - h0)
+                    for off, slot, cnt in ring_runs(h0 + lo + i - 1, hi - lo, RV):
+                        a = lo + off
+                        if j == 0:
+                            att = sh_ps[b][:, 0, i, :, a:a + cnt]
+                        elif j == 1:
+                            att = a16[m][:, n, :, hs + a:hs + a + cnt]
+                        else:
+                            att = sh_sb[b][:, i, :, a:a + cnt]
+                        eng = nc.vector if j == 0 else nc.gpsimd
+                        eng.tensor_tensor(
+                            out=t_q[:, n, a:a + cnt, :].rearrange("p r (g c) -> p r g c", c=CG),
+                            in0=v_ring[:, slot:slot + cnt, :].rearrange("p r (g c) -> p r g c", c=CG),
+                            in1=att.rearrange("p g r -> p r g").unsqueeze(3).to_broadcast([P, cnt, NG, CG]),
+                            op=ALU.mult)
+            avp[b] = t_q
+
+        work = {"todo": [], "pos": 0}
+
+        def av_sum_begin(b):
+            h0 = b * R
+            pending = []
+            work["todo"] = pending
+            work["pos"] = 0
+            t_o = psum.tile([P, R, W], F32, name="o_ps", tag="ops")
+            for r in range(R):
+                terms = [(i, j) for i in range(3) for j in range(3) if 0 <= h0 + r + i - 1 < H]
+                for idx, (i, j) in enumerate(terms):
+                    pending.append((t_o[:, r, :], avp[b][:, 3 * i + j, r, :], perms[j], idx == 0, idx == len(terms) - 1))
+            return t_o
+
+        def av_sum_step(count):
+            todo = work["todo"]
+            for step in range(work["pos"], min(work["pos"] + count, len(todo))):
+                dst, lhs, perm, first, last = todo[step]
+                nc.tensor.matmul(out=dst, lhsT=lhs, rhs=perm[:], start=first, stop=last, is_transpose=True)
+            work["pos"] = min(work["pos"] + count, len(todo))
+
+        def av_sum_end(b, t_o):
+            h0 = b * R
+            av_sum_step(len(work["todo"]))
+            t_sb = outp.tile([P, PIX], F32, name="o_sb")
+            nc.scalar.copy(out=t_sb[:], in_=t_o[:].rearrange("p r w -> p (r w)"))
+            nc.sync.dma_start(out=o0[:, h0 * W:(h0 + R) * W], in_=t_sb[:])
+
+        t_sbs = {}
+
+        def attn_out(m, part):
+            if part == 0:
+                t_new = outp.tile([P, W, WIN], F32, name="t_sb")
+                t_sbs[m] = t_new
+            t_t = t_sbs[m]
+            n0, nn = NGROUPS[part]
+            t_ps = psum.tile([P, 4, W], F32, name="t_ps", tag="tps")
+            for n in range(nn):
+                nc.tensor.transpose(t_ps[:, n, :], a16[m][:, n0 + n, :, :].rearrange("p g h -> p (g h)"), ident_f[:])
+            nc.scalar.copy(out=t_t[:, :, n0:n0 + nn], in_=t_ps[:, 0:nn, :].rearrange("p n w -> p w n"))
+            if part == len(NGROUPS) - 1:
+                for g in range(NG):
+                    nc.sync.dma_start(out=o1[g, m * MAC:(m + 1) * MAC, :],
+                                      in_=t_t[g * MAC:(g + 1) * MAC, :, :].rearrange("p w n -> p (w n)"))
+
+        def run(stage, b):
+            if 0 <= b < NB:
+                stage(b)
+
+        with tc.manual_schedule():
+            for t in range(-4, NB + 8):
+                run(softmax_a, t - 1)
+                run(regroup, t + 4)
+                run(mx_kv, t + 2)
+                run(mx_q, t + 1)
+                run(shift, t - 2)
+                t_o = av_sum_begin(t - 3) if 0 <= t - 3 < NB else None
+                if 0 <= t < NB:
+                    qk(t, av_sum_step)
+                run(av_products, t - 2)
+                run(quant, t + 3)
+                run(softmax_b, t - 1)
+                if t_o is not None:
+                    av_sum_end(t - 3, t_o)
+                mm, part = divmod(t - 5, MAC // R)
+                if 0 <= mm < H // MAC and part < len(NGROUPS):
+                    attn_out(mm, part)

@@ -29,6 +29,9 @@ NCHUNK = NB // CHUNK
 RAW_BUFS = 4
 NGROUPS = ((0, 4), (4, 4), (8, 1))
 QN = 8
+KEEP_STEPS = (0, 1, 2, 3, 4, 5, 6, 7, 8)
+KICK = 1
+DRAIN_RUN = 4
 
 FLOPS = 2 * 3 * 128 * 512 * H * W + 2 * 2 * WIN * 128 * H * W
 
@@ -155,25 +158,33 @@ def tile_mutliheadattention2d_kernel(tc, x, Wq, Wk, Wv, rel_t, rel_f, out_0, out
             nc.tensor.matmul_mx(out=dst, lhsT=w_codes[widx][:].bitcast(FP8X4), lhsT_scale=w_scales[widx][:],
                                 rhs=xc[b][:].bitcast(FP8X4), rhs_scale=xs[b][:], start=True, stop=True)
 
-        def mx_kv(b):
+        kv_ps = {}
+
+        def mx_k(b):
             k_ps = psum.tile([P, R, W], F32, name="k_ps", tag="kps")
             mx_w_stationary(k_ps[:].rearrange("p r w -> p (r w)"), 1, b)
+            kv_ps[("k", b)] = k_ps
+
+        def mx_v(b):
             v_ps = psum.tile([P, R, P], F32, name="v_ps", tag="vps")
             for r in range(R):
                 cols = slice(r * W, (r + 1) * W)
                 nc.tensor.matmul_mx(out=v_ps[:, r, :], lhsT=xc[b][:, cols].bitcast(FP8X4), lhsT_scale=xs[b][:, cols],
                                     rhs=w_codes[2][:].bitcast(FP8X4), rhs_scale=w_scales[2][:], start=True, stop=True)
+            kv_ps[("v", b)] = v_ps
+
+        def kv_out(b):
             ks = (b * R) % RK
-            nc.scalar.copy(out=k_ring[:, ks:ks + R, 1:W + 1], in_=k_ps[:])
+            nc.scalar.copy(out=k_ring[:, ks:ks + R, 1:W + 1], in_=kv_ps[("k", b)][:])
             vs = (b * R) % RV
-            nc.scalar.copy(out=v_ring[:, vs:vs + R, :], in_=v_ps[:])
+            nc.scalar.copy(out=v_ring[:, vs:vs + R, :], in_=kv_ps[("v", b)][:])
 
         def mx_q(b):
             t_q = psum.tile([P, R, W], F32, name="q_ps", tag="qps", bufs=2)
             mx_w_stationary(t_q[:].rearrange("p r w -> p (r w)"), 0, b)
             q_ps[b] = t_q
 
-        def qk(b, filler):
+        def qk(b, filler, keeper):
             h0 = b * R
             if b == NB - 1:
                 nc.vector.memset(k_ring[:, H % RK, :], 0.0)
@@ -188,6 +199,8 @@ def tile_mutliheadattention2d_kernel(tc, x, Wq, Wk, Wv, rel_t, rel_f, out_0, out
                             out=t_p[:, n, off:off + cnt, :], in0=k_ring[:, slot:slot + cnt, j:j + W],
                             scalar=r9[:, n:n + 1], in1=q_ps[b][:, off:off + cnt, :], op0=ALU.add, op1=ALU.mult)
                     for r in range(R):
+                        if r == R // 2 and n in KEEP_STEPS:
+                            keeper()
                         nc.tensor.matmul(out=t_e[:, n, :, r], lhsT=t_p[:, n, r, :], rhs=gsum[:, 0:QN], start=True, stop=True)
                     filler(R)
             e_ps[b] = t_e
@@ -276,7 +289,10 @@ def tile_mutliheadattention2d_kernel(tc, x, Wq, Wk, Wv, rel_t, rel_f, out_0, out
 
         def av_sum_end(b, t_o):
             h0 = b * R
-            av_sum_step(len(work["todo"]))
+            while work["pos"] < len(work["todo"]):
+                av_sum_step(DRAIN_RUN)
+                if b >= NB - 3 and work["pos"] < len(work["todo"]):
+                    keep["fn"]()
             t_sb = outp.tile([P, PIX], F32, name="o_sb")
             nc.scalar.copy(out=t_sb[:], in_=t_o[:].rearrange("p r w -> p (r w)"))
             nc.sync.dma_start(out=o0[:, h0 * W:(h0 + R) * W], in_=t_sb[:])
@@ -302,16 +318,33 @@ def tile_mutliheadattention2d_kernel(tc, x, Wq, Wk, Wv, rel_t, rel_f, out_0, out
             if 0 <= b < NB:
                 stage(b)
 
+        keep = {"fn": None}
+
         with tc.manual_schedule():
             for t in range(-4, NB + 8):
                 run(softmax_a, t - 1)
                 run(regroup, t + 4)
-                run(mx_kv, t + 2)
+                run(mx_k, t + 2)
                 run(mx_q, t + 1)
+                if t + 1 == NB:
+                    scratch = psum.tile([P, R, W], F32, name="scratch", tag="qps", bufs=2)
+                    q_ps[NB] = scratch
+                kb = min(t + 1, NB)
+                src_b = min(t + 1, NB - 1)
+
+                def keeper(kb=kb, src_b=src_b):
+                    mx_w_stationary(q_ps[kb][:].rearrange("p r w -> p (r w)"), 0, src_b)
+
+                keep["fn"] = keeper
+                if 0 <= t < NB + 3:
+                    for unused in range(KICK):
+                        keeper()
+                run(mx_v, t + 2)
+                run(kv_out, t + 2)
                 run(shift, t - 2)
                 t_o = av_sum_begin(t - 3) if 0 <= t - 3 < NB else None
                 if 0 <= t < NB:
-                    qk(t, av_sum_step)
+                    qk(t, av_sum_step, keeper)
                 run(av_products, t - 2)
                 run(quant, t + 3)
                 run(softmax_b, t - 1)

@@ -29,9 +29,6 @@ NCHUNK = NB // CHUNK
 RAW_BUFS = 4
 NGROUPS = ((0, 4), (4, 4), (8, 1))
 QN = 8
-KEEP_STEPS = (0, 1, 2, 3, 4, 5, 6, 7, 8)
-KICK = 1
-DRAIN_RUN = 4
 
 FLOPS = 2 * 3 * 128 * 512 * H * W + 2 * 2 * WIN * 128 * H * W
 
@@ -135,7 +132,6 @@ def tile_mutliheadattention2d_kernel(tc, x, Wq, Wk, Wv, rel_t, rel_f, out_0, out
         dif = {}
         a16 = {}
         sh_ps = {}
-        sh_sb = {}
         avp = {}
 
         def regroup(b):
@@ -158,33 +154,25 @@ def tile_mutliheadattention2d_kernel(tc, x, Wq, Wk, Wv, rel_t, rel_f, out_0, out
             nc.tensor.matmul_mx(out=dst, lhsT=w_codes[widx][:].bitcast(FP8X4), lhsT_scale=w_scales[widx][:],
                                 rhs=xc[b][:].bitcast(FP8X4), rhs_scale=xs[b][:], start=True, stop=True)
 
-        kv_ps = {}
-
-        def mx_k(b):
+        def mx_kv(b):
             k_ps = psum.tile([P, R, W], F32, name="k_ps", tag="kps")
             mx_w_stationary(k_ps[:].rearrange("p r w -> p (r w)"), 1, b)
-            kv_ps[("k", b)] = k_ps
-
-        def mx_v(b):
             v_ps = psum.tile([P, R, P], F32, name="v_ps", tag="vps")
             for r in range(R):
                 cols = slice(r * W, (r + 1) * W)
                 nc.tensor.matmul_mx(out=v_ps[:, r, :], lhsT=xc[b][:, cols].bitcast(FP8X4), lhsT_scale=xs[b][:, cols],
                                     rhs=w_codes[2][:].bitcast(FP8X4), rhs_scale=w_scales[2][:], start=True, stop=True)
-            kv_ps[("v", b)] = v_ps
-
-        def kv_out(b):
             ks = (b * R) % RK
-            nc.scalar.copy(out=k_ring[:, ks:ks + R, 1:W + 1], in_=kv_ps[("k", b)][:])
+            nc.scalar.copy(out=k_ring[:, ks:ks + R, 1:W + 1], in_=k_ps[:])
             vs = (b * R) % RV
-            nc.scalar.copy(out=v_ring[:, vs:vs + R, :], in_=kv_ps[("v", b)][:])
+            nc.scalar.copy(out=v_ring[:, vs:vs + R, :], in_=v_ps[:])
 
         def mx_q(b):
             t_q = psum.tile([P, R, W], F32, name="q_ps", tag="qps", bufs=2)
             mx_w_stationary(t_q[:].rearrange("p r w -> p (r w)"), 0, b)
             q_ps[b] = t_q
 
-        def qk(b, filler, keeper):
+        def qk(b, filler):
             h0 = b * R
             if b == NB - 1:
                 nc.vector.memset(k_ring[:, H % RK, :], 0.0)
@@ -199,8 +187,6 @@ def tile_mutliheadattention2d_kernel(tc, x, Wq, Wk, Wv, rel_t, rel_f, out_0, out
                             out=t_p[:, n, off:off + cnt, :], in0=k_ring[:, slot:slot + cnt, j:j + W],
                             scalar=r9[:, n:n + 1], in1=q_ps[b][:, off:off + cnt, :], op0=ALU.add, op1=ALU.mult)
                     for r in range(R):
-                        if r == R // 2 and n in KEEP_STEPS:
-                            keeper()
                         nc.tensor.matmul(out=t_e[:, n, :, r], lhsT=t_p[:, n, r, :], rhs=gsum[:, 0:QN], start=True, stop=True)
                     filler(R)
             e_ps[b] = t_e
@@ -224,7 +210,7 @@ def tile_mutliheadattention2d_kernel(tc, x, Wq, Wk, Wv, rel_t, rel_f, out_0, out
                 t_a = outp.tile([P, WIN, NG, MAC], F32, name="a16")
                 a16[m] = t_a
             hs = (b * R) % MAC
-            nc.gpsimd.tensor_tensor(out=a16[m][:, :, :, hs:hs + R], in0=dif[b][:].rearrange("p n (g r) -> p n g r", r=R),
+            nc.vector.tensor_tensor(out=a16[m][:, :, :, hs:hs + R], in0=dif[b][:].rearrange("p n (g r) -> p n g r", r=R),
                                     in1=t_r[:].rearrange("p (g r) -> p g r", r=R).unsqueeze(1).to_broadcast([P, WIN, NG, R]),
                                     op=ALU.mult)
 
@@ -235,10 +221,7 @@ def tile_mutliheadattention2d_kernel(tc, x, Wq, Wk, Wv, rel_t, rel_f, out_0, out
             av = a16[m][:].rearrange("p (i j) g h -> p i j g h", j=3)
             nc.tensor.matmul(out=t_sh[:, 0], lhsT=shl0[:], rhs=av[:, :, 0, :, hs:hs + R], start=True, stop=True)
             nc.tensor.matmul(out=t_sh[:, 1], lhsT=shl2[:], rhs=av[:, :, 2, :, hs:hs + R], start=True, stop=True)
-            t_sb = smallp.tile([P, 3, NG, R], F32, name="sh_sb")
-            nc.scalar.copy(out=t_sb[:], in_=t_sh[:, 1])
             sh_ps[b] = t_sh
-            sh_sb[b] = t_sb
 
         def av_products(b):
             h0 = b * R
@@ -257,9 +240,8 @@ def tile_mutliheadattention2d_kernel(tc, x, Wq, Wk, Wv, rel_t, rel_f, out_0, out
                         elif j == 1:
                             att = a16[m][:, n, :, hs + a:hs + a + cnt]
                         else:
-                            att = sh_sb[b][:, i, :, a:a + cnt]
-                        eng = nc.vector if j == 0 else nc.gpsimd
-                        eng.tensor_tensor(
+                            att = sh_ps[b][:, 1, i, :, a:a + cnt]
+                        nc.vector.tensor_tensor(
                             out=t_q[:, n, a:a + cnt, :].rearrange("p r (g c) -> p r g c", c=CG),
                             in0=v_ring[:, slot:slot + cnt, :].rearrange("p r (g c) -> p r g c", c=CG),
                             in1=att.rearrange("p g r -> p r g").unsqueeze(3).to_broadcast([P, cnt, NG, CG]),
@@ -289,10 +271,7 @@ def tile_mutliheadattention2d_kernel(tc, x, Wq, Wk, Wv, rel_t, rel_f, out_0, out
 
         def av_sum_end(b, t_o):
             h0 = b * R
-            while work["pos"] < len(work["todo"]):
-                av_sum_step(DRAIN_RUN)
-                if b >= NB - 3 and work["pos"] < len(work["todo"]):
-                    keep["fn"]()
+            av_sum_step(len(work["todo"]))
             t_sb = outp.tile([P, PIX], F32, name="o_sb")
             nc.scalar.copy(out=t_sb[:], in_=t_o[:].rearrange("p r w -> p (r w)"))
             nc.sync.dma_start(out=o0[:, h0 * W:(h0 + R) * W], in_=t_sb[:])
@@ -318,33 +297,16 @@ def tile_mutliheadattention2d_kernel(tc, x, Wq, Wk, Wv, rel_t, rel_f, out_0, out
             if 0 <= b < NB:
                 stage(b)
 
-        keep = {"fn": None}
-
         with tc.manual_schedule():
             for t in range(-4, NB + 8):
                 run(softmax_a, t - 1)
                 run(regroup, t + 4)
-                run(mx_k, t + 2)
+                run(mx_kv, t + 2)
                 run(mx_q, t + 1)
-                if t + 1 == NB:
-                    scratch = psum.tile([P, R, W], F32, name="scratch", tag="qps", bufs=2)
-                    q_ps[NB] = scratch
-                kb = min(t + 1, NB)
-                src_b = min(t + 1, NB - 1)
-
-                def keeper(kb=kb, src_b=src_b):
-                    mx_w_stationary(q_ps[kb][:].rearrange("p r w -> p (r w)"), 0, src_b)
-
-                keep["fn"] = keeper
-                if 0 <= t < NB + 3:
-                    for unused in range(KICK):
-                        keeper()
-                run(mx_v, t + 2)
-                run(kv_out, t + 2)
                 run(shift, t - 2)
                 t_o = av_sum_begin(t - 3) if 0 <= t - 3 < NB else None
                 if 0 <= t < NB:
-                    qk(t, av_sum_step, keeper)
+                    qk(t, av_sum_step)
                 run(av_products, t - 2)
                 run(quant, t + 3)
                 run(softmax_b, t - 1)

@@ -127,7 +127,6 @@ def tile_mutliheadattention2d_kernel(tc, x, Wq, Wk, Wv, rel_t, rel_f, out_0, out
         xc = {}
         xs = {}
         q_ps = {}
-        prod = {}
         e_ps = {}
         dif = {}
         a16 = {}
@@ -188,7 +187,8 @@ def tile_mutliheadattention2d_kernel(tc, x, Wq, Wk, Wv, rel_t, rel_f, out_0, out
                             scalar=r9[:, n:n + 1], in1=q_ps[b][:, off:off + cnt, :], op0=ALU.add, op1=ALU.mult)
                     for r in range(R):
                         nc.tensor.matmul(out=t_e[:, n, :, r], lhsT=t_p[:, n, r, :], rhs=gsum[:, 0:QN], start=True, stop=True)
-                    filler(R)
+                    if n % 2 == 1:
+                        filler(3)
             e_ps[b] = t_e
 
         def softmax_a(b):
@@ -229,6 +229,10 @@ def tile_mutliheadattention2d_kernel(tc, x, Wq, Wk, Wv, rel_t, rel_f, out_0, out
             hs = (b * R) % MAC
             t_q = prodp.tile([P, WIN, R, P], F32, name="avp")
             for j in (0, 1, 2):
+                if b == 0:
+                    nc.vector.memset(t_q[:, j, 0, :], 0.0)
+                if b == NB - 1:
+                    nc.vector.memset(t_q[:, 6 + j, R - 1, :], 0.0)
                 for i in range(3):
                     n = 3 * i + j
                     lo = max(0, 1 - i - h0)
@@ -246,6 +250,8 @@ def tile_mutliheadattention2d_kernel(tc, x, Wq, Wk, Wv, rel_t, rel_f, out_0, out
                             in0=v_ring[:, slot:slot + cnt, :].rearrange("p r (g c) -> p r g c", c=CG),
                             in1=att.rearrange("p g r -> p r g").unsqueeze(3).to_broadcast([P, cnt, NG, CG]),
                             op=ALU.mult)
+                for i in (1, 2):
+                    nc.gpsimd.tensor_tensor(out=t_q[:, j], in0=t_q[:, j], in1=t_q[:, 3 * i + j], op=ALU.add)
             avp[b] = t_q
 
         work = {"todo": [], "pos": 0}
@@ -257,9 +263,8 @@ def tile_mutliheadattention2d_kernel(tc, x, Wq, Wk, Wv, rel_t, rel_f, out_0, out
             work["pos"] = 0
             t_o = psum.tile([P, R, W], F32, name="o_ps", tag="ops")
             for r in range(R):
-                terms = [(i, j) for i in range(3) for j in range(3) if 0 <= h0 + r + i - 1 < H]
-                for idx, (i, j) in enumerate(terms):
-                    pending.append((t_o[:, r, :], avp[b][:, 3 * i + j, r, :], perms[j], idx == 0, idx == len(terms) - 1))
+                for j in range(3):
+                    pending.append((t_o[:, r, :], avp[b][:, j, r, :], perms[j], j == 0, j == 2))
             return t_o
 
         def av_sum_step(count):

@@ -28,7 +28,9 @@ CHUNK = 2
 NCHUNK = NB // CHUNK
 RAW_BUFS = 4
 NGROUPS = ((0, 4), (4, 4), (8, 1))
-QN = 8
+STEP_BUFS = 9
+FIRST = (0, 96, 160)
+LEAD = 12
 
 FLOPS = 2 * 3 * 128 * 512 * H * W + 2 * 2 * WIN * 128 * H * W
 
@@ -52,6 +54,7 @@ def tile_mutliheadattention2d_kernel(tc, x, Wq, Wk, Wv, rel_t, rel_f, out_0, out
         grpp = ctx.enter_context(tc.tile_pool(name="grpp", bufs=3))
         codp = ctx.enter_context(tc.tile_pool(name="codp", bufs=3))
         prodp = ctx.enter_context(tc.tile_pool(name="prodp", bufs=2))
+        stepp = ctx.enter_context(tc.tile_pool(name="stepp", bufs=STEP_BUFS))
         smallp = ctx.enter_context(tc.tile_pool(name="smallp", bufs=3))
         outp = ctx.enter_context(tc.tile_pool(name="outp", bufs=2))
         psum = ctx.enter_context(tc.psum_pool(name="psum", bufs=1))
@@ -85,19 +88,20 @@ def tile_mutliheadattention2d_kernel(tc, x, Wq, Wk, Wv, rel_t, rel_f, out_0, out
         masks.make_identity(nc, ident_b[:])
         perm0 = const.tile([P, P], F32, name="perm0")
         perm2 = const.tile([P, P], F32, name="perm2")
-        shl0 = const.tile([P, P], F32, name="shl0")
-        shl2 = const.tile([P, P], F32, name="shl2")
         nc.vector.tensor_copy(out=perm0[:, 1:P], in_=ident_f[:, 0:P - 1])
         nc.vector.tensor_copy(out=perm0[:, 0:1], in_=ident_f[:, P - 1:P])
         nc.vector.tensor_copy(out=perm2[:, 0:P - 1], in_=ident_f[:, 1:P])
         nc.vector.tensor_copy(out=perm2[:, P - 1:P], in_=ident_f[:, 0:1])
-        nc.vector.tensor_copy(out=shl0[:, 0:P - 1], in_=ident_f[:, 1:P])
-        nc.vector.memset(shl0[:, P - 1:P], 0.0)
-        nc.vector.tensor_copy(out=shl2[:, 1:P], in_=ident_f[:, 0:P - 1])
-        nc.vector.memset(shl2[:, 0:1], 0.0)
         perms = (perm0, ident_f, perm2)
         gsum = const.tile([P, NG], F32, name="gsum")
         nc.vector.tensor_reduce(out=gsum[:], in_=ident_f[:].rearrange("p (g c) -> p g c", c=CG), axis=AX.X, op=ALU.add)
+        gsum_b = const.tile([P, NG], BF16, name="gsum_b")
+        nc.vector.tensor_copy(out=gsum_b[:], in_=gsum[:])
+        pads = []
+        for idx in range(2):
+            t_pad = const.tile([P, 3, W + 2], F32, name="pad%d" % idx)
+            nc.vector.memset(t_pad[:], 0.0)
+            pads.append(t_pad)
         r9 = const.tile([P, WIN], F32, name="r9")
         nc.vector.tensor_copy(out=r9[0:64, :].rearrange("p (i j) -> p i j", j=3),
                               in_=rel_sb[0:64, :].unsqueeze(2).to_broadcast([64, 3, 3]))
@@ -127,10 +131,15 @@ def tile_mutliheadattention2d_kernel(tc, x, Wq, Wk, Wv, rel_t, rel_f, out_0, out
         xc = {}
         xs = {}
         q_ps = {}
+        prod = {}
         e_ps = {}
         dif = {}
         a16 = {}
         sh_ps = {}
+        split = {}
+        attn = {}
+        f_ps = {}
+        kv_ps = {}
         avp = {}
 
         def regroup(b):
@@ -161,6 +170,10 @@ def tile_mutliheadattention2d_kernel(tc, x, Wq, Wk, Wv, rel_t, rel_f, out_0, out
                 cols = slice(r * W, (r + 1) * W)
                 nc.tensor.matmul_mx(out=v_ps[:, r, :], lhsT=xc[b][:, cols].bitcast(FP8X4), lhsT_scale=xs[b][:, cols],
                                     rhs=w_codes[2][:].bitcast(FP8X4), rhs_scale=w_scales[2][:], start=True, stop=True)
+            kv_ps[b] = (k_ps, v_ps)
+
+        def kv_out(b):
+            k_ps, v_ps = kv_ps[b]
             ks = (b * R) % RK
             nc.scalar.copy(out=k_ring[:, ks:ks + R, 1:W + 1], in_=k_ps[:])
             vs = (b * R) % RV
@@ -171,24 +184,35 @@ def tile_mutliheadattention2d_kernel(tc, x, Wq, Wk, Wv, rel_t, rel_f, out_0, out
             mx_w_stationary(t_q[:].rearrange("p r w -> p (r w)"), 0, b)
             q_ps[b] = t_q
 
-        def qk(b, filler):
+        def qk_products(b):
             h0 = b * R
             if b == NB - 1:
                 nc.vector.memset(k_ring[:, H % RK, :], 0.0)
-            t_p = prodp.tile([P, WIN, R, W], F32, name="prod")
-            t_e = psum.tile([P, WIN, NG, R], F32, name="e_ps", tag="eps")
+            parts = []
             for i in range(3):
                 runs = ring_runs(h0 + i - 1, R, RK)
                 for j in range(3):
                     n = 3 * i + j
+                    t_p = stepp.tile([P, R, W], F32, name="prod")
                     for off, slot, cnt in runs:
                         nc.vector.scalar_tensor_tensor(
-                            out=t_p[:, n, off:off + cnt, :], in0=k_ring[:, slot:slot + cnt, j:j + W],
+                            out=t_p[:, off:off + cnt, :], in0=k_ring[:, slot:slot + cnt, j:j + W],
                             scalar=r9[:, n:n + 1], in1=q_ps[b][:, off:off + cnt, :], op0=ALU.add, op1=ALU.mult)
-                    for r in range(R):
-                        nc.tensor.matmul(out=t_e[:, n, :, r], lhsT=t_p[:, n, r, :], rhs=gsum[:, 0:QN], start=True, stop=True)
-                    if n % 2 == 1:
-                        filler(3)
+                    t_hi = stepp.tile([P, R, W], BF16, name="p_hi")
+                    nc.scalar.copy(out=t_hi[:], in_=t_p[:])
+                    t_lo = stepp.tile([P, R, W], BF16, name="p_lo")
+                    nc.gpsimd.tensor_tensor(out=t_lo[:], in0=t_p[:], in1=t_hi[:], op=ALU.subtract)
+                    parts.append((3 * j + i, t_hi, t_lo))
+                    if n == 1:
+                        run(shift_mid, b - 2)
+            split[b] = parts
+
+        def qk_sums(b):
+            t_e = psum.tile([P, WIN, NG, R], F32, name="e_ps", tag="eps")
+            for m, t_hi, t_lo in split[b]:
+                for r in range(R):
+                    nc.tensor.matmul(out=t_e[:, m, :, r], lhsT=t_hi[:, r, :], rhs=gsum_b[:], start=True, stop=False)
+                    nc.tensor.matmul(out=t_e[:, m, :, r], lhsT=t_lo[:, r, :], rhs=gsum_b[:], start=False, stop=True)
             e_ps[b] = t_e
 
         def softmax_a(b):
@@ -205,53 +229,53 @@ def tile_mutliheadattention2d_kernel(tc, x, Wq, Wk, Wv, rel_t, rel_f, out_0, out
             nc.vector.tensor_reduce(out=t_s[:], in_=dif[b][:].rearrange("p n m -> p m n"), axis=AX.X, op=ALU.add)
             t_r = smallp.tile([P, NG * R], F32, name="rsum")
             nc.vector.reciprocal(out=t_r[:], in_=t_s[:])
+            t_a = smallp.tile([P, WIN, NG, R], F32, name="att")
+            nc.vector.tensor_tensor(out=t_a[:], in0=dif[b][:].rearrange("p n (g r) -> p n g r", r=R),
+                                    in1=t_r[:].rearrange("p (g r) -> p g r", r=R).unsqueeze(1).to_broadcast([P, WIN, NG, R]),
+                                    op=ALU.mult)
+            attn[b] = t_a
+
+        def collect(b):
             m = b // (MAC // R)
             if b % (MAC // R) == 0:
                 t_a = outp.tile([P, WIN, NG, MAC], F32, name="a16")
                 a16[m] = t_a
             hs = (b * R) % MAC
-            nc.vector.tensor_tensor(out=a16[m][:, :, :, hs:hs + R], in0=dif[b][:].rearrange("p n (g r) -> p n g r", r=R),
-                                    in1=t_r[:].rearrange("p (g r) -> p g r", r=R).unsqueeze(1).to_broadcast([P, WIN, NG, R]),
-                                    op=ALU.mult)
+            nc.scalar.copy(out=a16[m][:, :, :, hs:hs + R], in_=attn[b][:])
 
-        def shift(b):
-            m = b // (MAC // R)
-            hs = (b * R) % MAC
-            t_sh = psum.tile([P, 2, 3, NG, R], F32, name="sh_ps", tag="shps")
-            av = a16[m][:].rearrange("p (i j) g h -> p i j g h", j=3)
-            nc.tensor.matmul(out=t_sh[:, 0], lhsT=shl0[:], rhs=av[:, :, 0, :, hs:hs + R], start=True, stop=True)
-            nc.tensor.matmul(out=t_sh[:, 1], lhsT=shl2[:], rhs=av[:, :, 2, :, hs:hs + R], start=True, stop=True)
+        def shift_begin(b):
+            flat = attn[b][:].rearrange("p n g r -> p (n g r)")
+            t_f = psum.tile([P, 3, W], F32, name="f_ps", tag="tps")
+            for j in range(3):
+                nc.tensor.transpose(t_f[:, j, :], flat[:, FIRST[j]:FIRST[j] + P], ident_f[:])
+            f_ps[b] = t_f
+
+        def shift_mid(b):
+            nc.scalar.copy(out=pads[b % 2][:, :, 1:W + 1], in_=f_ps[b][:])
+
+        def shift_end(b):
+            t_sh = psum.tile([P, 3, P], F32, name="sh_ps", tag="shps")
+            for j in range(3):
+                nc.tensor.transpose(t_sh[:, j, :], pads[b % 2][:, j, 2 - j:2 - j + W], ident_f[:])
             sh_ps[b] = t_sh
 
         def av_products(b):
             h0 = b * R
-            m = b // (MAC // R)
-            hs = (b * R) % MAC
             t_q = prodp.tile([P, WIN, R, P], F32, name="avp")
             for j in (0, 1, 2):
-                if b == 0:
-                    nc.vector.memset(t_q[:, j, 0, :], 0.0)
-                if b == NB - 1:
-                    nc.vector.memset(t_q[:, 6 + j, R - 1, :], 0.0)
                 for i in range(3):
                     n = 3 * i + j
                     lo = max(0, 1 - i - h0)
                     hi = min(R, H + 1 - i - h0)
                     for off, slot, cnt in ring_runs(h0 + lo + i - 1, hi - lo, RV):
                         a = lo + off
-                        if j == 0:
-                            att = sh_ps[b][:, 0, i, :, a:a + cnt]
-                        elif j == 1:
-                            att = a16[m][:, n, :, hs + a:hs + a + cnt]
-                        else:
-                            att = sh_ps[b][:, 1, i, :, a:a + cnt]
+                        col = (3 * j + i) * NG * R - FIRST[j]
+                        att = sh_ps[b][:, j, col:col + NG * R].rearrange("p (g r) -> p g r", r=R)[:, :, a:a + cnt]
                         nc.vector.tensor_tensor(
                             out=t_q[:, n, a:a + cnt, :].rearrange("p r (g c) -> p r g c", c=CG),
                             in0=v_ring[:, slot:slot + cnt, :].rearrange("p r (g c) -> p r g c", c=CG),
                             in1=att.rearrange("p g r -> p r g").unsqueeze(3).to_broadcast([P, cnt, NG, CG]),
                             op=ALU.mult)
-                for i in (1, 2):
-                    nc.gpsimd.tensor_tensor(out=t_q[:, j], in0=t_q[:, j], in1=t_q[:, 3 * i + j], op=ALU.add)
             avp[b] = t_q
 
         work = {"todo": [], "pos": 0}
@@ -263,8 +287,9 @@ def tile_mutliheadattention2d_kernel(tc, x, Wq, Wk, Wv, rel_t, rel_f, out_0, out
             work["pos"] = 0
             t_o = psum.tile([P, R, W], F32, name="o_ps", tag="ops")
             for r in range(R):
-                for j in range(3):
-                    pending.append((t_o[:, r, :], avp[b][:, j, r, :], perms[j], j == 0, j == 2))
+                terms = [(i, j) for i in range(3) for j in range(3) if 0 <= h0 + r + i - 1 < H]
+                for idx, (i, j) in enumerate(terms):
+                    pending.append((t_o[:, r, :], avp[b][:, 3 * i + j, r, :], perms[j], idx == 0, idx == len(terms) - 1))
             return t_o
 
         def av_sum_step(count):
@@ -291,7 +316,7 @@ def tile_mutliheadattention2d_kernel(tc, x, Wq, Wk, Wv, rel_t, rel_f, out_0, out
             n0, nn = NGROUPS[part]
             t_ps = psum.tile([P, 4, W], F32, name="t_ps", tag="tps")
             for n in range(nn):
-                nc.tensor.transpose(t_ps[:, n, :], a16[m][:, n0 + n, :, :].rearrange("p g h -> p (g h)"), ident_f[:])
+                nc.tensor.transpose(t_ps[:, n, :], a16[m][:, 3 * ((n0 + n) % 3) + (n0 + n) // 3, :, :].rearrange("p g h -> p (g h)"), ident_f[:])
             nc.scalar.copy(out=t_t[:, :, n0:n0 + nn], in_=t_ps[:, 0:nn, :].rearrange("p n w -> p w n"))
             if part == len(NGROUPS) - 1:
                 for g in range(NG):
@@ -304,17 +329,25 @@ def tile_mutliheadattention2d_kernel(tc, x, Wq, Wk, Wv, rel_t, rel_f, out_0, out
 
         with tc.manual_schedule():
             for t in range(-4, NB + 8):
-                run(softmax_a, t - 1)
-                run(regroup, t + 4)
                 run(mx_kv, t + 2)
                 run(mx_q, t + 1)
-                run(shift, t - 2)
+                run(shift_begin, t - 2)
                 t_o = av_sum_begin(t - 3) if 0 <= t - 3 < NB else None
+                av_sum_step(LEAD)
                 if 0 <= t < NB:
-                    qk(t, av_sum_step)
+                    qk_products(t)
+                else:
+                    run(shift_mid, t - 2)
+                run(shift_end, t - 2)
+                av_sum_step(len(work["todo"]))
+                run(softmax_a, t - 1)
+                run(qk_sums, t)
+                run(kv_out, t + 2)
                 run(av_products, t - 2)
+                run(regroup, t + 4)
                 run(quant, t + 3)
                 run(softmax_b, t - 1)
+                run(collect, t - 2)
                 if t_o is not None:
                     av_sum_end(t - 3, t_o)
                 mm, part = divmod(t - 5, MAC // R)

@@ -30,7 +30,10 @@ RAW_BUFS = 4
 NGROUPS = ((0, 4), (4, 4), (8, 1))
 STEP_BUFS = 9
 FIRST = (0, 96, 160)
-LEAD = 12
+LEAD = 24
+HEAD_SHARE = 3
+TAIL_SHARE = 3
+TAIL_BLOCKS = 4
 
 FLOPS = 2 * 3 * 128 * 512 * H * W + 2 * 2 * WIN * 128 * H * W
 
@@ -55,6 +58,7 @@ def tile_mutliheadattention2d_kernel(tc, x, Wq, Wk, Wv, rel_t, rel_f, out_0, out
         codp = ctx.enter_context(tc.tile_pool(name="codp", bufs=3))
         prodp = ctx.enter_context(tc.tile_pool(name="prodp", bufs=2))
         stepp = ctx.enter_context(tc.tile_pool(name="stepp", bufs=STEP_BUFS))
+        halfp = ctx.enter_context(tc.tile_pool(name="halfp", bufs=2 * WIN))
         smallp = ctx.enter_context(tc.tile_pool(name="smallp", bufs=3))
         outp = ctx.enter_context(tc.tile_pool(name="outp", bufs=2))
         psum = ctx.enter_context(tc.psum_pool(name="psum", bufs=1))
@@ -113,14 +117,17 @@ def tile_mutliheadattention2d_kernel(tc, x, Wq, Wk, Wv, rel_t, rel_f, out_0, out
 
         w_codes = []
         w_scales = []
+        w_tp = []
         for idx in range(3):
             w_de = const.tile([P, 4, P], BF16, name="w_de%d" % idx)
-            nc.vector.tensor_copy(out=w_de[:], in_=w_raw[idx][:].rearrange("o (p t) -> o t p", t=4))
-            w_ps = psum.tile([P, 4, P], BF16, name="w_ps", tag="tps")
+            nc.scalar.copy(out=w_de[:], in_=w_raw[idx][:].rearrange("o (p t) -> o t p", t=4))
+            w_ps = psum.tile([P, 4, P], BF16, name="w_ps", tag=("tps", "kps", "vps")[idx])
             for t in range(4):
                 nc.tensor.transpose(w_ps[:, t, :], w_de[:, t, :], ident_b[:])
+            w_tp.append(w_ps)
+        for idx in range(3):
             w_grp = const.tile([P, P, 4], BF16, name="w_grp%d" % idx, align_bytes=64)
-            nc.vector.tensor_copy(out=w_grp[:], in_=w_ps[:].rearrange("p t o -> p o t"))
+            nc.vector.tensor_copy(out=w_grp[:], in_=w_tp[idx][:].rearrange("p t o -> p o t"))
             w_c = const.tile([P, P], U32, name="w_c%d" % idx, align_bytes=64)
             w_s = const.tile([P, P], U8, name="w_s%d" % idx, align_bytes=64)
             nc.vector.quantize_mx(out=w_c[:].bitcast(FP8X4), scales=w_s[:], in_=w_grp[:].rearrange("p o t -> p (o t)"))
@@ -137,6 +144,8 @@ def tile_mutliheadattention2d_kernel(tc, x, Wq, Wk, Wv, rel_t, rel_f, out_0, out
         a16 = {}
         sh_ps = {}
         split = {}
+        tops = {}
+        sums = {}
         attn = {}
         f_ps = {}
         kv_ps = {}
@@ -145,8 +154,12 @@ def tile_mutliheadattention2d_kernel(tc, x, Wq, Wk, Wv, rel_t, rel_f, out_0, out
         def regroup(b):
             t_g = grpp.tile([P, PIX, 4], BF16, name="grp", align_bytes=64)
             src = raw[b // CHUNK][:, :, (b % CHUNK) * PIX:(b % CHUNK + 1) * PIX]
-            nc.scalar.copy(out=t_g[:].rearrange("p (c i) t -> p c t i", i=4),
-                           in_=src.rearrange("p t (c i) -> p c t i", i=4))
+            if b in (1, 3):
+                nc.vector.tensor_copy(out=t_g[:].rearrange("p (c i) t -> p c t i", i=4),
+                                      in_=src.rearrange("p t (c i) -> p c t i", i=4))
+            else:
+                nc.scalar.copy(out=t_g[:].rearrange("p (c i) t -> p c t i", i=4),
+                               in_=src.rearrange("p t (c i) -> p c t i", i=4))
             grp[b] = t_g
             if b % CHUNK == CHUNK - 1 and b // CHUNK + RAW_BUFS < NCHUNK:
                 load(b // CHUNK + RAW_BUFS)
@@ -184,11 +197,15 @@ def tile_mutliheadattention2d_kernel(tc, x, Wq, Wk, Wv, rel_t, rel_f, out_0, out
             mx_w_stationary(t_q[:].rearrange("p r w -> p (r w)"), 0, b)
             q_ps[b] = t_q
 
+        def vector_share(b):
+            return HEAD_SHARE if b < 3 else (TAIL_SHARE if b == NB - 1 else 0)
+
         def qk_products(b):
             h0 = b * R
             if b == NB - 1:
                 nc.vector.memset(k_ring[:, H % RK, :], 0.0)
             parts = []
+            late = []
             for i in range(3):
                 runs = ring_runs(h0 + i - 1, R, RK)
                 for j in range(3):
@@ -198,13 +215,16 @@ def tile_mutliheadattention2d_kernel(tc, x, Wq, Wk, Wv, rel_t, rel_f, out_0, out
                         nc.vector.scalar_tensor_tensor(
                             out=t_p[:, off:off + cnt, :], in0=k_ring[:, slot:slot + cnt, j:j + W],
                             scalar=r9[:, n:n + 1], in1=q_ps[b][:, off:off + cnt, :], op0=ALU.add, op1=ALU.mult)
-                    t_hi = stepp.tile([P, R, W], BF16, name="p_hi")
+                    t_hi = halfp.tile([P, R, W], BF16, name="p_hi")
                     nc.scalar.copy(out=t_hi[:], in_=t_p[:])
-                    t_lo = stepp.tile([P, R, W], BF16, name="p_lo")
-                    nc.gpsimd.tensor_tensor(out=t_lo[:], in0=t_p[:], in1=t_hi[:], op=ALU.subtract)
+                    t_lo = halfp.tile([P, R, W], BF16, name="p_lo")
+                    if n < WIN - vector_share(b):
+                        nc.gpsimd.tensor_tensor(out=t_lo[:], in0=t_p[:], in1=t_hi[:], op=ALU.subtract)
+                    else:
+                        late.append((t_lo, t_p, t_hi))
                     parts.append((3 * j + i, t_hi, t_lo))
-                    if n == 1:
-                        run(shift_mid, b - 2)
+            for t_lo, t_p, t_hi in late:
+                nc.vector.tensor_tensor(out=t_lo[:], in0=t_p[:], in1=t_hi[:], op=ALU.subtract)
             split[b] = parts
 
         def qk_sums(b):
@@ -215,23 +235,34 @@ def tile_mutliheadattention2d_kernel(tc, x, Wq, Wk, Wv, rel_t, rel_f, out_0, out
                     nc.tensor.matmul(out=t_e[:, m, :, r], lhsT=t_lo[:, r, :], rhs=gsum_b[:], start=False, stop=True)
             e_ps[b] = t_e
 
-        def softmax_a(b):
+        def softmax_max(b):
             t_m = smallp.tile([P, NG * R], F32, name="mx")
             nc.vector.tensor_reduce(out=t_m[:], in_=e_ps[b][:].rearrange("p n g r -> p (g r) n"), axis=AX.X, op=ALU.max)
+            tops[b] = t_m
+
+        def softmax_sub(b):
             t_d = smallp.tile([P, WIN, NG * R], F32, name="dif")
             nc.vector.tensor_tensor(out=t_d[:], in0=e_ps[b][:].rearrange("p n g r -> p n (g r)"),
-                                    in1=t_m[:].unsqueeze(1).to_broadcast([P, WIN, NG * R]), op=ALU.subtract)
-            nc.scalar.activation(out=t_d[:], in_=t_d[:], func=ACT.Exp)
+                                    in1=tops[b][:].unsqueeze(1).to_broadcast([P, WIN, NG * R]), op=ALU.subtract)
             dif[b] = t_d
 
-        def softmax_b(b):
+        def softmax_exp(b):
+            nc.scalar.activation(out=dif[b][:], in_=dif[b][:], func=ACT.Exp)
+
+        def softmax_sum(b):
             t_s = smallp.tile([P, NG * R], F32, name="ssum")
             nc.vector.tensor_reduce(out=t_s[:], in_=dif[b][:].rearrange("p n m -> p m n"), axis=AX.X, op=ALU.add)
+            sums[b] = t_s
+
+        def softmax_rec(b):
             t_r = smallp.tile([P, NG * R], F32, name="rsum")
-            nc.vector.reciprocal(out=t_r[:], in_=t_s[:])
+            nc.vector.reciprocal(out=t_r[:], in_=sums[b][:])
+            sums[b] = t_r
+
+        def softmax_mul(b):
             t_a = smallp.tile([P, WIN, NG, R], F32, name="att")
             nc.vector.tensor_tensor(out=t_a[:], in0=dif[b][:].rearrange("p n (g r) -> p n g r", r=R),
-                                    in1=t_r[:].rearrange("p (g r) -> p g r", r=R).unsqueeze(1).to_broadcast([P, WIN, NG, R]),
+                                    in1=sums[b][:].rearrange("p (g r) -> p g r", r=R).unsqueeze(1).to_broadcast([P, WIN, NG, R]),
                                     op=ALU.mult)
             attn[b] = t_a
 
@@ -259,11 +290,16 @@ def tile_mutliheadattention2d_kernel(tc, x, Wq, Wk, Wv, rel_t, rel_f, out_0, out
                 nc.tensor.transpose(t_sh[:, j, :], pads[b % 2][:, j, 2 - j:2 - j + W], ident_f[:])
             sh_ps[b] = t_sh
 
-        def av_products(b):
+        def av_products(b, j, rows=(0, 1, 2)):
+            if not 0 <= b < NB:
+                return
             h0 = b * R
-            t_q = prodp.tile([P, WIN, R, P], F32, name="avp")
-            for j in (0, 1, 2):
-                for i in range(3):
+            if j == 0:
+                t_new = prodp.tile([P, WIN, R, P], F32, name="avp")
+                avp[b] = t_new
+            t_q = avp[b]
+            if True:
+                for i in rows:
                     n = 3 * i + j
                     lo = max(0, 1 - i - h0)
                     hi = min(R, H + 1 - i - h0)
@@ -271,12 +307,15 @@ def tile_mutliheadattention2d_kernel(tc, x, Wq, Wk, Wv, rel_t, rel_f, out_0, out
                         a = lo + off
                         col = (3 * j + i) * NG * R - FIRST[j]
                         att = sh_ps[b][:, j, col:col + NG * R].rearrange("p (g r) -> p g r", r=R)[:, :, a:a + cnt]
-                        nc.vector.tensor_tensor(
+                        eng = nc.vector
+                        if j == 1 and b >= NB - TAIL_BLOCKS:
+                            att = attn[b][:, 3 + i, :, a:a + cnt]
+                            eng = nc.gpsimd
+                        eng.tensor_tensor(
                             out=t_q[:, n, a:a + cnt, :].rearrange("p r (g c) -> p r g c", c=CG),
                             in0=v_ring[:, slot:slot + cnt, :].rearrange("p r (g c) -> p r g c", c=CG),
                             in1=att.rearrange("p g r -> p r g").unsqueeze(3).to_broadcast([P, cnt, NG, CG]),
                             op=ALU.mult)
-            avp[b] = t_q
 
         work = {"todo": [], "pos": 0}
 
@@ -331,25 +370,33 @@ def tile_mutliheadattention2d_kernel(tc, x, Wq, Wk, Wv, rel_t, rel_f, out_0, out
             for t in range(-4, NB + 8):
                 run(mx_kv, t + 2)
                 run(mx_q, t + 1)
-                run(shift_begin, t - 2)
-                t_o = av_sum_begin(t - 3) if 0 <= t - 3 < NB else None
-                av_sum_step(LEAD)
-                if 0 <= t < NB:
-                    qk_products(t)
-                else:
-                    run(shift_mid, t - 2)
-                run(shift_end, t - 2)
+                run(shift_end, t - 3)
+                t_o = av_sum_begin(t - 4) if 0 <= t - 4 < NB else None
+                av_sum_step(LEAD if t < NB else 0)
+                run(qk_products, t)
+                run(qk_sums, t - 1)
                 av_sum_step(len(work["todo"]))
-                run(softmax_a, t - 1)
-                run(qk_sums, t)
+                run(softmax_sum, t - 2)
+                av_products(t - 3, 0)
+                run(softmax_rec, t - 2)
+                av_products(t - 3, 1)
                 run(kv_out, t + 2)
-                run(av_products, t - 2)
                 run(regroup, t + 4)
                 run(quant, t + 3)
-                run(softmax_b, t - 1)
+                run(softmax_mul, t - 2)
+                run(shift_begin, t - 2)
+                av_products(t - 3, 2, (0, 1))
+                run(softmax_max, t - 1)
+                av_products(t - 3, 2, (2,))
+                run(softmax_sub, t - 1)
+                if t >= NB:
+                    run(softmax_exp, t - 1)
                 run(collect, t - 2)
+                run(shift_mid, t - 2)
                 if t_o is not None:
-                    av_sum_end(t - 3, t_o)
+                    av_sum_end(t - 4, t_o)
+                if t < NB:
+                    run(softmax_exp, t - 1)
                 mm, part = divmod(t - 5, MAC // R)
                 if 0 <= mm < H // MAC and part < len(NGROUPS):
                     attn_out(mm, part)

@@ -31,9 +31,10 @@ NGROUPS = ((0, 4), (4, 4), (8, 1))
 STEP_BUFS = 9
 FIRST = (0, 96, 160)
 LEAD = 24
-HEAD_SHARE = 3
-TAIL_SHARE = 3
-TAIL_BLOCKS = 4
+HEAD_SHARE = 4
+MID_SHARE = 2
+TAIL_SHARE = 4
+TAIL_BLOCKS = 0
 
 FLOPS = 2 * 3 * 128 * 512 * H * W + 2 * 2 * WIN * 128 * H * W
 
@@ -144,6 +145,7 @@ def tile_mutliheadattention2d_kernel(tc, x, Wq, Wk, Wv, rel_t, rel_f, out_0, out
         a16 = {}
         sh_ps = {}
         split = {}
+        rest = {}
         tops = {}
         sums = {}
         attn = {}
@@ -198,7 +200,7 @@ def tile_mutliheadattention2d_kernel(tc, x, Wq, Wk, Wv, rel_t, rel_f, out_0, out
             q_ps[b] = t_q
 
         def vector_share(b):
-            return HEAD_SHARE if b < 3 else (TAIL_SHARE if b == NB - 1 else 0)
+            return HEAD_SHARE if b < 3 else (TAIL_SHARE if b == NB - 1 else MID_SHARE)
 
         def qk_products(b):
             h0 = b * R
@@ -223,9 +225,12 @@ def tile_mutliheadattention2d_kernel(tc, x, Wq, Wk, Wv, rel_t, rel_f, out_0, out
                     else:
                         late.append((t_lo, t_p, t_hi))
                     parts.append((3 * j + i, t_hi, t_lo))
-            for t_lo, t_p, t_hi in late:
-                nc.vector.tensor_tensor(out=t_lo[:], in0=t_p[:], in1=t_hi[:], op=ALU.subtract)
             split[b] = parts
+            rest[b] = late
+
+        def qk_rest(b):
+            for t_lo, t_p, t_hi in rest[b]:
+                nc.vector.tensor_tensor(out=t_lo[:], in0=t_p[:], in1=t_hi[:], op=ALU.subtract)
 
         def qk_sums(b):
             t_e = psum.tile([P, WIN, NG, R], F32, name="e_ps", tag="eps")
@@ -382,6 +387,7 @@ def tile_mutliheadattention2d_kernel(tc, x, Wq, Wk, Wv, rel_t, rel_f, out_0, out
                 av_products(t - 3, 1)
                 run(kv_out, t + 2)
                 run(regroup, t + 4)
+                run(qk_rest, t)
                 run(quant, t + 3)
                 run(softmax_mul, t - 2)
                 run(shift_begin, t - 2)

@@ -29,12 +29,13 @@ NCHUNK = NB // CHUNK
 RAW_BUFS = 4
 NGROUPS = ((0, 4), (4, 4), (8, 1))
 STEP_BUFS = 9
-FIRST = (0, 96, 160)
-LEAD = 24
-HEAD_SHARE = 4
-MID_SHARE = 2
-TAIL_SHARE = 4
-TAIL_BLOCKS = 0
+LEAD = 36
+HEAD_SHARE = 3
+MID_SHARE = 0
+WHOLE = 2
+BESIDE = 4
+GR = NG * R
+TAIL_SHARE = 3
 
 FLOPS = 2 * 3 * 128 * 512 * H * W + 2 * 2 * WIN * 128 * H * W
 
@@ -59,7 +60,8 @@ def tile_mutliheadattention2d_kernel(tc, x, Wq, Wk, Wv, rel_t, rel_f, out_0, out
         codp = ctx.enter_context(tc.tile_pool(name="codp", bufs=3))
         prodp = ctx.enter_context(tc.tile_pool(name="prodp", bufs=2))
         stepp = ctx.enter_context(tc.tile_pool(name="stepp", bufs=STEP_BUFS))
-        halfp = ctx.enter_context(tc.tile_pool(name="halfp", bufs=2 * WIN))
+        halfp = ctx.enter_context(tc.tile_pool(name="halfp", bufs=2 * (WIN - WHOLE)))
+        wholep = ctx.enter_context(tc.tile_pool(name="wholep", bufs=2 * WHOLE))
         smallp = ctx.enter_context(tc.tile_pool(name="smallp", bufs=3))
         outp = ctx.enter_context(tc.tile_pool(name="outp", bufs=2))
         psum = ctx.enter_context(tc.psum_pool(name="psum", bufs=1))
@@ -102,6 +104,11 @@ def tile_mutliheadattention2d_kernel(tc, x, Wq, Wk, Wv, rel_t, rel_f, out_0, out
         nc.vector.tensor_reduce(out=gsum[:], in_=ident_f[:].rearrange("p (g c) -> p g c", c=CG), axis=AX.X, op=ALU.add)
         gsum_b = const.tile([P, NG], BF16, name="gsum_b")
         nc.vector.tensor_copy(out=gsum_b[:], in_=gsum[:])
+        atts = []
+        for idx in range(3):
+            t_att = const.tile([P, 3 * GR * 2 + P], F32, name="att%d" % idx)
+            nc.vector.memset(t_att[:], 0.0)
+            atts.append(t_att)
         pads = []
         for idx in range(2):
             t_pad = const.tile([P, 3, W + 2], F32, name="pad%d" % idx)
@@ -146,6 +153,7 @@ def tile_mutliheadattention2d_kernel(tc, x, Wq, Wk, Wv, rel_t, rel_f, out_0, out
         sh_ps = {}
         split = {}
         rest = {}
+        whole = {}
         tops = {}
         sums = {}
         attn = {}
@@ -208,46 +216,61 @@ def tile_mutliheadattention2d_kernel(tc, x, Wq, Wk, Wv, rel_t, rel_f, out_0, out
                 nc.vector.memset(k_ring[:, H % RK, :], 0.0)
             parts = []
             late = []
+            full = []
             for i in range(3):
                 runs = ring_runs(h0 + i - 1, R, RK)
                 for j in range(3):
                     n = 3 * i + j
-                    t_p = stepp.tile([P, R, W], F32, name="prod")
+                    if n < WIN - WHOLE:
+                        t_p = stepp.tile([P, R, W], F32, name="prod")
+                    else:
+                        t_p = wholep.tile([P, R, W], F32, name="prod32")
                     for off, slot, cnt in runs:
                         nc.vector.scalar_tensor_tensor(
                             out=t_p[:, off:off + cnt, :], in0=k_ring[:, slot:slot + cnt, j:j + W],
                             scalar=r9[:, n:n + 1], in1=q_ps[b][:, off:off + cnt, :], op0=ALU.add, op1=ALU.mult)
+                    if n >= WIN - WHOLE:
+                        full.append((3 * j + i, t_p))
+                        continue
                     t_hi = halfp.tile([P, R, W], BF16, name="p_hi")
                     nc.scalar.copy(out=t_hi[:], in_=t_p[:])
                     t_lo = halfp.tile([P, R, W], BF16, name="p_lo")
-                    if n < WIN - vector_share(b):
+                    if n < WIN - WHOLE - vector_share(b):
                         nc.gpsimd.tensor_tensor(out=t_lo[:], in0=t_p[:], in1=t_hi[:], op=ALU.subtract)
                     else:
                         late.append((t_lo, t_p, t_hi))
                     parts.append((3 * j + i, t_hi, t_lo))
             split[b] = parts
             rest[b] = late
+            whole[b] = full
 
         def qk_rest(b):
             for t_lo, t_p, t_hi in rest[b]:
                 nc.vector.tensor_tensor(out=t_lo[:], in0=t_p[:], in1=t_hi[:], op=ALU.subtract)
 
+        def qk_whole(b):
+            t_e = psum.tile([P, WIN, R, NG], F32, name="e_ps", tag="eps")
+            e_ps[b] = t_e
+            for m, t_p in whole[b]:
+                for r in range(R):
+                    nc.tensor.matmul(out=t_e[:, m, r, :], lhsT=t_p[:, r, :], rhs=gsum[:], start=True, stop=True)
+                    av_sum_step(BESIDE)
+
         def qk_sums(b):
-            t_e = psum.tile([P, WIN, NG, R], F32, name="e_ps", tag="eps")
+            t_e = e_ps[b]
             for m, t_hi, t_lo in split[b]:
                 for r in range(R):
-                    nc.tensor.matmul(out=t_e[:, m, :, r], lhsT=t_hi[:, r, :], rhs=gsum_b[:], start=True, stop=False)
-                    nc.tensor.matmul(out=t_e[:, m, :, r], lhsT=t_lo[:, r, :], rhs=gsum_b[:], start=False, stop=True)
-            e_ps[b] = t_e
+                    nc.tensor.matmul(out=t_e[:, m, r, :], lhsT=t_hi[:, r, :], rhs=gsum_b[:], start=True, stop=False)
+                    nc.tensor.matmul(out=t_e[:, m, r, :], lhsT=t_lo[:, r, :], rhs=gsum_b[:], start=False, stop=True)
 
         def softmax_max(b):
             t_m = smallp.tile([P, NG * R], F32, name="mx")
-            nc.vector.tensor_reduce(out=t_m[:], in_=e_ps[b][:].rearrange("p n g r -> p (g r) n"), axis=AX.X, op=ALU.max)
+            nc.vector.tensor_reduce(out=t_m[:], in_=e_ps[b][:].rearrange("p n r g -> p (r g) n"), axis=AX.X, op=ALU.max)
             tops[b] = t_m
 
         def softmax_sub(b):
             t_d = smallp.tile([P, WIN, NG * R], F32, name="dif")
-            nc.vector.tensor_tensor(out=t_d[:], in0=e_ps[b][:].rearrange("p n g r -> p n (g r)"),
+            nc.vector.tensor_tensor(out=t_d[:], in0=e_ps[b][:].rearrange("p n r g -> p n (r g)"),
                                     in1=tops[b][:].unsqueeze(1).to_broadcast([P, WIN, NG * R]), op=ALU.subtract)
             dif[b] = t_d
 
@@ -265,10 +288,9 @@ def tile_mutliheadattention2d_kernel(tc, x, Wq, Wk, Wv, rel_t, rel_f, out_0, out
             sums[b] = t_r
 
         def softmax_mul(b):
-            t_a = smallp.tile([P, WIN, NG, R], F32, name="att")
-            nc.vector.tensor_tensor(out=t_a[:], in0=dif[b][:].rearrange("p n (g r) -> p n g r", r=R),
-                                    in1=sums[b][:].rearrange("p (g r) -> p g r", r=R).unsqueeze(1).to_broadcast([P, WIN, NG, R]),
-                                    op=ALU.mult)
+            t_a = atts[b % len(atts)]
+            nc.vector.tensor_tensor(out=t_a[:, 0:WIN * GR].rearrange("p (n m) -> p n m", m=GR), in0=dif[b][:],
+                                    in1=sums[b][:].unsqueeze(1).to_broadcast([P, WIN, GR]), op=ALU.mult)
             attn[b] = t_a
 
         def collect(b):
@@ -277,13 +299,13 @@ def tile_mutliheadattention2d_kernel(tc, x, Wq, Wk, Wv, rel_t, rel_f, out_0, out
                 t_a = outp.tile([P, WIN, NG, MAC], F32, name="a16")
                 a16[m] = t_a
             hs = (b * R) % MAC
-            nc.scalar.copy(out=a16[m][:, :, :, hs:hs + R], in_=attn[b][:])
+            nc.scalar.copy(out=a16[m][:, :, :, hs:hs + R],
+                           in_=attn[b][:, 0:WIN * GR].rearrange("p (n r g) -> p n g r", r=R, g=NG))
 
         def shift_begin(b):
-            flat = attn[b][:].rearrange("p n g r -> p (n g r)")
             t_f = psum.tile([P, 3, W], F32, name="f_ps", tag="tps")
             for j in range(3):
-                nc.tensor.transpose(t_f[:, j, :], flat[:, FIRST[j]:FIRST[j] + P], ident_f[:])
+                nc.tensor.transpose(t_f[:, j, :], attn[b][:, 3 * GR * j:3 * GR * j + P], ident_f[:])
             f_ps[b] = t_f
 
         def shift_mid(b):
@@ -295,32 +317,23 @@ def tile_mutliheadattention2d_kernel(tc, x, Wq, Wk, Wv, rel_t, rel_f, out_0, out
                 nc.tensor.transpose(t_sh[:, j, :], pads[b % 2][:, j, 2 - j:2 - j + W], ident_f[:])
             sh_ps[b] = t_sh
 
-        def av_products(b, j, rows=(0, 1, 2)):
+        def av_products(b, i):
             if not 0 <= b < NB:
                 return
             h0 = b * R
-            if j == 0:
+            if i == 0:
                 t_new = prodp.tile([P, WIN, R, P], F32, name="avp")
                 avp[b] = t_new
             t_q = avp[b]
-            if True:
-                for i in rows:
-                    n = 3 * i + j
-                    lo = max(0, 1 - i - h0)
-                    hi = min(R, H + 1 - i - h0)
-                    for off, slot, cnt in ring_runs(h0 + lo + i - 1, hi - lo, RV):
-                        a = lo + off
-                        col = (3 * j + i) * NG * R - FIRST[j]
-                        att = sh_ps[b][:, j, col:col + NG * R].rearrange("p (g r) -> p g r", r=R)[:, :, a:a + cnt]
-                        eng = nc.vector
-                        if j == 1 and b >= NB - TAIL_BLOCKS:
-                            att = attn[b][:, 3 + i, :, a:a + cnt]
-                            eng = nc.gpsimd
-                        eng.tensor_tensor(
-                            out=t_q[:, n, a:a + cnt, :].rearrange("p r (g c) -> p r g c", c=CG),
-                            in0=v_ring[:, slot:slot + cnt, :].rearrange("p r (g c) -> p r g c", c=CG),
-                            in1=att.rearrange("p g r -> p r g").unsqueeze(3).to_broadcast([P, cnt, NG, CG]),
-                            op=ALU.mult)
+            lo = max(0, 1 - i - h0)
+            hi = min(R, H + 1 - i - h0)
+            for off, slot, cnt in ring_runs(h0 + lo + i - 1, hi - lo, RV):
+                a = lo + off
+                nc.vector.tensor_tensor(
+                    out=t_q[:, 3 * i:3 * i + 3, a:a + cnt, :].rearrange("p j r (g c) -> p j (r g) c", c=CG),
+                    in0=v_ring[:, slot:slot + cnt, :].rearrange("p r (g c) -> p (r g) c", c=CG).unsqueeze(1).to_broadcast([P, 3, cnt * NG, CG]),
+                    in1=sh_ps[b][:, :, i * GR + a * NG:i * GR + (a + cnt) * NG].unsqueeze(3).to_broadcast([P, 3, cnt * NG, CG]),
+                    op=ALU.mult)
 
         work = {"todo": [], "pos": 0}
 
@@ -377,7 +390,8 @@ def tile_mutliheadattention2d_kernel(tc, x, Wq, Wk, Wv, rel_t, rel_f, out_0, out
                 run(mx_q, t + 1)
                 run(shift_end, t - 3)
                 t_o = av_sum_begin(t - 4) if 0 <= t - 4 < NB else None
-                av_sum_step(LEAD if t < NB else 0)
+                run(qk_whole, t - 1)
+                av_sum_step(max(0, LEAD - 4 * WHOLE * BESIDE) if t < NB else 0)
                 run(qk_products, t)
                 run(qk_sums, t - 1)
                 av_sum_step(len(work["todo"]))
@@ -387,22 +401,18 @@ def tile_mutliheadattention2d_kernel(tc, x, Wq, Wk, Wv, rel_t, rel_f, out_0, out
                 av_products(t - 3, 1)
                 run(kv_out, t + 2)
                 run(regroup, t + 4)
+                if t_o is not None:
+                    av_sum_end(t - 4, t_o)
+                mm, part = divmod(t - 6, MAC // R)
+                if 0 <= mm < H // MAC and part < len(NGROUPS):
+                    attn_out(mm, part)
                 run(qk_rest, t)
                 run(quant, t + 3)
                 run(softmax_mul, t - 2)
                 run(shift_begin, t - 2)
-                av_products(t - 3, 2, (0, 1))
+                av_products(t - 3, 2)
                 run(softmax_max, t - 1)
-                av_products(t - 3, 2, (2,))
                 run(softmax_sub, t - 1)
-                if t >= NB:
-                    run(softmax_exp, t - 1)
                 run(collect, t - 2)
                 run(shift_mid, t - 2)
-                if t_o is not None:
-                    av_sum_end(t - 4, t_o)
-                if t < NB:
-                    run(softmax_exp, t - 1)
-                mm, part = divmod(t - 5, MAC // R)
-                if 0 <= mm < H // MAC and part < len(NGROUPS):
-                    attn_out(mm, part)
+                run(softmax_exp, t - 1)

@@ -19,23 +19,20 @@ NG = 8
 CG = 16
 WIN = 9
 R = 4
-NB = H // R
+NQ = H // R
 PIX = R * W
-RK = 16
-RV = 32
-MAC = 16
-CHUNK = 2
-NCHUNK = NB // CHUNK
+MBR = 16
+QPM = MBR // R
+NMB = H // MBR
+SUB = 3 * QPM
+RQ = 32
+RK = 36
+RV = 64
 RAW_BUFS = 4
-NGROUPS = ((0, 4), (4, 4), (8, 1))
-STEP_BUFS = 9
-LEAD = 36
-HEAD_SHARE = 3
-MID_SHARE = 0
-WHOLE = 2
-BESIDE = 4
-GR = NG * R
-TAIL_SHARE = 3
+LAG = 24
+ESTEP = 13
+ASTEP = 12
+TAIL_MB = 6
 
 FLOPS = 2 * 3 * 128 * 512 * H * W + 2 * 2 * WIN * 128 * H * W
 
@@ -56,14 +53,16 @@ def tile_mutliheadattention2d_kernel(tc, x, Wq, Wk, Wv, rel_t, rel_f, out_0, out
     with ExitStack() as ctx:
         const = ctx.enter_context(tc.tile_pool(name="const", bufs=1))
         rawp = ctx.enter_context(tc.tile_pool(name="rawp", bufs=RAW_BUFS))
-        grpp = ctx.enter_context(tc.tile_pool(name="grpp", bufs=3))
+        grpp = ctx.enter_context(tc.tile_pool(name="grpp", bufs=2))
         codp = ctx.enter_context(tc.tile_pool(name="codp", bufs=3))
-        prodp = ctx.enter_context(tc.tile_pool(name="prodp", bufs=2))
-        stepp = ctx.enter_context(tc.tile_pool(name="stepp", bufs=STEP_BUFS))
-        halfp = ctx.enter_context(tc.tile_pool(name="halfp", bufs=2 * (WIN - WHOLE)))
-        wholep = ctx.enter_context(tc.tile_pool(name="wholep", bufs=2 * WHOLE))
-        smallp = ctx.enter_context(tc.tile_pool(name="smallp", bufs=3))
+        pp = ctx.enter_context(tc.tile_pool(name="pp", bufs=6))
+        qrp = ctx.enter_context(tc.tile_pool(name="qrp", bufs=2))
+        esp = ctx.enter_context(tc.tile_pool(name="esp", bufs=2))
+        shp = ctx.enter_context(tc.tile_pool(name="shp", bufs=4))
+        pvp = ctx.enter_context(tc.tile_pool(name="pvp", bufs=6))
         outp = ctx.enter_context(tc.tile_pool(name="outp", bufs=2))
+        attp = ctx.enter_context(tc.tile_pool(name="attp", bufs=1))
+        smallp = ctx.enter_context(tc.tile_pool(name="smallp", bufs=2))
         psum = ctx.enter_context(tc.psum_pool(name="psum", bufs=1))
 
         xv = x.rearrange("b (p j) h w -> p (b j) (h w)", j=4)
@@ -72,22 +71,20 @@ def tile_mutliheadattention2d_kernel(tc, x, Wq, Wk, Wv, rel_t, rel_f, out_0, out
 
         raw = {}
 
-        def load(c):
-            t_raw = rawp.tile([P, 4, CHUNK * PIX], BF16, name="raw")
-            nc.sync.dma_start(out=t_raw[:], in_=xv[:, :, c * CHUNK * PIX:(c + 1) * CHUNK * PIX])
-            raw[c] = t_raw
+        def load(q):
+            t_raw = rawp.tile([P, 4, PIX], BF16, name="raw")
+            nc.sync.dma_start(out=t_raw[:], in_=xv[:, :, q * PIX:(q + 1) * PIX])
+            raw[q] = t_raw
 
-        w_raw = []
+        w_raw = pp.tile([P, 3, 512], BF16, name="w_raw", tag="big", align_bytes=64)
         for idx, wsrc in enumerate((Wq, Wk, Wv)):
-            t_w = const.tile([P, 512], BF16, name="w_raw%d" % idx)
-            nc.sync.dma_start(out=t_w[:], in_=wsrc)
-            w_raw.append(t_w)
+            nc.sync.dma_start(out=w_raw[:, idx, :], in_=wsrc)
         load(0)
         rel_sb = const.tile([P, 3], BF16, name="rel_sb")
         nc.sync.dma_start(out=rel_sb[0:64, :], in_=rel_t)
         nc.sync.dma_start(out=rel_sb[64:128, :], in_=rel_f)
-        for c in range(1, RAW_BUFS):
-            load(c)
+        for q in range(1, RAW_BUFS):
+            load(q)
 
         ident_f = const.tile([P, P], F32, name="ident_f")
         masks.make_identity(nc, ident_f[:])
@@ -100,319 +97,329 @@ def tile_mutliheadattention2d_kernel(tc, x, Wq, Wk, Wv, rel_t, rel_f, out_0, out
         nc.vector.tensor_copy(out=perm2[:, 0:P - 1], in_=ident_f[:, 1:P])
         nc.vector.tensor_copy(out=perm2[:, P - 1:P], in_=ident_f[:, 0:1])
         perms = (perm0, ident_f, perm2)
-        gsum = const.tile([P, NG], F32, name="gsum")
-        nc.vector.tensor_reduce(out=gsum[:], in_=ident_f[:].rearrange("p (g c) -> p g c", c=CG), axis=AX.X, op=ALU.add)
-        gsum_b = const.tile([P, NG], BF16, name="gsum_b")
-        nc.vector.tensor_copy(out=gsum_b[:], in_=gsum[:])
-        atts = []
-        for idx in range(3):
-            t_att = const.tile([P, 3 * GR * 2 + P], F32, name="att%d" % idx)
-            nc.vector.memset(t_att[:], 0.0)
-            atts.append(t_att)
-        pads = []
-        for idx in range(2):
-            t_pad = const.tile([P, 3, W + 2], F32, name="pad%d" % idx)
-            nc.vector.memset(t_pad[:], 0.0)
-            pads.append(t_pad)
+        chperm = const.tile([P, P], F32, name="chperm")
+        nc.vector.tensor_copy(out=chperm[:].rearrange("p (c g) -> p c g", g=NG),
+                              in_=ident_f[:].rearrange("p (g c) -> p c g", c=CG))
+        gmask = const.tile([P, NG], F32, name="gmask")
+        nc.vector.tensor_reduce(out=gmask[:], in_=ident_f[:].rearrange("p (c g) -> p g c", g=NG), axis=AX.X, op=ALU.add)
         r9 = const.tile([P, WIN], F32, name="r9")
         nc.vector.tensor_copy(out=r9[0:64, :].rearrange("p (i j) -> p i j", j=3),
                               in_=rel_sb[0:64, :].unsqueeze(2).to_broadcast([64, 3, 3]))
         nc.vector.tensor_copy(out=r9[64:128, :].rearrange("p (i j) -> p i j", j=3),
                               in_=rel_sb[64:128, :].unsqueeze(1).to_broadcast([64, 3, 3]))
-        k_ring = const.tile([P, RK, W + 2], F32, name="k_ring")
+        r9_ps = psum.tile([P, WIN], F32, name="r9_ps", tag="aux")
+        nc.tensor.matmul(out=r9_ps[:], lhsT=chperm[:], rhs=r9[:], start=True, stop=True)
+        r9p = const.tile([P, WIN], F32, name="r9p")
+        nc.vector.tensor_copy(out=r9p[:], in_=r9_ps[:])
+        rmat = const.tile([P, WIN, NG], F32, name="rmat")
+        nc.vector.tensor_tensor(out=rmat[:], in0=r9p[:].unsqueeze(2).to_broadcast([P, WIN, NG]),
+                                in1=gmask[:].unsqueeze(1).to_broadcast([P, WIN, NG]), op=ALU.mult)
+        atts = []
+        for idx in range(2):
+            t_att = const.tile([P, WIN, W + 2], F32, name="att%d" % idx)
+            nc.gpsimd.memset(t_att[:], 0.0)
+            atts.append(t_att)
+        q_ring = const.tile([P, RQ, W + 2], F32, name="q_ring")
+        nc.gpsimd.memset(q_ring[:], 0.0)
+        k_ring = const.tile([P, RK, P], F32, name="k_ring")
         nc.gpsimd.memset(k_ring[:], 0.0)
         v_ring = const.tile([P, RV, P], F32, name="v_ring")
 
+        w_de = pp.tile([P, 3, 4, P], BF16, name="w_de", tag="big", align_bytes=64)
+        w_grp = pp.tile([P, 3, P, 4], BF16, name="w_grp", tag="big", align_bytes=64)
         w_codes = []
         w_scales = []
-        w_tp = []
         for idx in range(3):
-            w_de = const.tile([P, 4, P], BF16, name="w_de%d" % idx)
-            nc.scalar.copy(out=w_de[:], in_=w_raw[idx][:].rearrange("o (p t) -> o t p", t=4))
-            w_ps = psum.tile([P, 4, P], BF16, name="w_ps", tag=("tps", "kps", "vps")[idx])
+            nc.scalar.copy(out=w_de[:, idx, :, :], in_=w_raw[:, idx, :].rearrange("o (p t) -> o t p", t=4))
+            w_ps = psum.tile([P, 4, P], BF16, name="w_ps", tag="mx", bufs=2)
             for t in range(4):
-                nc.tensor.transpose(w_ps[:, t, :], w_de[:, t, :], ident_b[:])
-            w_tp.append(w_ps)
-        for idx in range(3):
-            w_grp = const.tile([P, P, 4], BF16, name="w_grp%d" % idx, align_bytes=64)
-            nc.vector.tensor_copy(out=w_grp[:], in_=w_tp[idx][:].rearrange("p t o -> p o t"))
+                nc.tensor.transpose(w_ps[:, t, :], w_de[:, idx, t, :], ident_b[:])
+            if idx < 2:
+                nc.vector.tensor_copy(out=w_grp[:, idx, :, :].rearrange("p (c g) t -> p c g t", g=NG),
+                                      in_=w_ps[:].rearrange("p t (g c) -> p c g t", c=CG))
+            else:
+                nc.vector.tensor_copy(out=w_grp[:, idx, :, :], in_=w_ps[:].rearrange("p t o -> p o t"))
             w_c = const.tile([P, P], U32, name="w_c%d" % idx, align_bytes=64)
             w_s = const.tile([P, P], U8, name="w_s%d" % idx, align_bytes=64)
-            nc.vector.quantize_mx(out=w_c[:].bitcast(FP8X4), scales=w_s[:], in_=w_grp[:].rearrange("p o t -> p (o t)"))
+            nc.vector.quantize_mx(out=w_c[:].bitcast(FP8X4), scales=w_s[:],
+                                  in_=w_grp[:, idx, :, :].rearrange("p o t -> p (o t)"))
             w_codes.append(w_c)
             w_scales.append(w_s)
 
         grp = {}
         xc = {}
         xs = {}
-        q_ps = {}
+        mxt = {}
+        qr9 = {}
+        qjt = {}
         prod = {}
-        e_ps = {}
-        dif = {}
-        a16 = {}
-        sh_ps = {}
-        split = {}
-        rest = {}
-        whole = {}
+        esb = {}
         tops = {}
         sums = {}
-        attn = {}
-        f_ps = {}
-        kv_ps = {}
-        avp = {}
+        sh = {}
+        pv = {}
 
-        def regroup(b):
+        def regroup(q):
             t_g = grpp.tile([P, PIX, 4], BF16, name="grp", align_bytes=64)
-            src = raw[b // CHUNK][:, :, (b % CHUNK) * PIX:(b % CHUNK + 1) * PIX]
-            if b in (1, 3):
+            if q in (1, 3):
                 nc.vector.tensor_copy(out=t_g[:].rearrange("p (c i) t -> p c t i", i=4),
-                                      in_=src.rearrange("p t (c i) -> p c t i", i=4))
+                                      in_=raw[q][:].rearrange("p t (c i) -> p c t i", i=4))
             else:
                 nc.scalar.copy(out=t_g[:].rearrange("p (c i) t -> p c t i", i=4),
-                               in_=src.rearrange("p t (c i) -> p c t i", i=4))
-            grp[b] = t_g
-            if b % CHUNK == CHUNK - 1 and b // CHUNK + RAW_BUFS < NCHUNK:
-                load(b // CHUNK + RAW_BUFS)
+                               in_=raw[q][:].rearrange("p t (c i) -> p c t i", i=4))
+            grp[q] = t_g
+            if q + RAW_BUFS < NQ:
+                load(q + RAW_BUFS)
 
-        def quant(b):
+        def quant(q):
             t_c = codp.tile([P, PIX], U32, name="xc", align_bytes=64)
             t_s = codp.tile([P, PIX], U8, name="xs", align_bytes=64)
-            nc.vector.quantize_mx(out=t_c[:].bitcast(FP8X4), scales=t_s[:], in_=grp[b][:].rearrange("p c t -> p (c t)"))
-            xc[b] = t_c
-            xs[b] = t_s
+            nc.vector.quantize_mx(out=t_c[:].bitcast(FP8X4), scales=t_s[:], in_=grp[q][:].rearrange("p c t -> p (c t)"))
+            xc[q] = t_c
+            xs[q] = t_s
 
-        def mx_w_stationary(dst, widx, b):
-            nc.tensor.matmul_mx(out=dst, lhsT=w_codes[widx][:].bitcast(FP8X4), lhsT_scale=w_scales[widx][:],
-                                rhs=xc[b][:].bitcast(FP8X4), rhs_scale=xs[b][:], start=True, stop=True)
-
-        def mx_kv(b):
-            k_ps = psum.tile([P, R, W], F32, name="k_ps", tag="kps")
-            mx_w_stationary(k_ps[:].rearrange("p r w -> p (r w)"), 1, b)
-            v_ps = psum.tile([P, R, P], F32, name="v_ps", tag="vps")
+        def mx_pixel(q, widx, name):
+            t_ps = psum.tile([P, R, P], F32, name=name, tag="mx", bufs=2)
             for r in range(R):
                 cols = slice(r * W, (r + 1) * W)
-                nc.tensor.matmul_mx(out=v_ps[:, r, :], lhsT=xc[b][:, cols].bitcast(FP8X4), lhsT_scale=xs[b][:, cols],
-                                    rhs=w_codes[2][:].bitcast(FP8X4), rhs_scale=w_scales[2][:], start=True, stop=True)
-            kv_ps[b] = (k_ps, v_ps)
+                nc.tensor.matmul_mx(out=t_ps[:, r, :], lhsT=xc[q][:, cols].bitcast(FP8X4), lhsT_scale=xs[q][:, cols],
+                                    rhs=w_codes[widx][:].bitcast(FP8X4), rhs_scale=w_scales[widx][:], start=True, stop=True)
+            return t_ps
 
-        def kv_out(b):
-            k_ps, v_ps = kv_ps[b]
-            ks = (b * R) % RK
-            nc.scalar.copy(out=k_ring[:, ks:ks + R, 1:W + 1], in_=k_ps[:])
-            vs = (b * R) % RV
+        def mx_qk(q):
+            q_ps = psum.tile([P, R, W], F32, name="q_ps", tag="mx", bufs=2)
+            nc.tensor.matmul_mx(out=q_ps[:].rearrange("p r w -> p (r w)"), lhsT=w_codes[0][:].bitcast(FP8X4),
+                                lhsT_scale=w_scales[0][:], rhs=xc[q][:].bitcast(FP8X4), rhs_scale=xs[q][:],
+                                start=True, stop=True)
+            k_ps = mx_pixel(q, 1, "k_ps")
+            qs = (q * R) % RQ
+            nc.scalar.copy(out=q_ring[:, qs:qs + R, 1:W + 1], in_=q_ps[:])
+            ks = (q * R) % RK
+            nc.scalar.copy(out=k_ring[:, ks:ks + R, :], in_=k_ps[:])
+
+        def mx_v(q):
+            v_ps = mx_pixel(q, 2, "v_ps")
+            vs = (q * R) % RV
             nc.scalar.copy(out=v_ring[:, vs:vs + R, :], in_=v_ps[:])
 
-        def mx_q(b):
-            t_q = psum.tile([P, R, W], F32, name="q_ps", tag="qps", bufs=2)
-            mx_w_stationary(t_q[:].rearrange("p r w -> p (r w)"), 0, b)
-            q_ps[b] = t_q
-
-        def vector_share(b):
-            return HEAD_SHARE if b < 3 else (TAIL_SHARE if b == NB - 1 else MID_SHARE)
-
-        def qk_products(b):
-            h0 = b * R
-            if b == NB - 1:
-                nc.vector.memset(k_ring[:, H % RK, :], 0.0)
-            parts = []
-            late = []
-            full = []
-            for i in range(3):
-                runs = ring_runs(h0 + i - 1, R, RK)
-                for j in range(3):
-                    n = 3 * i + j
-                    if n < WIN - WHOLE:
-                        t_p = stepp.tile([P, R, W], F32, name="prod")
-                    else:
-                        t_p = wholep.tile([P, R, W], F32, name="prod32")
-                    for off, slot, cnt in runs:
-                        nc.vector.scalar_tensor_tensor(
-                            out=t_p[:, off:off + cnt, :], in0=k_ring[:, slot:slot + cnt, j:j + W],
-                            scalar=r9[:, n:n + 1], in1=q_ps[b][:, off:off + cnt, :], op0=ALU.add, op1=ALU.mult)
-                    if n >= WIN - WHOLE:
-                        full.append((3 * j + i, t_p))
-                        continue
-                    t_hi = halfp.tile([P, R, W], BF16, name="p_hi")
-                    nc.scalar.copy(out=t_hi[:], in_=t_p[:])
-                    t_lo = halfp.tile([P, R, W], BF16, name="p_lo")
-                    if n < WIN - WHOLE - vector_share(b):
-                        nc.gpsimd.tensor_tensor(out=t_lo[:], in0=t_p[:], in1=t_hi[:], op=ALU.subtract)
-                    else:
-                        late.append((t_lo, t_p, t_hi))
-                    parts.append((3 * j + i, t_hi, t_lo))
-            split[b] = parts
-            rest[b] = late
-            whole[b] = full
-
-        def qk_rest(b):
-            for t_lo, t_p, t_hi in rest[b]:
-                nc.vector.tensor_tensor(out=t_lo[:], in0=t_p[:], in1=t_hi[:], op=ALU.subtract)
-
-        def qk_whole(b):
-            t_e = psum.tile([P, WIN, R, NG], F32, name="e_ps", tag="eps")
-            e_ps[b] = t_e
-            for m, t_p in whole[b]:
-                for r in range(R):
-                    nc.tensor.matmul(out=t_e[:, m, r, :], lhsT=t_p[:, r, :], rhs=gsum[:], start=True, stop=True)
-                    av_sum_step(BESIDE)
-
-        def qk_sums(b):
-            t_e = e_ps[b]
-            for m, t_hi, t_lo in split[b]:
-                for r in range(R):
-                    nc.tensor.matmul(out=t_e[:, m, r, :], lhsT=t_hi[:, r, :], rhs=gsum_b[:], start=True, stop=False)
-                    nc.tensor.matmul(out=t_e[:, m, r, :], lhsT=t_lo[:, r, :], rhs=gsum_b[:], start=False, stop=True)
-
-        def softmax_max(b):
-            t_m = smallp.tile([P, NG * R], F32, name="mx")
-            nc.vector.tensor_reduce(out=t_m[:], in_=e_ps[b][:].rearrange("p n r g -> p (r g) n"), axis=AX.X, op=ALU.max)
-            tops[b] = t_m
-
-        def softmax_sub(b):
-            t_d = smallp.tile([P, WIN, NG * R], F32, name="dif")
-            nc.vector.tensor_tensor(out=t_d[:], in0=e_ps[b][:].rearrange("p n r g -> p n (r g)"),
-                                    in1=tops[b][:].unsqueeze(1).to_broadcast([P, WIN, NG * R]), op=ALU.subtract)
-            dif[b] = t_d
-
-        def softmax_exp(b):
-            nc.scalar.activation(out=dif[b][:], in_=dif[b][:], func=ACT.Exp)
-
-        def softmax_sum(b):
-            t_s = smallp.tile([P, NG * R], F32, name="ssum")
-            nc.vector.tensor_reduce(out=t_s[:], in_=dif[b][:].rearrange("p n m -> p m n"), axis=AX.X, op=ALU.add)
-            sums[b] = t_s
-
-        def softmax_rec(b):
-            t_r = smallp.tile([P, NG * R], F32, name="rsum")
-            nc.vector.reciprocal(out=t_r[:], in_=sums[b][:])
-            sums[b] = t_r
-
-        def softmax_mul(b):
-            t_a = atts[b % len(atts)]
-            nc.vector.tensor_tensor(out=t_a[:, 0:WIN * GR].rearrange("p (n m) -> p n m", m=GR), in0=dif[b][:],
-                                    in1=sums[b][:].unsqueeze(1).to_broadcast([P, WIN, GR]), op=ALU.mult)
-            attn[b] = t_a
-
-        def collect(b):
-            m = b // (MAC // R)
-            if b % (MAC // R) == 0:
-                t_a = outp.tile([P, WIN, NG, MAC], F32, name="a16")
-                a16[m] = t_a
-            hs = (b * R) % MAC
-            nc.scalar.copy(out=a16[m][:, :, :, hs:hs + R],
-                           in_=attn[b][:, 0:WIN * GR].rearrange("p (n r g) -> p n g r", r=R, g=NG))
-
-        def shift_begin(b):
-            t_f = psum.tile([P, 3, W], F32, name="f_ps", tag="tps")
-            for j in range(3):
-                nc.tensor.transpose(t_f[:, j, :], attn[b][:, 3 * GR * j:3 * GR * j + P], ident_f[:])
-            f_ps[b] = t_f
-
-        def shift_mid(b):
-            nc.scalar.copy(out=pads[b % 2][:, :, 1:W + 1], in_=f_ps[b][:])
-
-        def shift_end(b):
-            t_sh = psum.tile([P, 3, P], F32, name="sh_ps", tag="shps")
-            for j in range(3):
-                nc.tensor.transpose(t_sh[:, j, :], pads[b % 2][:, j, 2 - j:2 - j + W], ident_f[:])
-            sh_ps[b] = t_sh
-
-        def av_products(b, i):
-            if not 0 <= b < NB:
-                return
-            h0 = b * R
-            if i == 0:
-                t_new = prodp.tile([P, WIN, R, P], F32, name="avp")
-                avp[b] = t_new
-            t_q = avp[b]
-            lo = max(0, 1 - i - h0)
-            hi = min(R, H + 1 - i - h0)
-            for off, slot, cnt in ring_runs(h0 + lo + i - 1, hi - lo, RV):
-                a = lo + off
-                nc.vector.tensor_tensor(
-                    out=t_q[:, 3 * i:3 * i + 3, a:a + cnt, :].rearrange("p j r (g c) -> p j (r g) c", c=CG),
-                    in0=v_ring[:, slot:slot + cnt, :].rearrange("p r (g c) -> p (r g) c", c=CG).unsqueeze(1).to_broadcast([P, 3, cnt * NG, CG]),
-                    in1=sh_ps[b][:, :, i * GR + a * NG:i * GR + (a + cnt) * NG].unsqueeze(3).to_broadcast([P, 3, cnt * NG, CG]),
-                    op=ALU.mult)
-
-        work = {"todo": [], "pos": 0}
-
-        def av_sum_begin(b):
-            h0 = b * R
-            pending = []
-            work["todo"] = pending
-            work["pos"] = 0
-            t_o = psum.tile([P, R, W], F32, name="o_ps", tag="ops")
+        def q_rel(q):
+            m, a = divmod(q, QPM)
+            qs = (q * R) % RQ
+            t_ps = psum.tile([P, R, WIN * NG], F32, name="qr_ps", tag="aux")
             for r in range(R):
-                terms = [(i, j) for i in range(3) for j in range(3) if 0 <= h0 + r + i - 1 < H]
-                for idx, (i, j) in enumerate(terms):
-                    pending.append((t_o[:, r, :], avp[b][:, 3 * i + j, r, :], perms[j], idx == 0, idx == len(terms) - 1))
-            return t_o
+                nc.tensor.matmul(out=t_ps[:, r, :], lhsT=q_ring[:, qs + r, 1:W + 1],
+                                 rhs=rmat[:].rearrange("p n g -> p (n g)"), start=True, stop=True)
+            if a == 0:
+                t_new = qrp.tile([P, WIN, P], F32, name="qr9")
+                qr9[m] = t_new
+            nc.scalar.copy(out=qr9[m][:, :, a * R * NG:(a + 1) * R * NG].rearrange("p n (r g) -> p n r g", g=NG),
+                           in_=t_ps[:].rearrange("p r (n g) -> p n r g", g=NG))
 
-        def av_sum_step(count):
+        def decode(u):
+            m, rem = divmod(u, SUB)
+            j, a = divmod(rem, QPM)
+            return m, j, a
+
+        def q_shift(u):
+            m, j, a = decode(u)
+            qs = ((m * QPM + a) * R) % RQ
+            t_ps = psum.tile([P, R, P], F32, name="qj", tag="qj", bufs=2)
+            for r in range(R):
+                nc.tensor.transpose(t_ps[:, r, :], q_ring[:, qs + r, 2 - j:2 - j + W], ident_f[:])
+            qjt[u] = t_ps
+
+        def qk_products(u):
+            m, j, a = decode(u)
+            h0 = m * MBR + a * R
+            if u == (NMB - 1) * SUB:
+                nc.gpsimd.memset(k_ring[:, H % RK, :], 0.0)
+            for i in range(3):
+                n = 3 * i + j
+                if a == 0:
+                    t_new = pp.tile([P, CG, P], F32, name="prod", tag="big", align_bytes=64)
+                    prod[(m, n)] = t_new
+                t_p = prod[(m, n)]
+                for off, slot, cnt in ring_runs(h0 + i - 1, R, RK):
+                    c0 = (a * R + off) * NG
+                    nc.vector.tensor_tensor(
+                        out=t_p[:, :, c0:c0 + cnt * NG].rearrange("p c (r g) -> p c r g", g=NG),
+                        in0=k_ring[:, slot:slot + cnt, :].rearrange("p r (c g) -> p c r g", g=NG),
+                        in1=qjt[u][:, off:off + cnt, :].rearrange("p r (c g) -> p c r g", g=NG), op=ALU.mult)
+
+        ework = {"todo": [], "pos": 0, "tile": None}
+
+        def e_begin(f):
+            m, j = divmod(f, 3)
+            t_e = psum.tile([P, 3, W], F32, name="e_ps", tag="eps")
+            pending = []
+            for i in range(3):
+                n = 3 * i + j
+                for c in range(CG):
+                    pending.append((t_e[:, i, :], prod[(m, n)][:, c, :], perms[j], c == 0, False))
+                pending.append((t_e[:, i, :], qr9[m][:, n, :], ident_f, False, True))
+            ework["todo"] = pending
+            ework["pos"] = 0
+            ework["tile"] = t_e
+
+        def work_step(work, count):
             todo = work["todo"]
             for step in range(work["pos"], min(work["pos"] + count, len(todo))):
                 dst, lhs, perm, first, last = todo[step]
                 nc.tensor.matmul(out=dst, lhsT=lhs, rhs=perm[:], start=first, stop=last, is_transpose=True)
             work["pos"] = min(work["pos"] + count, len(todo))
 
-        def av_sum_end(b, t_o):
-            h0 = b * R
-            av_sum_step(len(work["todo"]))
+        def e_end(f):
+            m, j = divmod(f, 3)
+            work_step(ework, len(ework["todo"]))
+            if j == 0:
+                t_new = esp.tile([P, 3, 3, W], F32, name="esb")
+                esb[m] = t_new
+            nc.scalar.copy(out=esb[m][:, :, j, :], in_=ework["tile"][:])
+
+        def softmax_max(m):
+            t_m = smallp.tile([P, W], F32, name="mx")
+            nc.vector.tensor_reduce(out=t_m[:], in_=esb[m][:].rearrange("p i j w -> p w (i j)"), axis=AX.X, op=ALU.max)
+            tops[m] = t_m
+
+        def softmax_sub(m):
+            flat = esb[m][:].rearrange("p i j w -> p (i j) w")
+            nc.vector.tensor_tensor(out=flat, in0=flat, in1=tops[m][:].unsqueeze(1).to_broadcast([P, WIN, W]), op=ALU.subtract)
+            nc.scalar.activation(out=flat, in_=flat, func=ACT.Exp)
+
+        def softmax_sum(m):
+            t_s = smallp.tile([P, W], F32, name="ssum")
+            nc.vector.tensor_reduce(out=t_s[:], in_=esb[m][:].rearrange("p i j w -> p w (i j)"), axis=AX.X, op=ALU.add)
+            t_r = smallp.tile([P, W], F32, name="rsum")
+            nc.vector.reciprocal(out=t_r[:], in_=t_s[:])
+            sums[m] = t_r
+
+        def softmax_mul(m):
+            t_a = atts[m % 2]
+            nc.vector.tensor_tensor(out=t_a[:, :, 1:W + 1], in0=esb[m][:].rearrange("p i j w -> p (i j) w"),
+                                    in1=sums[m][:].unsqueeze(1).to_broadcast([P, WIN, W]), op=ALU.mult)
+            t_t = attp.tile([P, W, WIN], F32, name="t_out")
+            nc.scalar.copy(out=t_t[:], in_=t_a[:, :, 1:W + 1].rearrange("p n w -> p w n"))
+            for r in range(MBR):
+                nc.sync.dma_start(out=o1[:, m * MBR + r, :], in_=t_t[r * NG:(r + 1) * NG, :, :].rearrange("p w n -> p (w n)"))
+
+        def in_psum(m, i):
+            return i == 1 or (m >= TAIL_MB and i == 2)
+
+        def shift(m, i):
+            tag = "shv" if i == 1 else ("qj" if in_psum(m, i) else "aux")
+            if tag == "qj":
+                t_ps = psum.tile([P, 3, P], F32, name="sh_ps", tag="qj", bufs=2)
+            else:
+                t_ps = psum.tile([P, 3, P], F32, name="sh_ps", tag=tag)
+            for j in range(3):
+                nc.tensor.transpose(t_ps[:, j, :], atts[m % 2][:, 3 * i + j, 2 - j:2 - j + W], ident_f[:])
+            if in_psum(m, i):
+                sh[(m, i)] = t_ps
+            else:
+                t_sb = shp.tile([P, 3, P], F32, name="sh_sb")
+                nc.scalar.copy(out=t_sb[:], in_=t_ps[:])
+                sh[(m, i)] = t_sb
+
+        def av_products(m, a, i):
+            h0 = m * MBR + a * R
+            t_q = pvp.tile([P, 3, R, P], F32, name="pv")
+            pv[(m, a, i)] = t_q
+            eng = nc.vector if in_psum(m, i) else nc.gpsimd
+            lo = max(0, 1 - i - h0)
+            hi = min(R, H + 1 - i - h0)
+            for off, slot, cnt in ring_runs(h0 + lo + i - 1, hi - lo, RV):
+                b = lo + off
+                x0 = (a * R + b) * NG
+                eng.tensor_tensor(
+                    out=t_q[:, :, b:b + cnt, :].rearrange("p j r (g c) -> p j (r g) c", c=CG),
+                    in0=v_ring[:, slot:slot + cnt, :].rearrange("p r (g c) -> p (r g) c", c=CG).unsqueeze(1).to_broadcast([P, 3, cnt * NG, CG]),
+                    in1=sh[(m, i)][:, :, x0:x0 + cnt * NG].unsqueeze(3).to_broadcast([P, 3, cnt * NG, CG]),
+                    op=ALU.mult)
+
+        awork = {"todo": [], "pos": 0, "tile": None}
+
+        def av_begin(m, a):
+            h0 = m * MBR + a * R
+            t_o = psum.tile([P, R, W], F32, name="o_ps", tag="ops")
+            pending = []
+            for r in range(R):
+                terms = [(i, j) for i in range(3) for j in range(3) if 0 <= h0 + r + i - 1 < H]
+                for idx, (i, j) in enumerate(terms):
+                    pending.append((t_o[:, r, :], pv[(m, a, i)][:, j, r, :], perms[j], idx == 0, idx == len(terms) - 1))
+            awork["todo"] = pending
+            awork["pos"] = 0
+            awork["tile"] = t_o
+
+        def av_end(m, a):
+            h0 = m * MBR + a * R
+            work_step(awork, len(awork["todo"]))
             t_sb = outp.tile([P, PIX], F32, name="o_sb")
-            nc.scalar.copy(out=t_sb[:], in_=t_o[:].rearrange("p r w -> p (r w)"))
+            nc.scalar.copy(out=t_sb[:], in_=awork["tile"][:].rearrange("p r w -> p (r w)"))
             nc.sync.dma_start(out=o0[:, h0 * W:(h0 + R) * W], in_=t_sb[:])
 
-        t_sbs = {}
-
-        def attn_out(m, part):
-            if part == 0:
-                t_new = outp.tile([P, W, WIN], F32, name="t_sb")
-                t_sbs[m] = t_new
-            t_t = t_sbs[m]
-            n0, nn = NGROUPS[part]
-            t_ps = psum.tile([P, 4, W], F32, name="t_ps", tag="tps")
-            for n in range(nn):
-                nc.tensor.transpose(t_ps[:, n, :], a16[m][:, 3 * ((n0 + n) % 3) + (n0 + n) // 3, :, :].rearrange("p g h -> p (g h)"), ident_f[:])
-            nc.scalar.copy(out=t_t[:, :, n0:n0 + nn], in_=t_ps[:, 0:nn, :].rearrange("p n w -> p w n"))
-            if part == len(NGROUPS) - 1:
-                for g in range(NG):
-                    nc.sync.dma_start(out=o1[g, m * MAC:(m + 1) * MAC, :],
-                                      in_=t_t[g * MAC:(g + 1) * MAC, :, :].rearrange("p w n -> p (w n)"))
-
-        def run(stage, b):
-            if 0 <= b < NB:
-                stage(b)
+        def due(u, base, period, count):
+            idx, rem = divmod(u - base, period)
+            return idx if rem == 0 and 0 <= idx < count else None
 
         with tc.manual_schedule():
-            for t in range(-4, NB + 8):
-                run(mx_kv, t + 2)
-                run(mx_q, t + 1)
-                run(shift_end, t - 3)
-                t_o = av_sum_begin(t - 4) if 0 <= t - 4 < NB else None
-                run(qk_whole, t - 1)
-                av_sum_step(max(0, LEAD - 4 * WHOLE * BESIDE) if t < NB else 0)
-                run(qk_products, t)
-                run(qk_sums, t - 1)
-                av_sum_step(len(work["todo"]))
-                run(softmax_sum, t - 2)
-                av_products(t - 3, 0)
-                run(softmax_rec, t - 2)
-                av_products(t - 3, 1)
-                run(kv_out, t + 2)
-                run(regroup, t + 4)
-                if t_o is not None:
-                    av_sum_end(t - 4, t_o)
-                mm, part = divmod(t - 6, MAC // R)
-                if 0 <= mm < H // MAC and part < len(NGROUPS):
-                    attn_out(mm, part)
-                run(qk_rest, t)
-                run(quant, t + 3)
-                run(softmax_mul, t - 2)
-                run(shift_begin, t - 2)
-                av_products(t - 3, 2)
-                run(softmax_max, t - 1)
-                run(softmax_sub, t - 1)
-                run(collect, t - 2)
-                run(shift_mid, t - 2)
-                run(softmax_exp, t - 1)
+            for u in range(-18, (NMB - 1) * SUB + LAG + SUB + 3):
+                q = due(u, -12, 3, NQ)
+                if q is not None:
+                    mx_qk(q)
+                q = due(u, -11, 3, NQ)
+                if q is not None:
+                    mx_v(q)
+                q = due(u, -7, 3, NQ)
+                if q is not None:
+                    q_rel(q)
+                m = due(u, 20, SUB, NMB)
+                if m is not None:
+                    shift(m, 0)
+                m = due(u, 21, SUB, NMB)
+                if m is not None and not in_psum(m, 2):
+                    shift(m, 2)
+                m = due(u, LAG - 1, SUB, NMB)
+                if m is not None:
+                    shift(m, 1)
+                m = due(u, LAG, SUB, NMB)
+                if m is not None and in_psum(m, 2):
+                    shift(m, 2)
+                k = due(u, LAG + 3, 3, NQ)
+                if k is not None:
+                    av_begin(k // QPM, k % QPM)
+                work_step(awork, ASTEP)
+                k = due(u, LAG + 5, 3, NQ)
+                if k is not None:
+                    av_end(k // QPM, k % QPM)
+                if 0 <= u + 1 < NMB * SUB:
+                    q_shift(u + 1)
+                f = due(u, 4, QPM, 3 * NMB)
+                if f is not None:
+                    e_begin(f)
+                work_step(ework, ESTEP)
+                f = due(u, 7, QPM, 3 * NMB)
+                if f is not None:
+                    e_end(f)
+                if 0 <= u < NMB * SUB:
+                    qk_products(u)
+                if 0 <= u - LAG < NMB * SUB:
+                    k, i = divmod(u - LAG, 3)
+                    av_products(k // QPM, k % QPM, i)
+                q = due(u, -18, 3, NQ)
+                if q is not None:
+                    regroup(q)
+                q = due(u, -15, 3, NQ)
+                if q is not None:
+                    quant(q)
+                m = due(u, 16, SUB, NMB)
+                if m is not None:
+                    softmax_max(m)
+                m = due(u, 17, SUB, NMB)
+                if m is not None:
+                    softmax_sub(m)
+                m = due(u, 18, SUB, NMB)
+                if m is not None:
+                    softmax_sum(m)
+                m = due(u, 19, SUB, NMB)
+                if m is not None:
+                    softmax_mul(m)

@@ -63,6 +63,7 @@ def tile_mutliheadattention2d_kernel(tc, x, Wq, Wk, Wv, rel_t, rel_f, out_0, out
         outp = ctx.enter_context(tc.tile_pool(name="outp", bufs=2))
         attp = ctx.enter_context(tc.tile_pool(name="attp", bufs=1))
         smallp = ctx.enter_context(tc.tile_pool(name="smallp", bufs=2))
+        halfp = ctx.enter_context(tc.tile_pool(name="halfp", bufs=3))
         psum = ctx.enter_context(tc.psum_pool(name="psum", bufs=1))
 
         xv = x.rearrange("b (p j) h w -> p (b j) (h w)", j=4)
@@ -114,6 +115,8 @@ def tile_mutliheadattention2d_kernel(tc, x, Wq, Wk, Wv, rel_t, rel_f, out_0, out
         rmat = const.tile([P, WIN, NG], F32, name="rmat")
         nc.vector.tensor_tensor(out=rmat[:], in0=r9p[:].unsqueeze(2).to_broadcast([P, WIN, NG]),
                                 in1=gmask[:].unsqueeze(1).to_broadcast([P, WIN, NG]), op=ALU.mult)
+        rmat_b = const.tile([P, WIN * NG], BF16, name="rmat_b")
+        nc.vector.tensor_copy(out=rmat_b[:], in_=rmat[:].rearrange("p n g -> p (n g)"))
         atts = []
         for idx in range(2):
             t_att = const.tile([P, WIN, W + 2], F32, name="att%d" % idx)
@@ -149,7 +152,8 @@ def tile_mutliheadattention2d_kernel(tc, x, Wq, Wk, Wv, rel_t, rel_f, out_0, out
         grp = {}
         xc = {}
         xs = {}
-        mxt = {}
+        q_hi = {}
+        q_lo = {}
         qr9 = {}
         qjt = {}
         prod = {}
@@ -194,6 +198,12 @@ def tile_mutliheadattention2d_kernel(tc, x, Wq, Wk, Wv, rel_t, rel_f, out_0, out
             k_ps = mx_pixel(q, 1, "k_ps")
             qs = (q * R) % RQ
             nc.scalar.copy(out=q_ring[:, qs:qs + R, 1:W + 1], in_=q_ps[:])
+            t_hi = halfp.tile([P, R, W], BF16, name="q_hi")
+            nc.scalar.copy(out=t_hi[:], in_=q_ps[:])
+            t_lo = halfp.tile([P, R, W], BF16, name="q_lo")
+            nc.gpsimd.tensor_tensor(out=t_lo[:], in0=q_ring[:, qs:qs + R, 1:W + 1], in1=t_hi[:], op=ALU.subtract)
+            q_hi[q] = t_hi
+            q_lo[q] = t_lo
             ks = (q * R) % RK
             nc.scalar.copy(out=k_ring[:, ks:ks + R, :], in_=k_ps[:])
 
@@ -204,11 +214,10 @@ def tile_mutliheadattention2d_kernel(tc, x, Wq, Wk, Wv, rel_t, rel_f, out_0, out
 
         def q_rel(q):
             m, a = divmod(q, QPM)
-            qs = (q * R) % RQ
             t_ps = psum.tile([P, R, WIN * NG], F32, name="qr_ps", tag="aux")
             for r in range(R):
-                nc.tensor.matmul(out=t_ps[:, r, :], lhsT=q_ring[:, qs + r, 1:W + 1],
-                                 rhs=rmat[:].rearrange("p n g -> p (n g)"), start=True, stop=True)
+                nc.tensor.matmul(out=t_ps[:, r, :], lhsT=q_hi[q][:, r, :], rhs=rmat_b[:], start=True, stop=False)
+                nc.tensor.matmul(out=t_ps[:, r, :], lhsT=q_lo[q][:, r, :], rhs=rmat_b[:], start=False, stop=True)
             if a == 0:
                 t_new = qrp.tile([P, WIN, P], F32, name="qr9")
                 qr9[m] = t_new

@@ -33,6 +33,57 @@ LAG = 24
 ESTEP = 13
 ASTEP = 12
 TAIL_MB = 6
+QJ_BUFS = 2
+MX_BUFS = 3
+AUX_TAG = "mx"
+LOAD_ON_SCALAR = False
+SM_ON_G = False
+G_PIECES = 1
+RG_PIECES = ((0, 4),)
+
+OFF = {
+    "pe_mxq": (-12, 3, 32),
+    "pe_mxk": (-12, 3, 32),
+    "s_q": (-12, 3, 32),
+    "g_qlo": (-11, 3, 32),
+    "s_k": (-12, 3, 32),
+    "pe_mxv": (-11, 3, 32),
+    "s_v": (-11, 3, 32),
+    "pe_qrel": (-7, 3, 32),
+    "s_qr": (-7, 3, 32),
+    "pe_sh0": (21, 12, 8),
+    "s_sh0": (21, 12, 8),
+    "pe_sh2": (22, 12, 8),
+    "s_sh2": (22, 12, 8),
+    "pe_sh1": (23, 12, 8),
+    "pe_sh2t": (24, 12, 8),
+    "pe_abegin": (27, 3, 32),
+    "pe_asteps": (27, 1, 96),
+    "pe_aend": (29, 3, 32),
+    "s_osb": (29, 3, 32),
+    "pe_qshift": (-1, 1, 96),
+    "pe_ebegin": (4, 4, 24),
+    "pe_esteps": (4, 1, 96),
+    "pe_eend": (7, 4, 24),
+    "s_esb": (7, 4, 24),
+    "v_qk": (0, 1, 96),
+    "av": (24, 1, 96),
+    "s_rg0": (-18, 3, 32),
+    "v_quant": (-15, 3, 32),
+    "v_max": (16, 12, 8),
+    "v_sub": (17, 12, 8),
+    "s_exp": (18, 12, 8),
+    "v_sum": (19, 12, 8),
+    "v_mul": (20, 12, 8),
+    "s_tout": (21, 12, 8),
+}
+ORDER = (
+    "pe_qshift", "pe_mxq", "pe_mxk", "s_q", "g_qlo", "s_k", "pe_mxv", "s_v",
+    "pe_qrel", "s_qr", "pe_sh0", "s_sh0", "pe_sh2", "s_sh2", "pe_sh1", "pe_sh2t",
+    "pe_abegin", "pe_asteps", "pe_aend", "s_osb", "pe_ebegin", "pe_esteps", "pe_eend", "s_esb",
+    "v_qk", "av", "s_rg0", "s_rg1", "s_rg2", "s_rg3", "v_quant", "v_max",
+    "v_sub", "s_exp", "v_sum", "v_mul", "s_tout",
+)
 
 FLOPS = 2 * 3 * 128 * 512 * H * W + 2 * 2 * WIN * 128 * H * W
 
@@ -72,9 +123,10 @@ def tile_mutliheadattention2d_kernel(tc, x, Wq, Wk, Wv, rel_t, rel_f, out_0, out
 
         raw = {}
 
-        def load(q):
+        def load(q, late=False):
             t_raw = rawp.tile([P, 4, PIX], BF16, name="raw")
-            nc.sync.dma_start(out=t_raw[:], in_=xv[:, :, q * PIX:(q + 1) * PIX])
+            queue = nc.scalar if (late and LOAD_ON_SCALAR) else nc.sync
+            queue.dma_start(out=t_raw[:], in_=xv[:, :, q * PIX:(q + 1) * PIX])
             raw[q] = t_raw
 
         w_raw = pp.tile([P, 3, 512], BF16, name="w_raw", tag="big", align_bytes=64)
@@ -108,7 +160,7 @@ def tile_mutliheadattention2d_kernel(tc, x, Wq, Wk, Wv, rel_t, rel_f, out_0, out
                               in_=rel_sb[0:64, :].unsqueeze(2).to_broadcast([64, 3, 3]))
         nc.vector.tensor_copy(out=r9[64:128, :].rearrange("p (i j) -> p i j", j=3),
                               in_=rel_sb[64:128, :].unsqueeze(1).to_broadcast([64, 3, 3]))
-        r9_ps = psum.tile([P, WIN], F32, name="r9_ps", tag="aux")
+        r9_ps = psum.tile([P, WIN], F32, name="r9_ps", tag="mx", bufs=MX_BUFS) if AUX_TAG == "mx" else psum.tile([P, WIN], F32, name="r9_ps", tag="aux")
         nc.tensor.matmul(out=r9_ps[:], lhsT=chperm[:], rhs=r9[:], start=True, stop=True)
         r9p = const.tile([P, WIN], F32, name="r9p")
         nc.vector.tensor_copy(out=r9p[:], in_=r9_ps[:])
@@ -134,7 +186,7 @@ def tile_mutliheadattention2d_kernel(tc, x, Wq, Wk, Wv, rel_t, rel_f, out_0, out
         w_scales = []
         for idx in range(3):
             nc.scalar.copy(out=w_de[:, idx, :, :], in_=w_raw[:, idx, :].rearrange("o (p t) -> o t p", t=4))
-            w_ps = psum.tile([P, 4, P], BF16, name="w_ps", tag="mx", bufs=2)
+            w_ps = psum.tile([P, 4, P], BF16, name="w_ps", tag="mx", bufs=MX_BUFS)
             for t in range(4):
                 nc.tensor.transpose(w_ps[:, t, :], w_de[:, idx, t, :], ident_b[:])
             if idx < 2:
@@ -163,19 +215,21 @@ def tile_mutliheadattention2d_kernel(tc, x, Wq, Wk, Wv, rel_t, rel_f, out_0, out
         sh = {}
         pv = {}
 
-        def regroup(q):
-            t_g = grpp.tile([P, PIX, 4], BF16, name="grp", align_bytes=64)
-            if q in (1, 3):
-                nc.vector.tensor_copy(out=t_g[:].rearrange("p (c i) t -> p c t i", i=4),
-                                      in_=raw[q][:].rearrange("p t (c i) -> p c t i", i=4))
-            else:
-                nc.scalar.copy(out=t_g[:].rearrange("p (c i) t -> p c t i", i=4),
-                               in_=raw[q][:].rearrange("p t (c i) -> p c t i", i=4))
-            grp[q] = t_g
-            if q + RAW_BUFS < NQ:
-                load(q + RAW_BUFS)
+        ps = {}
 
-        def quant(q):
+        def s_rg(q, piece):
+            first, count = RG_PIECES[piece]
+            if first == 0:
+                t_new = grpp.tile([P, PIX, 4], BF16, name="grp", align_bytes=64)
+                grp[q] = t_new
+            cols = slice(first * W, (first + count) * W)
+            eng_copy = nc.vector.tensor_copy if q in (1, 3) else nc.scalar.copy
+            eng_copy(out=grp[q][:, cols, :].rearrange("p (c i) t -> p c t i", i=4),
+                     in_=raw[q][:, :, cols].rearrange("p t (c i) -> p c t i", i=4))
+            if first + count == R and q + RAW_BUFS < NQ:
+                load(q + RAW_BUFS, True)
+
+        def v_quant(q):
             t_c = codp.tile([P, PIX], U32, name="xc", align_bytes=64)
             t_s = codp.tile([P, PIX], U8, name="xs", align_bytes=64)
             nc.vector.quantize_mx(out=t_c[:].bitcast(FP8X4), scales=t_s[:], in_=grp[q][:].rearrange("p c t -> p (c t)"))
@@ -183,61 +237,81 @@ def tile_mutliheadattention2d_kernel(tc, x, Wq, Wk, Wv, rel_t, rel_f, out_0, out
             xs[q] = t_s
 
         def mx_pixel(q, widx, name):
-            t_ps = psum.tile([P, R, P], F32, name=name, tag="mx", bufs=2)
+            t_ps = psum.tile([P, R, P], F32, name=name, tag="mx", bufs=MX_BUFS)
             for r in range(R):
                 cols = slice(r * W, (r + 1) * W)
                 nc.tensor.matmul_mx(out=t_ps[:, r, :], lhsT=xc[q][:, cols].bitcast(FP8X4), lhsT_scale=xs[q][:, cols],
                                     rhs=w_codes[widx][:].bitcast(FP8X4), rhs_scale=w_scales[widx][:], start=True, stop=True)
             return t_ps
 
-        def mx_qk(q):
-            q_ps = psum.tile([P, R, W], F32, name="q_ps", tag="mx", bufs=2)
+        def pe_mxq(q):
+            q_ps = psum.tile([P, R, W], F32, name="q_ps", tag="mx", bufs=MX_BUFS)
             nc.tensor.matmul_mx(out=q_ps[:].rearrange("p r w -> p (r w)"), lhsT=w_codes[0][:].bitcast(FP8X4),
                                 lhsT_scale=w_scales[0][:], rhs=xc[q][:].bitcast(FP8X4), rhs_scale=xs[q][:],
                                 start=True, stop=True)
-            k_ps = mx_pixel(q, 1, "k_ps")
+            ps[("q", q)] = q_ps
+
+        def pe_mxk(q):
+            ps[("k", q)] = mx_pixel(q, 1, "k_ps")
+
+        def pe_mxv(q):
+            ps[("v", q)] = mx_pixel(q, 2, "v_ps")
+
+        def s_q(q):
             qs = (q * R) % RQ
-            nc.scalar.copy(out=q_ring[:, qs:qs + R, 1:W + 1], in_=q_ps[:])
+            nc.scalar.copy(out=q_ring[:, qs:qs + R, 1:W + 1], in_=ps[("q", q)][:])
             t_hi = halfp.tile([P, R, W], BF16, name="q_hi")
-            nc.scalar.copy(out=t_hi[:], in_=q_ps[:])
-            t_lo = halfp.tile([P, R, W], BF16, name="q_lo")
-            nc.gpsimd.tensor_tensor(out=t_lo[:], in0=q_ring[:, qs:qs + R, 1:W + 1], in1=t_hi[:], op=ALU.subtract)
+            nc.scalar.copy(out=t_hi[:], in_=ps[("q", q)][:])
             q_hi[q] = t_hi
+
+        def g_qlo(q):
+            qs = (q * R) % RQ
+            t_lo = halfp.tile([P, R, W], BF16, name="q_lo")
+            nc.gpsimd.tensor_tensor(out=t_lo[:], in0=q_ring[:, qs:qs + R, 1:W + 1], in1=q_hi[q][:], op=ALU.subtract)
             q_lo[q] = t_lo
+
+        def s_k(q):
             ks = (q * R) % RK
-            nc.scalar.copy(out=k_ring[:, ks:ks + R, :], in_=k_ps[:])
+            nc.scalar.copy(out=k_ring[:, ks:ks + R, :], in_=ps[("k", q)][:])
 
-        def mx_v(q):
-            v_ps = mx_pixel(q, 2, "v_ps")
+        def s_v(q):
             vs = (q * R) % RV
-            nc.scalar.copy(out=v_ring[:, vs:vs + R, :], in_=v_ps[:])
+            nc.scalar.copy(out=v_ring[:, vs:vs + R, :], in_=ps[("v", q)][:])
 
-        def q_rel(q):
-            m, a = divmod(q, QPM)
-            t_ps = psum.tile([P, R, WIN * NG], F32, name="qr_ps", tag="aux")
+        def aux_tile(shape, name):
+            if AUX_TAG == "mx":
+                return psum.tile(shape, F32, name=name, tag="mx", bufs=MX_BUFS)
+            return psum.tile(shape, F32, name=name, tag="aux")
+
+        def pe_qrel(q):
+            t_ps = aux_tile([P, R, WIN * NG], "qr_ps")
             for r in range(R):
                 nc.tensor.matmul(out=t_ps[:, r, :], lhsT=q_hi[q][:, r, :], rhs=rmat_b[:], start=True, stop=False)
                 nc.tensor.matmul(out=t_ps[:, r, :], lhsT=q_lo[q][:, r, :], rhs=rmat_b[:], start=False, stop=True)
+            ps[("qr", q)] = t_ps
+
+        def s_qr(q):
+            m, a = divmod(q, QPM)
             if a == 0:
                 t_new = qrp.tile([P, WIN, P], F32, name="qr9")
                 qr9[m] = t_new
             nc.scalar.copy(out=qr9[m][:, :, a * R * NG:(a + 1) * R * NG].rearrange("p n (r g) -> p n r g", g=NG),
-                           in_=t_ps[:].rearrange("p r (n g) -> p n r g", g=NG))
+                           in_=ps[("qr", q)][:].rearrange("p r (n g) -> p n r g", g=NG))
 
         def decode(u):
             m, rem = divmod(u, SUB)
             j, a = divmod(rem, QPM)
             return m, j, a
 
-        def q_shift(u):
+        def pe_qshift(u):
             m, j, a = decode(u)
             qs = ((m * QPM + a) * R) % RQ
-            t_ps = psum.tile([P, R, P], F32, name="qj", tag="qj", bufs=2)
+            t_ps = psum.tile([P, R, P], F32, name="qj", tag="qj", bufs=QJ_BUFS)
             for r in range(R):
                 nc.tensor.transpose(t_ps[:, r, :], q_ring[:, qs + r, 2 - j:2 - j + W], ident_f[:])
             qjt[u] = t_ps
 
-        def qk_products(u):
+        def v_qk(u):
             m, j, a = decode(u)
             h0 = m * MBR + a * R
             if u == (NMB - 1) * SUB:
@@ -257,7 +331,7 @@ def tile_mutliheadattention2d_kernel(tc, x, Wq, Wk, Wv, rel_t, rel_f, out_0, out
 
         ework = {"todo": [], "pos": 0, "tile": None}
 
-        def e_begin(f):
+        def pe_ebegin(f):
             m, j = divmod(f, 3)
             t_e = psum.tile([P, 3, W], F32, name="e_ps", tag="eps")
             pending = []
@@ -268,7 +342,7 @@ def tile_mutliheadattention2d_kernel(tc, x, Wq, Wk, Wv, rel_t, rel_f, out_0, out
                 pending.append((t_e[:, i, :], qr9[m][:, n, :], ident_f, False, True))
             ework["todo"] = pending
             ework["pos"] = 0
-            ework["tile"] = t_e
+            ps[("e", f)] = t_e
 
         def work_step(work, count):
             todo = work["todo"]
@@ -277,77 +351,94 @@ def tile_mutliheadattention2d_kernel(tc, x, Wq, Wk, Wv, rel_t, rel_f, out_0, out
                 nc.tensor.matmul(out=dst, lhsT=lhs, rhs=perm[:], start=first, stop=last, is_transpose=True)
             work["pos"] = min(work["pos"] + count, len(todo))
 
-        def e_end(f):
-            m, j = divmod(f, 3)
+        def pe_esteps(idx):
+            work_step(ework, ESTEP)
+
+        def pe_eend(f):
             work_step(ework, len(ework["todo"]))
+
+        def s_esb(f):
+            m, j = divmod(f, 3)
             if j == 0:
                 t_new = esp.tile([P, 3, 3, W], F32, name="esb")
                 esb[m] = t_new
-            nc.scalar.copy(out=esb[m][:, :, j, :], in_=ework["tile"][:])
+            nc.scalar.copy(out=esb[m][:, :, j, :], in_=ps[("e", f)][:])
 
-        def softmax_max(m):
+        def v_max(m):
             t_m = smallp.tile([P, W], F32, name="mx")
             nc.vector.tensor_reduce(out=t_m[:], in_=esb[m][:].rearrange("p i j w -> p w (i j)"), axis=AX.X, op=ALU.max)
             tops[m] = t_m
 
-        def softmax_sub(m):
+        sm_eng = nc.gpsimd if SM_ON_G else nc.vector
+
+        def v_sub(m):
             flat = esb[m][:].rearrange("p i j w -> p (i j) w")
-            nc.vector.tensor_tensor(out=flat, in0=flat, in1=tops[m][:].unsqueeze(1).to_broadcast([P, WIN, W]), op=ALU.subtract)
+            sm_eng.tensor_tensor(out=flat, in0=flat, in1=tops[m][:].unsqueeze(1).to_broadcast([P, WIN, W]), op=ALU.subtract)
+
+        def s_exp(m):
+            flat = esb[m][:].rearrange("p i j w -> p (i j) w")
             nc.scalar.activation(out=flat, in_=flat, func=ACT.Exp)
 
-        def softmax_sum(m):
+        def v_sum(m):
             t_s = smallp.tile([P, W], F32, name="ssum")
             nc.vector.tensor_reduce(out=t_s[:], in_=esb[m][:].rearrange("p i j w -> p w (i j)"), axis=AX.X, op=ALU.add)
             t_r = smallp.tile([P, W], F32, name="rsum")
             nc.vector.reciprocal(out=t_r[:], in_=t_s[:])
             sums[m] = t_r
 
-        def softmax_mul(m):
-            t_a = atts[m % 2]
-            nc.vector.tensor_tensor(out=t_a[:, :, 1:W + 1], in0=esb[m][:].rearrange("p i j w -> p (i j) w"),
-                                    in1=sums[m][:].unsqueeze(1).to_broadcast([P, WIN, W]), op=ALU.mult)
+        def v_mul(m):
+            sm_eng.tensor_tensor(out=atts[m % 2][:, :, 1:W + 1], in0=esb[m][:].rearrange("p i j w -> p (i j) w"),
+                                 in1=sums[m][:].unsqueeze(1).to_broadcast([P, WIN, W]), op=ALU.mult)
+
+        def s_tout(m):
             t_t = attp.tile([P, W, WIN], F32, name="t_out")
-            nc.scalar.copy(out=t_t[:], in_=t_a[:, :, 1:W + 1].rearrange("p n w -> p w n"))
+            nc.scalar.copy(out=t_t[:], in_=atts[m % 2][:, :, 1:W + 1].rearrange("p n w -> p w n"))
             for r in range(MBR):
                 nc.sync.dma_start(out=o1[:, m * MBR + r, :], in_=t_t[r * NG:(r + 1) * NG, :, :].rearrange("p w n -> p (w n)"))
 
         def in_psum(m, i):
             return i == 1 or (m >= TAIL_MB and i == 2)
 
-        def shift(m, i):
-            tag = "shv" if i == 1 else ("qj" if in_psum(m, i) else "aux")
-            if tag == "qj":
-                t_ps = psum.tile([P, 3, P], F32, name="sh_ps", tag="qj", bufs=2)
+        def pe_shift(m, i):
+            if i == 1:
+                t_ps = psum.tile([P, 3, P], F32, name="sh_ps", tag="shv")
+            elif in_psum(m, i):
+                t_ps = psum.tile([P, 3, P], F32, name="sh_ps", tag="qj", bufs=QJ_BUFS)
             else:
-                t_ps = psum.tile([P, 3, P], F32, name="sh_ps", tag=tag)
+                t_ps = aux_tile([P, 3, P], "sh_ps")
             for j in range(3):
                 nc.tensor.transpose(t_ps[:, j, :], atts[m % 2][:, 3 * i + j, 2 - j:2 - j + W], ident_f[:])
-            if in_psum(m, i):
-                sh[(m, i)] = t_ps
-            else:
-                t_sb = shp.tile([P, 3, P], F32, name="sh_sb")
-                nc.scalar.copy(out=t_sb[:], in_=t_ps[:])
-                sh[(m, i)] = t_sb
+            sh[(m, i)] = t_ps
 
-        def av_products(m, a, i):
+        def s_shift(m, i):
+            t_sb = shp.tile([P, 3, P], F32, name="sh_sb")
+            nc.scalar.copy(out=t_sb[:], in_=sh[(m, i)][:])
+            sh[(m, i)] = t_sb
+
+        def av(idx):
+            k, i = divmod(idx, 3)
+            m, a = divmod(k, QPM)
             h0 = m * MBR + a * R
             t_q = pvp.tile([P, 3, R, P], F32, name="pv")
             pv[(m, a, i)] = t_q
             eng = nc.vector if in_psum(m, i) else nc.gpsimd
+            nj = 3 if in_psum(m, i) else 3 // G_PIECES
             lo = max(0, 1 - i - h0)
             hi = min(R, H + 1 - i - h0)
             for off, slot, cnt in ring_runs(h0 + lo + i - 1, hi - lo, RV):
                 b = lo + off
                 x0 = (a * R + b) * NG
-                eng.tensor_tensor(
-                    out=t_q[:, :, b:b + cnt, :].rearrange("p j r (g c) -> p j (r g) c", c=CG),
-                    in0=v_ring[:, slot:slot + cnt, :].rearrange("p r (g c) -> p (r g) c", c=CG).unsqueeze(1).to_broadcast([P, 3, cnt * NG, CG]),
-                    in1=sh[(m, i)][:, :, x0:x0 + cnt * NG].unsqueeze(3).to_broadcast([P, 3, cnt * NG, CG]),
-                    op=ALU.mult)
+                for j0 in range(0, 3, nj):
+                    eng.tensor_tensor(
+                        out=t_q[:, j0:j0 + nj, b:b + cnt, :].rearrange("p j r (g c) -> p j (r g) c", c=CG),
+                        in0=v_ring[:, slot:slot + cnt, :].rearrange("p r (g c) -> p (r g) c", c=CG).unsqueeze(1).to_broadcast([P, nj, cnt * NG, CG]),
+                        in1=sh[(m, i)][:, j0:j0 + nj, x0:x0 + cnt * NG].unsqueeze(3).to_broadcast([P, nj, cnt * NG, CG]),
+                        op=ALU.mult)
 
         awork = {"todo": [], "pos": 0, "tile": None}
 
-        def av_begin(m, a):
+        def pe_abegin(k):
+            m, a = divmod(k, QPM)
             h0 = m * MBR + a * R
             t_o = psum.tile([P, R, W], F32, name="o_ps", tag="ops")
             pending = []
@@ -357,78 +448,42 @@ def tile_mutliheadattention2d_kernel(tc, x, Wq, Wk, Wv, rel_t, rel_f, out_0, out
                     pending.append((t_o[:, r, :], pv[(m, a, i)][:, j, r, :], perms[j], idx == 0, idx == len(terms) - 1))
             awork["todo"] = pending
             awork["pos"] = 0
-            awork["tile"] = t_o
+            ps[("o", k)] = t_o
 
-        def av_end(m, a):
-            h0 = m * MBR + a * R
+        def pe_asteps(idx):
+            work_step(awork, ASTEP)
+
+        def pe_aend(k):
             work_step(awork, len(awork["todo"]))
+
+        def s_osb(k):
             t_sb = outp.tile([P, PIX], F32, name="o_sb")
-            nc.scalar.copy(out=t_sb[:], in_=awork["tile"][:].rearrange("p r w -> p (r w)"))
-            nc.sync.dma_start(out=o0[:, h0 * W:(h0 + R) * W], in_=t_sb[:])
+            nc.scalar.copy(out=t_sb[:], in_=ps[("o", k)][:].rearrange("p r w -> p (r w)"))
+            nc.sync.dma_start(out=o0[:, k * PIX:(k + 1) * PIX], in_=t_sb[:])
 
-        def due(u, base, period, count):
-            idx, rem = divmod(u - base, period)
-            return idx if rem == 0 and 0 <= idx < count else None
+        def only(cond, fn):
+            return lambda m: fn(m) if cond(m) else None
 
+        calls = {
+            "pe_mxq": pe_mxq, "pe_mxk": pe_mxk, "pe_mxv": pe_mxv, "s_q": s_q, "g_qlo": g_qlo, "s_k": s_k, "s_v": s_v,
+            "pe_qrel": pe_qrel, "s_qr": s_qr,
+            "pe_sh0": lambda m: pe_shift(m, 0), "s_sh0": lambda m: s_shift(m, 0),
+            "pe_sh2": only(lambda m: not in_psum(m, 2), lambda m: pe_shift(m, 2)),
+            "s_sh2": only(lambda m: not in_psum(m, 2), lambda m: s_shift(m, 2)),
+            "pe_sh1": lambda m: pe_shift(m, 1), "pe_sh2t": only(lambda m: in_psum(m, 2), lambda m: pe_shift(m, 2)),
+            "pe_abegin": pe_abegin, "pe_asteps": pe_asteps, "pe_aend": pe_aend, "s_osb": s_osb,
+            "pe_qshift": pe_qshift, "pe_ebegin": pe_ebegin, "pe_esteps": pe_esteps, "pe_eend": pe_eend, "s_esb": s_esb,
+            "v_qk": v_qk, "av": av, "v_quant": v_quant,
+            "s_rg0": lambda q: s_rg(q, 0), "s_rg1": lambda q: s_rg(q, 1), "s_rg2": lambda q: s_rg(q, 2), "s_rg3": lambda q: s_rg(q, 3),
+            "v_max": v_max, "v_sub": v_sub, "s_exp": s_exp, "v_sum": v_sum, "v_mul": v_mul, "s_tout": s_tout,
+        }
+        first_u = min([OFF[name][0] for name in ORDER if name in OFF])
+        last_u = max([OFF[name][0] + OFF[name][1] * (OFF[name][2] - 1) for name in ORDER if name in OFF])
         with tc.manual_schedule():
-            for u in range(-18, (NMB - 1) * SUB + LAG + SUB + 3):
-                q = due(u, -12, 3, NQ)
-                if q is not None:
-                    mx_qk(q)
-                q = due(u, -11, 3, NQ)
-                if q is not None:
-                    mx_v(q)
-                q = due(u, -7, 3, NQ)
-                if q is not None:
-                    q_rel(q)
-                m = due(u, 20, SUB, NMB)
-                if m is not None:
-                    shift(m, 0)
-                m = due(u, 21, SUB, NMB)
-                if m is not None and not in_psum(m, 2):
-                    shift(m, 2)
-                m = due(u, LAG - 1, SUB, NMB)
-                if m is not None:
-                    shift(m, 1)
-                m = due(u, LAG, SUB, NMB)
-                if m is not None and in_psum(m, 2):
-                    shift(m, 2)
-                k = due(u, LAG + 3, 3, NQ)
-                if k is not None:
-                    av_begin(k // QPM, k % QPM)
-                work_step(awork, ASTEP)
-                k = due(u, LAG + 5, 3, NQ)
-                if k is not None:
-                    av_end(k // QPM, k % QPM)
-                if 0 <= u + 1 < NMB * SUB:
-                    q_shift(u + 1)
-                f = due(u, 4, QPM, 3 * NMB)
-                if f is not None:
-                    e_begin(f)
-                work_step(ework, ESTEP)
-                f = due(u, 7, QPM, 3 * NMB)
-                if f is not None:
-                    e_end(f)
-                if 0 <= u < NMB * SUB:
-                    qk_products(u)
-                if 0 <= u - LAG < NMB * SUB:
-                    k, i = divmod(u - LAG, 3)
-                    av_products(k // QPM, k % QPM, i)
-                q = due(u, -18, 3, NQ)
-                if q is not None:
-                    regroup(q)
-                q = due(u, -15, 3, NQ)
-                if q is not None:
-                    quant(q)
-                m = due(u, 16, SUB, NMB)
-                if m is not None:
-                    softmax_max(m)
-                m = due(u, 17, SUB, NMB)
-                if m is not None:
-                    softmax_sub(m)
-                m = due(u, 18, SUB, NMB)
-                if m is not None:
-                    softmax_sum(m)
-                m = due(u, 19, SUB, NMB)
-                if m is not None:
-                    softmax_mul(m)
+            for u in range(first_u, last_u + 1):
+                for name in ORDER:
+                    if name in OFF:
+                        base, period, count = OFF[name]
+                        idx, rem = divmod(u - base, period)
+                        if rem == 0 and 0 <= idx < count:
+                            calls[name](idx)

@@ -37,9 +37,16 @@ QJ_BUFS = 2
 MX_BUFS = 3
 AUX_TAG = "mx"
 LOAD_ON_SCALAR = False
-SM_ON_G = False
+SM_ON_G = True
 G_PIECES = 1
 RG_PIECES = ((0, 4),)
+WARM_N = 1
+MX_PRE = 0
+V_SPLIT = False
+G_WHEN = (0, 1, 2)
+QN_PIECES = 1
+QR_F32 = False
+V_RG = (1, 3)
 
 OFF = {
     "pe_mxq": (-12, 3, 32),
@@ -223,21 +230,32 @@ def tile_mutliheadattention2d_kernel(tc, x, Wq, Wk, Wv, rel_t, rel_f, out_0, out
                 t_new = grpp.tile([P, PIX, 4], BF16, name="grp", align_bytes=64)
                 grp[q] = t_new
             cols = slice(first * W, (first + count) * W)
-            eng_copy = nc.vector.tensor_copy if q in (1, 3) else nc.scalar.copy
+            eng_copy = nc.vector.tensor_copy if q in V_RG else nc.scalar.copy
             eng_copy(out=grp[q][:, cols, :].rearrange("p (c i) t -> p c t i", i=4),
                      in_=raw[q][:, :, cols].rearrange("p t (c i) -> p c t i", i=4))
             if first + count == R and q + RAW_BUFS < NQ:
                 load(q + RAW_BUFS, True)
 
-        def v_quant(q):
-            t_c = codp.tile([P, PIX], U32, name="xc", align_bytes=64)
-            t_s = codp.tile([P, PIX], U8, name="xs", align_bytes=64)
-            nc.vector.quantize_mx(out=t_c[:].bitcast(FP8X4), scales=t_s[:], in_=grp[q][:].rearrange("p c t -> p (c t)"))
-            xc[q] = t_c
-            xs[q] = t_s
+        def v_quant(q, piece=0):
+            if piece == 0:
+                t_c = codp.tile([P, PIX], U32, name="xc", align_bytes=64)
+                t_s = codp.tile([P, PIX], U8, name="xs", align_bytes=64)
+                xc[q] = t_c
+                xs[q] = t_s
+            n = PIX // QN_PIECES
+            cols = slice(piece * n, (piece + 1) * n)
+            nc.vector.quantize_mx(out=xc[q][:, cols].bitcast(FP8X4), scales=xs[q][:, cols],
+                                  in_=grp[q][:, cols, :].rearrange("p c t -> p (c t)"))
+
+        def q_pass(q, t_ps):
+            nc.tensor.matmul_mx(out=t_ps[:].rearrange("p r w -> p (r w)"), lhsT=w_codes[0][:].bitcast(FP8X4),
+                                lhsT_scale=w_scales[0][:], rhs=xc[q][:].bitcast(FP8X4), rhs_scale=xs[q][:],
+                                start=True, stop=True)
 
         def mx_pixel(q, widx, name):
             t_ps = psum.tile([P, R, P], F32, name=name, tag="mx", bufs=MX_BUFS)
+            for rep in range(MX_PRE):
+                q_pass(q, t_ps)
             for r in range(R):
                 cols = slice(r * W, (r + 1) * W)
                 nc.tensor.matmul_mx(out=t_ps[:, r, :], lhsT=xc[q][:, cols].bitcast(FP8X4), lhsT_scale=xs[q][:, cols],
@@ -246,9 +264,8 @@ def tile_mutliheadattention2d_kernel(tc, x, Wq, Wk, Wv, rel_t, rel_f, out_0, out
 
         def pe_mxq(q):
             q_ps = psum.tile([P, R, W], F32, name="q_ps", tag="mx", bufs=MX_BUFS)
-            nc.tensor.matmul_mx(out=q_ps[:].rearrange("p r w -> p (r w)"), lhsT=w_codes[0][:].bitcast(FP8X4),
-                                lhsT_scale=w_scales[0][:], rhs=xc[q][:].bitcast(FP8X4), rhs_scale=xs[q][:],
-                                start=True, stop=True)
+            for rep in range(MX_PRE + 1):
+                q_pass(q, q_ps)
             ps[("q", q)] = q_ps
 
         def pe_mxk(q):
@@ -260,9 +277,10 @@ def tile_mutliheadattention2d_kernel(tc, x, Wq, Wk, Wv, rel_t, rel_f, out_0, out
         def s_q(q):
             qs = (q * R) % RQ
             nc.scalar.copy(out=q_ring[:, qs:qs + R, 1:W + 1], in_=ps[("q", q)][:])
-            t_hi = halfp.tile([P, R, W], BF16, name="q_hi")
-            nc.scalar.copy(out=t_hi[:], in_=ps[("q", q)][:])
-            q_hi[q] = t_hi
+            if not QR_F32:
+                t_hi = halfp.tile([P, R, W], BF16, name="q_hi")
+                nc.scalar.copy(out=t_hi[:], in_=ps[("q", q)][:])
+                q_hi[q] = t_hi
 
         def g_qlo(q):
             qs = (q * R) % RQ
@@ -285,9 +303,14 @@ def tile_mutliheadattention2d_kernel(tc, x, Wq, Wk, Wv, rel_t, rel_f, out_0, out
 
         def pe_qrel(q):
             t_ps = aux_tile([P, R, WIN * NG], "qr_ps")
+            qs = (q * R) % RQ
             for r in range(R):
-                nc.tensor.matmul(out=t_ps[:, r, :], lhsT=q_hi[q][:, r, :], rhs=rmat_b[:], start=True, stop=False)
-                nc.tensor.matmul(out=t_ps[:, r, :], lhsT=q_lo[q][:, r, :], rhs=rmat_b[:], start=False, stop=True)
+                if QR_F32:
+                    nc.tensor.matmul(out=t_ps[:, r, :], lhsT=q_ring[:, qs + r, 1:W + 1],
+                                     rhs=rmat[:].rearrange("p n g -> p (n g)"), start=True, stop=True)
+                else:
+                    nc.tensor.matmul(out=t_ps[:, r, :], lhsT=q_hi[q][:, r, :], rhs=rmat_b[:], start=True, stop=False)
+                    nc.tensor.matmul(out=t_ps[:, r, :], lhsT=q_lo[q][:, r, :], rhs=rmat_b[:], start=False, stop=True)
             ps[("qr", q)] = t_ps
 
         def s_qr(q):
@@ -415,25 +438,36 @@ def tile_mutliheadattention2d_kernel(tc, x, Wq, Wk, Wv, rel_t, rel_f, out_0, out
             nc.scalar.copy(out=t_sb[:], in_=sh[(m, i)][:])
             sh[(m, i)] = t_sb
 
-        def av(idx):
-            k, i = divmod(idx, 3)
-            m, a = divmod(k, QPM)
+        def av_piece(eng, m, a, i, j0, nj):
             h0 = m * MBR + a * R
-            t_q = pvp.tile([P, 3, R, P], F32, name="pv")
-            pv[(m, a, i)] = t_q
-            eng = nc.vector if in_psum(m, i) else nc.gpsimd
-            nj = 3 if in_psum(m, i) else 3 // G_PIECES
+            t_q = pv[(m, a, i)]
             lo = max(0, 1 - i - h0)
             hi = min(R, H + 1 - i - h0)
             for off, slot, cnt in ring_runs(h0 + lo + i - 1, hi - lo, RV):
                 b = lo + off
                 x0 = (a * R + b) * NG
-                for j0 in range(0, 3, nj):
-                    eng.tensor_tensor(
-                        out=t_q[:, j0:j0 + nj, b:b + cnt, :].rearrange("p j r (g c) -> p j (r g) c", c=CG),
-                        in0=v_ring[:, slot:slot + cnt, :].rearrange("p r (g c) -> p (r g) c", c=CG).unsqueeze(1).to_broadcast([P, nj, cnt * NG, CG]),
-                        in1=sh[(m, i)][:, j0:j0 + nj, x0:x0 + cnt * NG].unsqueeze(3).to_broadcast([P, nj, cnt * NG, CG]),
-                        op=ALU.mult)
+                eng.tensor_tensor(
+                    out=t_q[:, j0:j0 + nj, b:b + cnt, :].rearrange("p j r (g c) -> p j (r g) c", c=CG),
+                    in0=v_ring[:, slot:slot + cnt, :].rearrange("p r (g c) -> p (r g) c", c=CG).unsqueeze(1).to_broadcast([P, nj, cnt * NG, CG]),
+                    in1=sh[(m, i)][:, j0:j0 + nj, x0:x0 + cnt * NG].unsqueeze(3).to_broadcast([P, nj, cnt * NG, CG]),
+                    op=ALU.mult)
+
+        def av(idx):
+            k, s = divmod(idx, 3)
+            m, a = divmod(k, QPM)
+            if s == 0:
+                for i in range(3):
+                    t_new = pvp.tile([P, 3, R, P], F32, name="pv")
+                    pv[(m, a, i)] = t_new
+            for i in range(3):
+                if in_psum(m, i):
+                    if V_SPLIT:
+                        av_piece(nc.vector, m, a, i, s, 1)
+                    elif s == i:
+                        av_piece(nc.vector, m, a, i, 0, 3)
+                elif s == G_WHEN[i]:
+                    for j0 in range(0, 3, 3 // G_PIECES):
+                        av_piece(nc.gpsimd, m, a, i, j0, 3 // G_PIECES)
 
         awork = {"todo": [], "pos": 0, "tile": None}
 
@@ -461,6 +495,12 @@ def tile_mutliheadattention2d_kernel(tc, x, Wq, Wk, Wv, rel_t, rel_f, out_0, out
             nc.scalar.copy(out=t_sb[:], in_=ps[("o", k)][:].rearrange("p r w -> p (r w)"))
             nc.sync.dma_start(out=o0[:, k * PIX:(k + 1) * PIX], in_=t_sb[:])
 
+        def pe_warm(idx):
+            t_ps = psum.tile([P, PIX], F32, name="warm_ps", tag="mx", bufs=MX_BUFS)
+            for rep in range(WARM_N):
+                nc.tensor.matmul_mx(out=t_ps[:], lhsT=w_codes[0][:].bitcast(FP8X4), lhsT_scale=w_scales[0][:],
+                                    rhs=xc[NQ - 1][:].bitcast(FP8X4), rhs_scale=xs[NQ - 1][:], start=True, stop=True)
+
         def only(cond, fn):
             return lambda m: fn(m) if cond(m) else None
 
@@ -473,9 +513,9 @@ def tile_mutliheadattention2d_kernel(tc, x, Wq, Wk, Wv, rel_t, rel_f, out_0, out
             "pe_sh1": lambda m: pe_shift(m, 1), "pe_sh2t": only(lambda m: in_psum(m, 2), lambda m: pe_shift(m, 2)),
             "pe_abegin": pe_abegin, "pe_asteps": pe_asteps, "pe_aend": pe_aend, "s_osb": s_osb,
             "pe_qshift": pe_qshift, "pe_ebegin": pe_ebegin, "pe_esteps": pe_esteps, "pe_eend": pe_eend, "s_esb": s_esb,
-            "v_qk": v_qk, "av": av, "v_quant": v_quant,
+            "v_qk": v_qk, "av": av, "v_quant": v_quant, "v_quant1": lambda q: v_quant(q, 1),
             "s_rg0": lambda q: s_rg(q, 0), "s_rg1": lambda q: s_rg(q, 1), "s_rg2": lambda q: s_rg(q, 2), "s_rg3": lambda q: s_rg(q, 3),
-            "v_max": v_max, "v_sub": v_sub, "s_exp": s_exp, "v_sum": v_sum, "v_mul": v_mul, "s_tout": s_tout,
+            "pe_warm": pe_warm, "v_max": v_max, "v_sub": v_sub, "s_exp": s_exp, "v_sum": v_sum, "v_mul": v_mul, "s_tout": s_tout,
         }
         first_u = min([OFF[name][0] for name in ORDER if name in OFF])
         last_u = max([OFF[name][0] + OFF[name][1] * (OFF[name][2] - 1) for name in ORDER if name in OFF])

@@ -41,31 +41,37 @@ SM_ON_G = True
 G_PIECES = 1
 RG_PIECES = ((0, 4),)
 WARM_N = 1
+WARM_K0 = NQ
 MX_PRE = 0
 V_SPLIT = False
+AV_ADD = False
+V_EXTRA = False
+V_WHEN = (1, 1, 2)
+EADD_MB = 0
+OPS_MX_K0 = 22
+ADD_WHEN = 2
 G_WHEN = (0, 1, 2)
 QN_PIECES = 1
 QR_F32 = False
-V_RG = (1, 3)
+V_RG = (2, 3, 4,)
 
 OFF = {
-    "pe_mxq": (-12, 3, 32),
-    "pe_mxk": (-12, 3, 32),
-    "s_q": (-12, 3, 32),
-    "g_qlo": (-11, 3, 32),
-    "s_k": (-12, 3, 32),
-    "pe_mxv": (-11, 3, 32),
-    "s_v": (-11, 3, 32),
-    "pe_qrel": (-7, 3, 32),
-    "s_qr": (-7, 3, 32),
-    "pe_sh0": (21, 12, 8),
-    "s_sh0": (21, 12, 8),
-    "pe_sh2": (22, 12, 8),
-    "s_sh2": (22, 12, 8),
+    "pe_mxq": (-10, 3, 32),
+    "pe_mxk": (-10, 3, 32),
+    "s_q": (-10, 3, 32),
+    "g_qlo": (-9, 3, 32),
+    "s_k": (-10, 3, 32),
+    "pe_mxv": (-9, 3, 32),
+    "s_v": (-9, 3, 32),
+    "pe_qrel": (-5, 3, 32),
+    "s_qr": (-5, 3, 32),
+    "pe_sh0": (22, 12, 8),
+    "s_sh0": (22, 12, 8),
+    "pe_sh2": (23, 12, 8),
+    "s_sh2": (23, 12, 8),
     "pe_sh1": (23, 12, 8),
     "pe_sh2t": (24, 12, 8),
     "pe_abegin": (27, 3, 32),
-    "pe_asteps": (27, 1, 96),
     "pe_aend": (29, 3, 32),
     "s_osb": (29, 3, 32),
     "pe_qshift": (-1, 1, 96),
@@ -75,21 +81,24 @@ OFF = {
     "s_esb": (7, 4, 24),
     "v_qk": (0, 1, 96),
     "av": (24, 1, 96),
-    "s_rg0": (-18, 3, 32),
-    "v_quant": (-15, 3, 32),
+    "s_rg0": (-16, 3, 32),
+    "v_quant": (-13, 3, 32),
     "v_max": (16, 12, 8),
     "v_sub": (17, 12, 8),
     "s_exp": (18, 12, 8),
     "v_sum": (19, 12, 8),
     "v_mul": (20, 12, 8),
     "s_tout": (21, 12, 8),
+    "pe_asteps0": (27, 3, 32),
+    "pe_asteps1": (28, 3, 32),
+    "pe_asteps2": (29, 3, 32),
 }
 ORDER = (
     "pe_qshift", "pe_mxq", "pe_mxk", "s_q", "g_qlo", "s_k", "pe_mxv", "s_v",
     "pe_qrel", "s_qr", "pe_sh0", "s_sh0", "pe_sh2", "s_sh2", "pe_sh1", "pe_sh2t",
-    "pe_abegin", "pe_asteps", "pe_aend", "s_osb", "pe_ebegin", "pe_esteps", "pe_eend", "s_esb",
-    "v_qk", "av", "s_rg0", "s_rg1", "s_rg2", "s_rg3", "v_quant", "v_max",
-    "v_sub", "s_exp", "v_sum", "v_mul", "s_tout",
+    "pe_asteps1", "pe_asteps2", "pe_aend", "s_osb", "pe_ebegin", "pe_esteps", "pe_eend", "s_esb",
+    "pe_abegin", "pe_asteps0", "v_qk", "av", "s_rg0", "s_rg1", "s_rg2", "s_rg3",
+    "v_quant", "v_max", "v_sub", "s_exp", "v_sum", "v_mul", "s_tout",
 )
 
 FLOPS = 2 * 3 * 128 * 512 * H * W + 2 * 2 * WIN * 128 * H * W
@@ -360,7 +369,7 @@ def tile_mutliheadattention2d_kernel(tc, x, Wq, Wk, Wv, rel_t, rel_f, out_0, out
             pending = []
             for i in range(3):
                 n = 3 * i + j
-                for c in range(CG):
+                for c in range(CG // 2 if m < EADD_MB else CG):
                     pending.append((t_e[:, i, :], prod[(m, n)][:, c, :], perms[j], c == 0, False))
                 pending.append((t_e[:, i, :], qr9[m][:, n, :], ident_f, False, True))
             ework["todo"] = pending
@@ -419,26 +428,39 @@ def tile_mutliheadattention2d_kernel(tc, x, Wq, Wk, Wv, rel_t, rel_f, out_0, out
             for r in range(MBR):
                 nc.sync.dma_start(out=o1[:, m * MBR + r, :], in_=t_t[r * NG:(r + 1) * NG, :, :].rearrange("p w n -> p (w n)"))
 
-        def in_psum(m, i):
-            return i == 1 or (m >= TAIL_MB and i == 2)
+        def tail(m):
+            return m >= TAIL_MB
+
+        def on_vector(m, i, j):
+            return i == 1 or (i == 2 and (tail(m) or (V_EXTRA and j == 1)))
 
         def pe_shift(m, i):
             if i == 1:
-                t_ps = psum.tile([P, 3, P], F32, name="sh_ps", tag="shv")
-            elif in_psum(m, i):
-                t_ps = psum.tile([P, 3, P], F32, name="sh_ps", tag="qj", bufs=QJ_BUFS)
+                t_ps = psum.tile([P, 4, P], F32, name="sh_ps", tag="shv")
+                todo = [(1, 0, 0), (1, 1, 1), (1, 2, 2)] + ([(2, 1, 3)] if (V_EXTRA or tail(m)) else [])
+                sh[(m, "v")] = t_ps
+            elif i == 2 and tail(m):
+                t_ps = psum.tile([P, 2, P], F32, name="sh_ps", tag="qj", bufs=QJ_BUFS)
+                todo = [(2, 0, 0), (2, 2, 1)]
+                sh[(m, "t")] = t_ps
+            elif i == 2 and V_EXTRA:
+                t_ps = aux_tile([P, 2, P], "sh_ps")
+                todo = [(2, 0, 0), (2, 2, 1)]
+                sh[(m, i)] = t_ps
             else:
                 t_ps = aux_tile([P, 3, P], "sh_ps")
-            for j in range(3):
-                nc.tensor.transpose(t_ps[:, j, :], atts[m % 2][:, 3 * i + j, 2 - j:2 - j + W], ident_f[:])
-            sh[(m, i)] = t_ps
+                todo = [(i, 0, 0), (i, 1, 1), (i, 2, 2)]
+                sh[(m, i)] = t_ps
+            for ii, j, slot in todo:
+                nc.tensor.transpose(t_ps[:, slot, :], atts[m % 2][:, 3 * ii + j, 2 - j:2 - j + W], ident_f[:])
 
         def s_shift(m, i):
             t_sb = shp.tile([P, 3, P], F32, name="sh_sb")
-            nc.scalar.copy(out=t_sb[:], in_=sh[(m, i)][:])
+            n = sh[(m, i)].shape[1]
+            nc.scalar.copy(out=t_sb[:, 0:n, :], in_=sh[(m, i)][:])
             sh[(m, i)] = t_sb
 
-        def av_piece(eng, m, a, i, j0, nj):
+        def av_mul(eng, m, a, i, j0, nj, jstep, src, s0):
             h0 = m * MBR + a * R
             t_q = pv[(m, a, i)]
             lo = max(0, 1 - i - h0)
@@ -447,10 +469,13 @@ def tile_mutliheadattention2d_kernel(tc, x, Wq, Wk, Wv, rel_t, rel_f, out_0, out
                 b = lo + off
                 x0 = (a * R + b) * NG
                 eng.tensor_tensor(
-                    out=t_q[:, j0:j0 + nj, b:b + cnt, :].rearrange("p j r (g c) -> p j (r g) c", c=CG),
+                    out=t_q[:, j0:j0 + (nj - 1) * jstep + 1:jstep, b:b + cnt, :].rearrange("p j r (g c) -> p j (r g) c", c=CG),
                     in0=v_ring[:, slot:slot + cnt, :].rearrange("p r (g c) -> p (r g) c", c=CG).unsqueeze(1).to_broadcast([P, nj, cnt * NG, CG]),
-                    in1=sh[(m, i)][:, j0:j0 + nj, x0:x0 + cnt * NG].unsqueeze(3).to_broadcast([P, nj, cnt * NG, CG]),
+                    in1=src[:, s0:s0 + nj, x0:x0 + cnt * NG].unsqueeze(3).to_broadcast([P, nj, cnt * NG, CG]),
                     op=ALU.mult)
+
+        def summed(k):
+            return AV_ADD and 0 < k < NQ - 1 and not tail(k // QPM)
 
         def av(idx):
             k, s = divmod(idx, 3)
@@ -459,25 +484,48 @@ def tile_mutliheadattention2d_kernel(tc, x, Wq, Wk, Wv, rel_t, rel_f, out_0, out
                 for i in range(3):
                     t_new = pvp.tile([P, 3, R, P], F32, name="pv")
                     pv[(m, a, i)] = t_new
+            if s == G_WHEN[0]:
+                av_mul(nc.gpsimd, m, a, 0, 0, 3, 1, sh[(m, 0)], 0)
+            if s == V_WHEN[0]:
+                av_mul(nc.vector, m, a, 1, 0, 3, 1, sh[(m, "v")], 0)
+            if tail(m):
+                if s == V_WHEN[1]:
+                    av_mul(nc.vector, m, a, 2, 1, 1, 1, sh[(m, "v")], 3)
+                if s == V_WHEN[2]:
+                    av_mul(nc.vector, m, a, 2, 0, 2, 2, sh[(m, "t")], 0)
+            elif V_EXTRA:
+                if s == V_WHEN[1]:
+                    av_mul(nc.vector, m, a, 2, 1, 1, 1, sh[(m, "v")], 3)
+                if s == G_WHEN[2]:
+                    av_mul(nc.gpsimd, m, a, 2, 0, 2, 2, sh[(m, 2)], 0)
+            elif s == G_WHEN[2]:
+                av_mul(nc.gpsimd, m, a, 2, 0, 3, 1, sh[(m, 2)], 0)
+            if s == ADD_WHEN and summed(k):
+                step = 2 if V_EXTRA else 1
+                nc.gpsimd.tensor_tensor(out=pv[(m, a, 0)][:, 0:3:step], in0=pv[(m, a, 0)][:, 0:3:step], in1=pv[(m, a, 2)][:, 0:3:step], op=ALU.add)
+
+        def g_eadd(u):
+            m, j, a = decode(u)
+            cols = slice(a * R * NG, (a + 1) * R * NG)
             for i in range(3):
-                if in_psum(m, i):
-                    if V_SPLIT:
-                        av_piece(nc.vector, m, a, i, s, 1)
-                    elif s == i:
-                        av_piece(nc.vector, m, a, i, 0, 3)
-                elif s == G_WHEN[i]:
-                    for j0 in range(0, 3, 3 // G_PIECES):
-                        av_piece(nc.gpsimd, m, a, i, j0, 3 // G_PIECES)
+                t_p = prod[(m, 3 * i + j)]
+                nc.gpsimd.tensor_tensor(out=t_p[:, 0:CG // 2, cols], in0=t_p[:, 0:CG // 2, cols], in1=t_p[:, CG // 2:CG, cols], op=ALU.add)
 
         awork = {"todo": [], "pos": 0, "tile": None}
 
         def pe_abegin(k):
             m, a = divmod(k, QPM)
             h0 = m * MBR + a * R
-            t_o = psum.tile([P, R, W], F32, name="o_ps", tag="ops")
+            if k >= OPS_MX_K0:
+                t_o = psum.tile([P, R, W], F32, name="o_ps", tag="mx", bufs=MX_BUFS)
+            else:
+                t_o = psum.tile([P, R, W], F32, name="o_ps", tag="ops")
+            if k >= WARM_K0:
+                for rep in range(WARM_N):
+                    q_pass(NQ - 1, t_o)
             pending = []
             for r in range(R):
-                terms = [(i, j) for i in range(3) for j in range(3) if 0 <= h0 + r + i - 1 < H]
+                terms = [(i, j) for i in range(3) for j in range(3) if 0 <= h0 + r + i - 1 < H and not (i == 2 and summed(k) and not (V_EXTRA and j == 1))]
                 for idx, (i, j) in enumerate(terms):
                     pending.append((t_o[:, r, :], pv[(m, a, i)][:, j, r, :], perms[j], idx == 0, idx == len(terms) - 1))
             awork["todo"] = pending
@@ -508,11 +556,12 @@ def tile_mutliheadattention2d_kernel(tc, x, Wq, Wk, Wv, rel_t, rel_f, out_0, out
             "pe_mxq": pe_mxq, "pe_mxk": pe_mxk, "pe_mxv": pe_mxv, "s_q": s_q, "g_qlo": g_qlo, "s_k": s_k, "s_v": s_v,
             "pe_qrel": pe_qrel, "s_qr": s_qr,
             "pe_sh0": lambda m: pe_shift(m, 0), "s_sh0": lambda m: s_shift(m, 0),
-            "pe_sh2": only(lambda m: not in_psum(m, 2), lambda m: pe_shift(m, 2)),
-            "s_sh2": only(lambda m: not in_psum(m, 2), lambda m: s_shift(m, 2)),
-            "pe_sh1": lambda m: pe_shift(m, 1), "pe_sh2t": only(lambda m: in_psum(m, 2), lambda m: pe_shift(m, 2)),
-            "pe_abegin": pe_abegin, "pe_asteps": pe_asteps, "pe_aend": pe_aend, "s_osb": s_osb,
-            "pe_qshift": pe_qshift, "pe_ebegin": pe_ebegin, "pe_esteps": pe_esteps, "pe_eend": pe_eend, "s_esb": s_esb,
+            "pe_sh2": only(lambda m: not tail(m), lambda m: pe_shift(m, 2)),
+            "s_sh2": only(lambda m: not tail(m), lambda m: s_shift(m, 2)),
+            "pe_sh1": lambda m: pe_shift(m, 1), "pe_sh2t": only(tail, lambda m: pe_shift(m, 2)),
+            "g_eadd": g_eadd, "pe_ebegin_h": pe_ebegin,
+            "pe_abegin": pe_abegin, "pe_asteps": pe_asteps, "pe_asteps0": pe_asteps, "pe_asteps1": pe_asteps, "pe_asteps2": pe_asteps, "pe_aend": pe_aend, "s_osb": s_osb,
+            "pe_qshift": pe_qshift, "pe_ebegin": lambda idx: pe_ebegin(idx + 3 * EADD_MB), "pe_esteps": pe_esteps, "pe_eend": pe_eend, "s_esb": s_esb,
             "v_qk": v_qk, "av": av, "v_quant": v_quant, "v_quant1": lambda q: v_quant(q, 1),
             "s_rg0": lambda q: s_rg(q, 0), "s_rg1": lambda q: s_rg(q, 1), "s_rg2": lambda q: s_rg(q, 2), "s_rg3": lambda q: s_rg(q, 3),
             "pe_warm": pe_warm, "v_max": v_max, "v_sub": v_sub, "s_exp": s_exp, "v_sum": v_sum, "v_mul": v_mul, "s_tout": s_tout,

@@ -38,16 +38,21 @@ MX_BUFS = 3
 AUX_TAG = "mx"
 LOAD_ON_SCALAR = False
 SM_ON_G = True
+MUL_ON_V = False
+SUB_ON_V = False
 G_PIECES = 1
 RG_PIECES = ((0, 4),)
 WARM_N = 1
 WARM_K0 = NQ
 MX_PRE = 0
 V_SPLIT = False
-AV_ADD = False
-V_EXTRA = False
+AV_ADD = True
+ADD_MOD = 2
+V_EXTRA = True
 V_WHEN = (1, 1, 2)
 EADD_MB = 0
+RED_N = ()
+V_ADD = False
 OPS_MX_K0 = 22
 ADD_WHEN = 2
 G_WHEN = (0, 1, 2)
@@ -130,6 +135,7 @@ def tile_mutliheadattention2d_kernel(tc, x, Wq, Wk, Wv, rel_t, rel_f, out_0, out
         outp = ctx.enter_context(tc.tile_pool(name="outp", bufs=2))
         attp = ctx.enter_context(tc.tile_pool(name="attp", bufs=1))
         smallp = ctx.enter_context(tc.tile_pool(name="smallp", bufs=2))
+        redp = ctx.enter_context(tc.tile_pool(name="redp", bufs=2))
         halfp = ctx.enter_context(tc.tile_pool(name="halfp", bufs=3))
         psum = ctx.enter_context(tc.psum_pool(name="psum", bufs=1))
 
@@ -297,6 +303,11 @@ def tile_mutliheadattention2d_kernel(tc, x, Wq, Wk, Wv, rel_t, rel_f, out_0, out
             nc.gpsimd.tensor_tensor(out=t_lo[:], in0=q_ring[:, qs:qs + R, 1:W + 1], in1=q_hi[q][:], op=ALU.subtract)
             q_lo[q] = t_lo
 
+        def v_qlo(q):
+            t_lo = halfp.tile([P, R, W], BF16, name="q_lo")
+            nc.vector.tensor_tensor(out=t_lo[:], in0=ps[("q", q)][:], in1=q_hi[q][:], op=ALU.subtract)
+            q_lo[q] = t_lo
+
         def s_k(q):
             ks = (q * R) % RK
             nc.scalar.copy(out=k_ring[:, ks:ks + R, :], in_=ps[("k", q)][:])
@@ -362,15 +373,26 @@ def tile_mutliheadattention2d_kernel(tc, x, Wq, Wk, Wv, rel_t, rel_f, out_0, out
                         in1=qjt[u][:, off:off + cnt, :].rearrange("p r (c g) -> p c r g", g=NG), op=ALU.mult)
 
         ework = {"todo": [], "pos": 0, "tile": None}
+        ered = {}
+
+        def v_red(f):
+            m, j = divmod(f, 3)
+            for i in [i for i in range(3) if 3 * i + j in RED_N]:
+                t_r = redp.tile([P, P], F32, name="ered")
+                nc.vector.tensor_reduce(out=t_r[:], in_=prod[(m, 3 * i + j)][:].rearrange("p c x -> p x c"), axis=AX.X, op=ALU.add)
+                ered[(m, 3 * i + j)] = t_r
 
         def pe_ebegin(f):
             m, j = divmod(f, 3)
             t_e = psum.tile([P, 3, W], F32, name="e_ps", tag="eps")
             pending = []
-            for i in range(3):
+            for i in [i for i in range(3) if 3 * i + j not in RED_N] + [i for i in range(3) if 3 * i + j in RED_N]:
                 n = 3 * i + j
-                for c in range(CG // 2 if m < EADD_MB else CG):
-                    pending.append((t_e[:, i, :], prod[(m, n)][:, c, :], perms[j], c == 0, False))
+                if n in RED_N:
+                    pending.append((t_e[:, i, :], ered[(m, n)][:], perms[j], True, False))
+                else:
+                    for c in range(CG // 2 if m < EADD_MB else CG):
+                        pending.append((t_e[:, i, :], prod[(m, n)][:, c, :], perms[j], c == 0, False))
                 pending.append((t_e[:, i, :], qr9[m][:, n, :], ident_f, False, True))
             ework["todo"] = pending
             ework["pos"] = 0
@@ -405,7 +427,7 @@ def tile_mutliheadattention2d_kernel(tc, x, Wq, Wk, Wv, rel_t, rel_f, out_0, out
 
         def v_sub(m):
             flat = esb[m][:].rearrange("p i j w -> p (i j) w")
-            sm_eng.tensor_tensor(out=flat, in0=flat, in1=tops[m][:].unsqueeze(1).to_broadcast([P, WIN, W]), op=ALU.subtract)
+            (nc.vector if SUB_ON_V else sm_eng).tensor_tensor(out=flat, in0=flat, in1=tops[m][:].unsqueeze(1).to_broadcast([P, WIN, W]), op=ALU.subtract)
 
         def s_exp(m):
             flat = esb[m][:].rearrange("p i j w -> p (i j) w")
@@ -419,7 +441,7 @@ def tile_mutliheadattention2d_kernel(tc, x, Wq, Wk, Wv, rel_t, rel_f, out_0, out
             sums[m] = t_r
 
         def v_mul(m):
-            sm_eng.tensor_tensor(out=atts[m % 2][:, :, 1:W + 1], in0=esb[m][:].rearrange("p i j w -> p (i j) w"),
+            (nc.vector if MUL_ON_V else sm_eng).tensor_tensor(out=atts[m % 2][:, :, 1:W + 1], in0=esb[m][:].rearrange("p i j w -> p (i j) w"),
                                  in1=sums[m][:].unsqueeze(1).to_broadcast([P, WIN, W]), op=ALU.mult)
 
         def s_tout(m):
@@ -475,7 +497,7 @@ def tile_mutliheadattention2d_kernel(tc, x, Wq, Wk, Wv, rel_t, rel_f, out_0, out
                     op=ALU.mult)
 
         def summed(k):
-            return AV_ADD and 0 < k < NQ - 1 and not tail(k // QPM)
+            return AV_ADD and 0 < k < NQ - 1 and not tail(k // QPM) and k % ADD_MOD == 0
 
         def av(idx):
             k, s = divmod(idx, 3)
@@ -504,6 +526,14 @@ def tile_mutliheadattention2d_kernel(tc, x, Wq, Wk, Wv, rel_t, rel_f, out_0, out
                 step = 2 if V_EXTRA else 1
                 nc.gpsimd.tensor_tensor(out=pv[(m, a, 0)][:, 0:3:step], in0=pv[(m, a, 0)][:, 0:3:step], in1=pv[(m, a, 2)][:, 0:3:step], op=ALU.add)
 
+        def vsummed(k):
+            return V_ADD and 0 < k < NQ - 1
+
+        def v_add(k):
+            m, a = divmod(k, QPM)
+            if vsummed(k):
+                nc.vector.tensor_tensor(out=pv[(m, a, 1)][:], in0=pv[(m, a, 1)][:], in1=pv[(m, a, 0)][:], op=ALU.add)
+
         def g_eadd(u):
             m, j, a = decode(u)
             cols = slice(a * R * NG, (a + 1) * R * NG)
@@ -525,7 +555,7 @@ def tile_mutliheadattention2d_kernel(tc, x, Wq, Wk, Wv, rel_t, rel_f, out_0, out
                     q_pass(NQ - 1, t_o)
             pending = []
             for r in range(R):
-                terms = [(i, j) for i in range(3) for j in range(3) if 0 <= h0 + r + i - 1 < H and not (i == 2 and summed(k) and not (V_EXTRA and j == 1))]
+                terms = [(i, j) for i in range(3) for j in range(3) if 0 <= h0 + r + i - 1 < H and not (i == 2 and summed(k) and not (V_EXTRA and j == 1)) and not (i == 0 and vsummed(k))]
                 for idx, (i, j) in enumerate(terms):
                     pending.append((t_o[:, r, :], pv[(m, a, i)][:, j, r, :], perms[j], idx == 0, idx == len(terms) - 1))
             awork["todo"] = pending
@@ -559,7 +589,7 @@ def tile_mutliheadattention2d_kernel(tc, x, Wq, Wk, Wv, rel_t, rel_f, out_0, out
             "pe_sh2": only(lambda m: not tail(m), lambda m: pe_shift(m, 2)),
             "s_sh2": only(lambda m: not tail(m), lambda m: s_shift(m, 2)),
             "pe_sh1": lambda m: pe_shift(m, 1), "pe_sh2t": only(tail, lambda m: pe_shift(m, 2)),
-            "g_eadd": g_eadd, "pe_ebegin_h": pe_ebegin,
+            "g_eadd": g_eadd, "v_qlo": v_qlo, "v_red": v_red, "v_add": v_add, "pe_ebegin_h": pe_ebegin,
             "pe_abegin": pe_abegin, "pe_asteps": pe_asteps, "pe_asteps0": pe_asteps, "pe_asteps1": pe_asteps, "pe_asteps2": pe_asteps, "pe_aend": pe_aend, "s_osb": s_osb,
             "pe_qshift": pe_qshift, "pe_ebegin": lambda idx: pe_ebegin(idx + 3 * EADD_MB), "pe_esteps": pe_esteps, "pe_eend": pe_eend, "s_esb": s_esb,
             "v_qk": v_qk, "av": av, "v_quant": v_quant, "v_quant1": lambda q: v_quant(q, 1),

@@ -68,8 +68,8 @@ OFF = {
     "s_k": (-10, 3, 32),
     "pe_mxv": (-9, 3, 32),
     "s_v": (-9, 3, 32),
-    "pe_qrel": (-5, 3, 32),
-    "s_qr": (-5, 3, 32),
+    "pe_qrel": (-6, 3, 32),
+    "s_qr": (-6, 3, 32),
     "pe_sh0": (22, 12, 8),
     "s_sh0": (22, 12, 8),
     "pe_sh2": (23, 12, 8),

@@ -47,7 +47,10 @@ WARM_K0 = NQ
 MX_PRE = 0
 V_SPLIT = False
 AV_ADD = True
-ADD_MOD = 2
+VT_ADD = False
+S_01 = True
+S_00 = False
+ADD_MOD = 1
 V_EXTRA = True
 V_WHEN = (1, 1, 2)
 EADD_MB = 0
@@ -97,13 +100,14 @@ OFF = {
     "pe_asteps0": (27, 3, 32),
     "pe_asteps1": (28, 3, 32),
     "pe_asteps2": (29, 3, 32),
+    "s_av": (24, 1, 96),
 }
 ORDER = (
     "pe_qshift", "pe_mxq", "pe_mxk", "s_q", "g_qlo", "s_k", "pe_mxv", "s_v",
     "pe_qrel", "s_qr", "pe_sh0", "s_sh0", "pe_sh2", "s_sh2", "pe_sh1", "pe_sh2t",
     "pe_asteps1", "pe_asteps2", "pe_aend", "s_osb", "pe_ebegin", "pe_esteps", "pe_eend", "s_esb",
-    "pe_abegin", "pe_asteps0", "v_qk", "av", "s_rg0", "s_rg1", "s_rg2", "s_rg3",
-    "v_quant", "v_max", "v_sub", "s_exp", "v_sum", "v_mul", "s_tout",
+    "pe_abegin", "pe_asteps0", "v_qk", "av", "s_av", "s_rg0", "s_rg1", "s_rg2",
+    "s_rg3", "v_quant", "v_max", "v_sub", "s_exp", "v_sum", "v_mul", "s_tout",
 )
 
 FLOPS = 2 * 3 * 128 * 512 * H * W + 2 * 2 * WIN * 128 * H * W
@@ -482,7 +486,7 @@ def tile_mutliheadattention2d_kernel(tc, x, Wq, Wk, Wv, rel_t, rel_f, out_0, out
             nc.scalar.copy(out=t_sb[:, 0:n, :], in_=sh[(m, i)][:])
             sh[(m, i)] = t_sb
 
-        def av_mul(eng, m, a, i, j0, nj, jstep, src, s0):
+        def av_mul(eng, m, a, i, j0, nj, jstep, src, s0, sstep=1):
             h0 = m * MBR + a * R
             t_q = pv[(m, a, i)]
             lo = max(0, 1 - i - h0)
@@ -493,7 +497,7 @@ def tile_mutliheadattention2d_kernel(tc, x, Wq, Wk, Wv, rel_t, rel_f, out_0, out
                 eng.tensor_tensor(
                     out=t_q[:, j0:j0 + (nj - 1) * jstep + 1:jstep, b:b + cnt, :].rearrange("p j r (g c) -> p j (r g) c", c=CG),
                     in0=v_ring[:, slot:slot + cnt, :].rearrange("p r (g c) -> p (r g) c", c=CG).unsqueeze(1).to_broadcast([P, nj, cnt * NG, CG]),
-                    in1=src[:, s0:s0 + nj, x0:x0 + cnt * NG].unsqueeze(3).to_broadcast([P, nj, cnt * NG, CG]),
+                    in1=src[:, s0:s0 + (nj - 1) * sstep + 1:sstep, x0:x0 + cnt * NG].unsqueeze(3).to_broadcast([P, nj, cnt * NG, CG]),
                     op=ALU.mult)
 
         def summed(k):
@@ -507,7 +511,12 @@ def tile_mutliheadattention2d_kernel(tc, x, Wq, Wk, Wv, rel_t, rel_f, out_0, out
                     t_new = pvp.tile([P, 3, R, P], F32, name="pv")
                     pv[(m, a, i)] = t_new
             if s == G_WHEN[0]:
-                av_mul(nc.gpsimd, m, a, 0, 0, 3, 1, sh[(m, 0)], 0)
+                if S_00 and not tail(m):
+                    av_mul(nc.gpsimd, m, a, 0, 2, 1, 1, sh[(m, 0)], 2)
+                elif S_01 and not tail(m):
+                    av_mul(nc.gpsimd, m, a, 0, 0, 2, 2, sh[(m, 0)], 0, 2)
+                else:
+                    av_mul(nc.gpsimd, m, a, 0, 0, 3, 1, sh[(m, 0)], 0)
             if s == V_WHEN[0]:
                 av_mul(nc.vector, m, a, 1, 0, 3, 1, sh[(m, "v")], 0)
             if tail(m):
@@ -523,14 +532,33 @@ def tile_mutliheadattention2d_kernel(tc, x, Wq, Wk, Wv, rel_t, rel_f, out_0, out
             elif s == G_WHEN[2]:
                 av_mul(nc.gpsimd, m, a, 2, 0, 3, 1, sh[(m, 2)], 0)
             if s == ADD_WHEN and summed(k):
-                step = 2 if V_EXTRA else 1
+                step = 2 if (V_EXTRA and not S_00) else 1
                 nc.gpsimd.tensor_tensor(out=pv[(m, a, 0)][:, 0:3:step], in0=pv[(m, a, 0)][:, 0:3:step], in1=pv[(m, a, 2)][:, 0:3:step], op=ALU.add)
+
+        def s_av(idx):
+            k, s = divmod(idx, 3)
+            m, a = divmod(k, QPM)
+            h0 = m * MBR + a * R
+            if S_01 and not tail(m):
+                for r in ((0, 1), (2,), (3,))[s]:
+                    if h0 + r - 1 >= 0:
+                        slot = (h0 + r - 1) % RV
+                        for j in ((0, 1) if S_00 else (1,)):
+                            for g in range(NG):
+                                x = (a * R + r) * NG + g
+                                nc.scalar.activation(out=pv[(m, a, 0)][:, j, r, g * CG:(g + 1) * CG], in_=v_ring[:, slot, g * CG:(g + 1) * CG],
+                                                     func=ACT.Copy, scale=sh[(m, 0)][:, j, x:x + 1])
 
         def vsummed(k):
             return V_ADD and 0 < k < NQ - 1
 
+        def tsummed(k):
+            return VT_ADD and tail(k // QPM) and k < NQ - 1
+
         def v_add(k):
             m, a = divmod(k, QPM)
+            if tsummed(k):
+                nc.vector.tensor_tensor(out=pv[(m, a, 1)][:], in0=pv[(m, a, 1)][:], in1=pv[(m, a, 2)][:], op=ALU.add)
             if vsummed(k):
                 nc.vector.tensor_tensor(out=pv[(m, a, 1)][:], in0=pv[(m, a, 1)][:], in1=pv[(m, a, 0)][:], op=ALU.add)
 
@@ -555,7 +583,7 @@ def tile_mutliheadattention2d_kernel(tc, x, Wq, Wk, Wv, rel_t, rel_f, out_0, out
                     q_pass(NQ - 1, t_o)
             pending = []
             for r in range(R):
-                terms = [(i, j) for i in range(3) for j in range(3) if 0 <= h0 + r + i - 1 < H and not (i == 2 and summed(k) and not (V_EXTRA and j == 1)) and not (i == 0 and vsummed(k))]
+                terms = [(i, j) for i in range(3) for j in range(3) if 0 <= h0 + r + i - 1 < H and not (i == 2 and summed(k) and not (V_EXTRA and not S_00 and j == 1)) and not (i == 0 and vsummed(k)) and not (i == 2 and tsummed(k))]
                 for idx, (i, j) in enumerate(terms):
                     pending.append((t_o[:, r, :], pv[(m, a, i)][:, j, r, :], perms[j], idx == 0, idx == len(terms) - 1))
             awork["todo"] = pending
@@ -589,7 +617,7 @@ def tile_mutliheadattention2d_kernel(tc, x, Wq, Wk, Wv, rel_t, rel_f, out_0, out
             "pe_sh2": only(lambda m: not tail(m), lambda m: pe_shift(m, 2)),
             "s_sh2": only(lambda m: not tail(m), lambda m: s_shift(m, 2)),
             "pe_sh1": lambda m: pe_shift(m, 1), "pe_sh2t": only(tail, lambda m: pe_shift(m, 2)),
-            "g_eadd": g_eadd, "v_qlo": v_qlo, "v_red": v_red, "v_add": v_add, "pe_ebegin_h": pe_ebegin,
+            "g_eadd": g_eadd, "s_av": s_av, "v_qlo": v_qlo, "v_red": v_red, "v_add": v_add, "pe_ebegin_h": pe_ebegin,
             "pe_abegin": pe_abegin, "pe_asteps": pe_asteps, "pe_asteps0": pe_asteps, "pe_asteps1": pe_asteps, "pe_asteps2": pe_asteps, "pe_aend": pe_aend, "s_osb": s_osb,
             "pe_qshift": pe_qshift, "pe_ebegin": lambda idx: pe_ebegin(idx + 3 * EADD_MB), "pe_esteps": pe_esteps, "pe_eend": pe_eend, "s_esb": s_esb,
             "v_qk": v_qk, "av": av, "v_quant": v_quant, "v_quant1": lambda q: v_quant(q, 1),

@@ -45,11 +45,15 @@ RG_PIECES = ((0, 4),)
 WARM_N = 1
 WARM_K0 = NQ
 MX_PRE = 0
+PRE_Q = 0
+PRE_V = 0
 V_SPLIT = False
 AV_ADD = True
 VT_ADD = False
 S_01 = True
 S_00 = False
+S_21 = False
+S_ROWS = ((0, 1), (2,), (3,))
 ADD_MOD = 1
 V_EXTRA = True
 V_WHEN = (1, 1, 2)
@@ -198,12 +202,12 @@ def tile_mutliheadattention2d_kernel(tc, x, Wq, Wk, Wv, rel_t, rel_f, out_0, out
         atts = []
         for idx in range(2):
             t_att = const.tile([P, WIN, W + 2], F32, name="att%d" % idx)
-            nc.gpsimd.memset(t_att[:], 0.0)
+            nc.gpsimd.memset(t_att[:, :, 0:W + 2:W + 1], 0.0)
             atts.append(t_att)
         q_ring = const.tile([P, RQ, W + 2], F32, name="q_ring")
-        nc.gpsimd.memset(q_ring[:], 0.0)
+        nc.gpsimd.memset(q_ring[:, :, 0:W + 2:W + 1], 0.0)
         k_ring = const.tile([P, RK, P], F32, name="k_ring")
-        nc.gpsimd.memset(k_ring[:], 0.0)
+        nc.gpsimd.memset(k_ring[:, RK - 1, :], 0.0)
         v_ring = const.tile([P, RV, P], F32, name="v_ring")
 
         w_de = pp.tile([P, 3, 4, P], BF16, name="w_de", tag="big", align_bytes=64)
@@ -271,9 +275,9 @@ def tile_mutliheadattention2d_kernel(tc, x, Wq, Wk, Wv, rel_t, rel_f, out_0, out
                                 lhsT_scale=w_scales[0][:], rhs=xc[q][:].bitcast(FP8X4), rhs_scale=xs[q][:],
                                 start=True, stop=True)
 
-        def mx_pixel(q, widx, name):
+        def mx_pixel(q, widx, name, extra=0):
             t_ps = psum.tile([P, R, P], F32, name=name, tag="mx", bufs=MX_BUFS)
-            for rep in range(MX_PRE):
+            for rep in range(MX_PRE + extra):
                 q_pass(q, t_ps)
             for r in range(R):
                 cols = slice(r * W, (r + 1) * W)
@@ -283,7 +287,7 @@ def tile_mutliheadattention2d_kernel(tc, x, Wq, Wk, Wv, rel_t, rel_f, out_0, out
 
         def pe_mxq(q):
             q_ps = psum.tile([P, R, W], F32, name="q_ps", tag="mx", bufs=MX_BUFS)
-            for rep in range(MX_PRE + 1):
+            for rep in range(MX_PRE + PRE_Q + 1):
                 q_pass(q, q_ps)
             ps[("q", q)] = q_ps
 
@@ -291,7 +295,7 @@ def tile_mutliheadattention2d_kernel(tc, x, Wq, Wk, Wv, rel_t, rel_f, out_0, out
             ps[("k", q)] = mx_pixel(q, 1, "k_ps")
 
         def pe_mxv(q):
-            ps[("v", q)] = mx_pixel(q, 2, "v_ps")
+            ps[("v", q)] = mx_pixel(q, 2, "v_ps", PRE_V)
 
         def s_q(q):
             qs = (q * R) % RQ
@@ -463,13 +467,13 @@ def tile_mutliheadattention2d_kernel(tc, x, Wq, Wk, Wv, rel_t, rel_f, out_0, out
         def pe_shift(m, i):
             if i == 1:
                 t_ps = psum.tile([P, 4, P], F32, name="sh_ps", tag="shv")
-                todo = [(1, 0, 0), (1, 1, 1), (1, 2, 2)] + ([(2, 1, 3)] if (V_EXTRA or tail(m)) else [])
+                todo = [(1, 0, 0), (1, 1, 1), (1, 2, 2)] + ([(2, 1, 3)] if ((V_EXTRA and not S_21) or tail(m)) else [])
                 sh[(m, "v")] = t_ps
             elif i == 2 and tail(m):
                 t_ps = psum.tile([P, 2, P], F32, name="sh_ps", tag="qj", bufs=QJ_BUFS)
                 todo = [(2, 0, 0), (2, 2, 1)]
                 sh[(m, "t")] = t_ps
-            elif i == 2 and V_EXTRA:
+            elif i == 2 and V_EXTRA and not S_21:
                 t_ps = aux_tile([P, 2, P], "sh_ps")
                 todo = [(2, 0, 0), (2, 2, 1)]
                 sh[(m, i)] = t_ps
@@ -525,10 +529,10 @@ def tile_mutliheadattention2d_kernel(tc, x, Wq, Wk, Wv, rel_t, rel_f, out_0, out
                 if s == V_WHEN[2]:
                     av_mul(nc.vector, m, a, 2, 0, 2, 2, sh[(m, "t")], 0)
             elif V_EXTRA:
-                if s == V_WHEN[1]:
+                if s == V_WHEN[1] and not S_21:
                     av_mul(nc.vector, m, a, 2, 1, 1, 1, sh[(m, "v")], 3)
                 if s == G_WHEN[2]:
-                    av_mul(nc.gpsimd, m, a, 2, 0, 2, 2, sh[(m, 2)], 0)
+                    av_mul(nc.gpsimd, m, a, 2, 0, 2, 2, sh[(m, 2)], 0, 2 if S_21 else 1)
             elif s == G_WHEN[2]:
                 av_mul(nc.gpsimd, m, a, 2, 0, 3, 1, sh[(m, 2)], 0)
             if s == ADD_WHEN and summed(k):
@@ -540,7 +544,7 @@ def tile_mutliheadattention2d_kernel(tc, x, Wq, Wk, Wv, rel_t, rel_f, out_0, out
             m, a = divmod(k, QPM)
             h0 = m * MBR + a * R
             if S_01 and not tail(m):
-                for r in ((0, 1), (2,), (3,))[s]:
+                for r in S_ROWS[s]:
                     if h0 + r - 1 >= 0:
                         slot = (h0 + r - 1) % RV
                         for j in ((0, 1) if S_00 else (1,)):
@@ -548,6 +552,19 @@ def tile_mutliheadattention2d_kernel(tc, x, Wq, Wk, Wv, rel_t, rel_f, out_0, out
                                 x = (a * R + r) * NG + g
                                 nc.scalar.activation(out=pv[(m, a, 0)][:, j, r, g * CG:(g + 1) * CG], in_=v_ring[:, slot, g * CG:(g + 1) * CG],
                                                      func=ACT.Copy, scale=sh[(m, 0)][:, j, x:x + 1])
+
+        def s_av2(idx):
+            k, s = divmod(idx, 3)
+            m, a = divmod(k, QPM)
+            h0 = m * MBR + a * R
+            if S_21 and not tail(m):
+                for r in S_ROWS[s]:
+                    if h0 + r + 1 < H:
+                        slot = (h0 + r + 1) % RV
+                        for g in range(NG):
+                            x = (a * R + r) * NG + g
+                            nc.scalar.activation(out=pv[(m, a, 2)][:, 1, r, g * CG:(g + 1) * CG], in_=v_ring[:, slot, g * CG:(g + 1) * CG],
+                                                 func=ACT.Copy, scale=sh[(m, 2)][:, 1, x:x + 1])
 
         def vsummed(k):
             return V_ADD and 0 < k < NQ - 1
@@ -617,7 +634,7 @@ def tile_mutliheadattention2d_kernel(tc, x, Wq, Wk, Wv, rel_t, rel_f, out_0, out
             "pe_sh2": only(lambda m: not tail(m), lambda m: pe_shift(m, 2)),
             "s_sh2": only(lambda m: not tail(m), lambda m: s_shift(m, 2)),
             "pe_sh1": lambda m: pe_shift(m, 1), "pe_sh2t": only(tail, lambda m: pe_shift(m, 2)),
-            "g_eadd": g_eadd, "s_av": s_av, "v_qlo": v_qlo, "v_red": v_red, "v_add": v_add, "pe_ebegin_h": pe_ebegin,
+            "g_eadd": g_eadd, "s_av": s_av, "s_av2": s_av2, "v_qlo": v_qlo, "v_red": v_red, "v_add": v_add, "pe_ebegin_h": pe_ebegin,
             "pe_abegin": pe_abegin, "pe_asteps": pe_asteps, "pe_asteps0": pe_asteps, "pe_asteps1": pe_asteps, "pe_asteps2": pe_asteps, "pe_aend": pe_aend, "s_osb": s_osb,
             "pe_qshift": pe_qshift, "pe_ebegin": lambda idx: pe_ebegin(idx + 3 * EADD_MB), "pe_esteps": pe_esteps, "pe_eend": pe_eend, "s_esb": s_esb,
             "v_qk": v_qk, "av": av, "v_quant": v_quant, "v_quant1": lambda q: v_quant(q, 1),

@@ -27,7 +27,7 @@ NMB = H // MBR
 SUB = 3 * QPM
 RQ = 32
 RK = 36
-RV = 64
+RV = 52
 RAW_BUFS = 4
 LAG = 24
 ESTEP = 13
@@ -66,6 +66,13 @@ G_WHEN = (0, 1, 2)
 QN_PIECES = 1
 QR_F32 = False
 V_RG = (2, 3, 4,)
+OUT_BUFS = 3
+COD_BUFS = 3
+O_QUEUE = "sync"
+T_QUEUE = "sync"
+JS = (0, 1, 2)
+QPIX = False
+QR_COLS = 72
 
 OFF = {
     "pe_mxq": (-10, 3, 32),
@@ -134,13 +141,13 @@ def tile_mutliheadattention2d_kernel(tc, x, Wq, Wk, Wv, rel_t, rel_f, out_0, out
         const = ctx.enter_context(tc.tile_pool(name="const", bufs=1))
         rawp = ctx.enter_context(tc.tile_pool(name="rawp", bufs=RAW_BUFS))
         grpp = ctx.enter_context(tc.tile_pool(name="grpp", bufs=2))
-        codp = ctx.enter_context(tc.tile_pool(name="codp", bufs=3))
+        codp = ctx.enter_context(tc.tile_pool(name="codp", bufs=COD_BUFS))
         pp = ctx.enter_context(tc.tile_pool(name="pp", bufs=6))
         qrp = ctx.enter_context(tc.tile_pool(name="qrp", bufs=2))
         esp = ctx.enter_context(tc.tile_pool(name="esp", bufs=2))
         shp = ctx.enter_context(tc.tile_pool(name="shp", bufs=4))
         pvp = ctx.enter_context(tc.tile_pool(name="pvp", bufs=6))
-        outp = ctx.enter_context(tc.tile_pool(name="outp", bufs=2))
+        outp = ctx.enter_context(tc.tile_pool(name="outp", bufs=OUT_BUFS))
         attp = ctx.enter_context(tc.tile_pool(name="attp", bufs=1))
         smallp = ctx.enter_context(tc.tile_pool(name="smallp", bufs=2))
         redp = ctx.enter_context(tc.tile_pool(name="redp", bufs=2))
@@ -352,14 +359,20 @@ def tile_mutliheadattention2d_kernel(tc, x, Wq, Wk, Wv, rel_t, rel_f, out_0, out
         def decode(u):
             m, rem = divmod(u, SUB)
             j, a = divmod(rem, QPM)
-            return m, j, a
+            return m, JS[j], a
 
         def pe_qshift(u):
             m, j, a = decode(u)
             qs = ((m * QPM + a) * R) % RQ
             t_ps = psum.tile([P, R, P], F32, name="qj", tag="qj", bufs=QJ_BUFS)
+            q = m * QPM + a
             for r in range(R):
-                nc.tensor.transpose(t_ps[:, r, :], q_ring[:, qs + r, 2 - j:2 - j + W], ident_f[:])
+                if QPIX and j == 1:
+                    cols = slice(r * W, (r + 1) * W)
+                    nc.tensor.matmul_mx(out=t_ps[:, r, :], lhsT=xc[q][:, cols].bitcast(FP8X4), lhsT_scale=xs[q][:, cols],
+                                        rhs=w_codes[0][:].bitcast(FP8X4), rhs_scale=w_scales[0][:], start=True, stop=True)
+                else:
+                    nc.tensor.transpose(t_ps[:, r, :], q_ring[:, qs + r, 2 - j:2 - j + W], ident_f[:])
             qjt[u] = t_ps
 
         def v_qk(u):
@@ -384,14 +397,16 @@ def tile_mutliheadattention2d_kernel(tc, x, Wq, Wk, Wv, rel_t, rel_f, out_0, out
         ered = {}
 
         def v_red(f):
-            m, j = divmod(f, 3)
+            m, jj = divmod(f, 3)
+            j = JS[jj]
             for i in [i for i in range(3) if 3 * i + j in RED_N]:
                 t_r = redp.tile([P, P], F32, name="ered")
                 nc.vector.tensor_reduce(out=t_r[:], in_=prod[(m, 3 * i + j)][:].rearrange("p c x -> p x c"), axis=AX.X, op=ALU.add)
                 ered[(m, 3 * i + j)] = t_r
 
         def pe_ebegin(f):
-            m, j = divmod(f, 3)
+            m, jj = divmod(f, 3)
+            j = JS[jj]
             t_e = psum.tile([P, 3, W], F32, name="e_ps", tag="eps")
             pending = []
             for i in [i for i in range(3) if 3 * i + j not in RED_N] + [i for i in range(3) if 3 * i + j in RED_N]:
@@ -420,8 +435,9 @@ def tile_mutliheadattention2d_kernel(tc, x, Wq, Wk, Wv, rel_t, rel_f, out_0, out
             work_step(ework, len(ework["todo"]))
 
         def s_esb(f):
-            m, j = divmod(f, 3)
-            if j == 0:
+            m, jj = divmod(f, 3)
+            j = JS[jj]
+            if jj == 0:
                 t_new = esp.tile([P, 3, 3, W], F32, name="esb")
                 esb[m] = t_new
             nc.scalar.copy(out=esb[m][:, :, j, :], in_=ps[("e", f)][:])
@@ -456,7 +472,7 @@ def tile_mutliheadattention2d_kernel(tc, x, Wq, Wk, Wv, rel_t, rel_f, out_0, out
             t_t = attp.tile([P, W, WIN], F32, name="t_out")
             nc.scalar.copy(out=t_t[:], in_=atts[m % 2][:, :, 1:W + 1].rearrange("p n w -> p w n"))
             for r in range(MBR):
-                nc.sync.dma_start(out=o1[:, m * MBR + r, :], in_=t_t[r * NG:(r + 1) * NG, :, :].rearrange("p w n -> p (w n)"))
+                {"sync": nc.sync, "scalar": nc.scalar, "gpsimd": nc.gpsimd}[T_QUEUE].dma_start(out=o1[:, m * MBR + r, :], in_=t_t[r * NG:(r + 1) * NG, :, :].rearrange("p w n -> p (w n)"))
 
         def tail(m):
             return m >= TAIL_MB
@@ -616,7 +632,7 @@ def tile_mutliheadattention2d_kernel(tc, x, Wq, Wk, Wv, rel_t, rel_f, out_0, out
         def s_osb(k):
             t_sb = outp.tile([P, PIX], F32, name="o_sb")
             nc.scalar.copy(out=t_sb[:], in_=ps[("o", k)][:].rearrange("p r w -> p (r w)"))
-            nc.sync.dma_start(out=o0[:, k * PIX:(k + 1) * PIX], in_=t_sb[:])
+            {"sync": nc.sync, "scalar": nc.scalar, "gpsimd": nc.gpsimd}[O_QUEUE].dma_start(out=o0[:, k * PIX:(k + 1) * PIX], in_=t_sb[:])
 
         def pe_warm(idx):
             t_ps = psum.tile([P, PIX], F32, name="warm_ps", tag="mx", bufs=MX_BUFS)

@@ -67,11 +67,11 @@ QN_PIECES = 1
 QR_F32 = False
 V_RG = (2, 3, 4,)
 OUT_BUFS = 3
-COD_BUFS = 3
+COD_BUFS = 5
 O_QUEUE = "sync"
 T_QUEUE = "sync"
-JS = (0, 1, 2)
-QPIX = False
+JS = (1, 0, 2)
+QPIX = True
 QR_COLS = 72
 
 OFF = {

@@ -57,7 +57,9 @@ S_ROWS = ((0, 1), (2,), (3,))
 ADD_MOD = 1
 V_EXTRA = True
 V_WHEN = (1, 1, 2)
-EADD_MB = 0
+EADD_MS = ()
+E_ROWS = (0, 1, 2)
+EADD_I = (0, 1, 2)
 RED_N = ()
 V_ADD = False
 OPS_MX_K0 = 22
@@ -66,15 +68,45 @@ G_WHEN = (0, 1, 2)
 QN_PIECES = 1
 QR_F32 = False
 V_RG = (2, 3, 4,)
-OUT_BUFS = 3
+OUT_BUFS = 2
 COD_BUFS = 5
 O_QUEUE = "sync"
 T_QUEUE = "sync"
 JS = (1, 0, 2)
 QPIX = True
 QR_COLS = 72
+SUM_ON_G = False
+G_SPLIT = False
+SM_SPLIT = 3
+SM_V_M = 8
+PV_BUFS = (2, 2, 2)
+ATT_BUFS = 2
+HALF_BUFS = 3
+G_RG = ()
+LOADS = ("w0", "w1", "w2", "x0", "rel", "x1", "x2", "x3")
+W_ORDER = (0, 1, 2)
+HEAD = {}
+W_TAG = "qj"
+A_ROWS = (0, 1, 2)
+PLAN = {
+    "banks": [[(1, 0), (1, 1), (1, 2)]],
+    "stage": {0: (0, 1, 2), 2: (0, 1, 2)},
+    "mul": [("g", 0, 0, (0, 2)), ("v", 1, 1, (0, 1, 2)), ("g", 2, 2, (0, 1, 2))],
+    "short": [(0, 1)],
+    "add": [("g", 2, 0, 2, (0,))],
+}
+TAIL_PLAN = {
+    "banks": [[(1, 0), (1, 1), (1, 2), (2, 1)], [(2, 0), (2, 2)]],
+    "stage": {0: (0, 1, 2)},
+    "mul": [("g", 0, 0, (0, 1, 2)), ("v", 1, 1, (0, 1, 2)), ("v", 1, 2, (1,)), ("v", 2, 2, (0, 2))],
+    "short": [],
+    "add": [],
+}
 
 OFF = {
+    "w_turn": (-18, 0, 3),
+    "w_quant": (-18, 0, 3),
+    "rel_mat": (-18, 0, 1),
     "pe_mxq": (-10, 3, 32),
     "pe_mxk": (-10, 3, 32),
     "s_q": (-10, 3, 32),
@@ -83,7 +115,7 @@ OFF = {
     "pe_mxv": (-9, 3, 32),
     "s_v": (-9, 3, 32),
     "pe_qrel": (-6, 3, 32),
-    "s_qr": (-6, 3, 32),
+    "s_qr": (-5, 3, 32),
     "pe_sh0": (22, 12, 8),
     "s_sh0": (22, 12, 8),
     "pe_sh2": (23, 12, 8),
@@ -99,26 +131,31 @@ OFF = {
     "pe_eend": (7, 4, 24),
     "s_esb": (7, 4, 24),
     "v_qk": (0, 1, 96),
+    "g_eadd": (0, 1, 96),
     "av": (24, 1, 96),
     "s_rg0": (-16, 3, 32),
     "v_quant": (-13, 3, 32),
     "v_max": (16, 12, 8),
     "v_sub": (17, 12, 8),
-    "s_exp": (18, 12, 8),
+    "s_exp": (17, 12, 8),
     "v_sum": (19, 12, 8),
+    "g_sum": (19, 12, 8),
     "v_mul": (20, 12, 8),
     "s_tout": (21, 12, 8),
     "pe_asteps0": (27, 3, 32),
     "pe_asteps1": (28, 3, 32),
     "pe_asteps2": (29, 3, 32),
     "s_av": (24, 1, 96),
+    "av_add": (24, 1, 96),
+    "av_vadd": (25, 1, 96),
 }
 ORDER = (
+    "w_turn", "w_quant", "rel_mat",
     "pe_qshift", "pe_mxq", "pe_mxk", "s_q", "g_qlo", "s_k", "pe_mxv", "s_v",
     "pe_qrel", "s_qr", "pe_sh0", "s_sh0", "pe_sh2", "s_sh2", "pe_sh1", "pe_sh2t",
     "pe_asteps1", "pe_asteps2", "pe_aend", "s_osb", "pe_ebegin", "pe_esteps", "pe_eend", "s_esb",
-    "pe_abegin", "pe_asteps0", "v_qk", "av", "s_av", "s_rg0", "s_rg1", "s_rg2",
-    "s_rg3", "v_quant", "v_max", "v_sub", "s_exp", "v_sum", "v_mul", "s_tout",
+    "pe_abegin", "pe_asteps0", "v_qk", "g_eadd", "av", "s_av", "av_add", "av_vadd", "s_rg0",
+    "v_quant", "v_max", "v_sub", "s_exp", "g_sum", "v_sum", "v_mul", "s_tout",
 )
 
 FLOPS = 2 * 3 * 128 * 512 * H * W + 2 * 2 * WIN * 128 * H * W
@@ -138,6 +175,7 @@ def ring_runs(first, count, ring):
 def tile_mutliheadattention2d_kernel(tc, x, Wq, Wk, Wv, rel_t, rel_f, out_0, out_1):
     nc = tc.nc
     with ExitStack() as ctx:
+        ctx.enter_context(tc.manual_schedule())
         const = ctx.enter_context(tc.tile_pool(name="const", bufs=1))
         rawp = ctx.enter_context(tc.tile_pool(name="rawp", bufs=RAW_BUFS))
         grpp = ctx.enter_context(tc.tile_pool(name="grpp", bufs=2))
@@ -146,12 +184,13 @@ def tile_mutliheadattention2d_kernel(tc, x, Wq, Wk, Wv, rel_t, rel_f, out_0, out
         qrp = ctx.enter_context(tc.tile_pool(name="qrp", bufs=2))
         esp = ctx.enter_context(tc.tile_pool(name="esp", bufs=2))
         shp = ctx.enter_context(tc.tile_pool(name="shp", bufs=4))
-        pvp = ctx.enter_context(tc.tile_pool(name="pvp", bufs=6))
+        pvp = ctx.enter_context(tc.tile_pool(name="pvp", bufs=1))
         outp = ctx.enter_context(tc.tile_pool(name="outp", bufs=OUT_BUFS))
         attp = ctx.enter_context(tc.tile_pool(name="attp", bufs=1))
         smallp = ctx.enter_context(tc.tile_pool(name="smallp", bufs=2))
+        foldp = ctx.enter_context(tc.tile_pool(name="foldp", bufs=1))
         redp = ctx.enter_context(tc.tile_pool(name="redp", bufs=2))
-        halfp = ctx.enter_context(tc.tile_pool(name="halfp", bufs=3))
+        halfp = ctx.enter_context(tc.tile_pool(name="halfp", bufs=HALF_BUFS))
         psum = ctx.enter_context(tc.psum_pool(name="psum", bufs=1))
 
         xv = x.rearrange("b (p j) h w -> p (b j) (h w)", j=4)
@@ -167,14 +206,22 @@ def tile_mutliheadattention2d_kernel(tc, x, Wq, Wk, Wv, rel_t, rel_f, out_0, out
             raw[q] = t_raw
 
         w_raw = pp.tile([P, 3, 512], BF16, name="w_raw", tag="big", align_bytes=64)
-        for idx, wsrc in enumerate((Wq, Wk, Wv)):
-            nc.sync.dma_start(out=w_raw[:, idx, :], in_=wsrc)
-        load(0)
         rel_sb = const.tile([P, 3], BF16, name="rel_sb")
-        nc.sync.dma_start(out=rel_sb[0:64, :], in_=rel_t)
-        nc.sync.dma_start(out=rel_sb[64:128, :], in_=rel_f)
-        for q in range(1, RAW_BUFS):
-            load(q)
+
+        def load_w(idx):
+            nc.sync.dma_start(out=w_raw[:, idx, :], in_=(Wq, Wk, Wv)[idx])
+
+        def load_rel():
+            nc.sync.dma_start(out=rel_sb[0:64, :], in_=rel_t)
+            nc.sync.dma_start(out=rel_sb[64:128, :], in_=rel_f)
+
+        for item in LOADS:
+            if item == "rel":
+                load_rel()
+            elif item[0] == "w":
+                load_w(int(item[1]))
+            else:
+                load(int(item[1]))
 
         ident_f = const.tile([P, P], F32, name="ident_f")
         masks.make_identity(nc, ident_f[:])
@@ -192,22 +239,8 @@ def tile_mutliheadattention2d_kernel(tc, x, Wq, Wk, Wv, rel_t, rel_f, out_0, out
                               in_=ident_f[:].rearrange("p (g c) -> p c g", c=CG))
         gmask = const.tile([P, NG], F32, name="gmask")
         nc.vector.tensor_reduce(out=gmask[:], in_=ident_f[:].rearrange("p (c g) -> p g c", g=NG), axis=AX.X, op=ALU.add)
-        r9 = const.tile([P, WIN], F32, name="r9")
-        nc.vector.tensor_copy(out=r9[0:64, :].rearrange("p (i j) -> p i j", j=3),
-                              in_=rel_sb[0:64, :].unsqueeze(2).to_broadcast([64, 3, 3]))
-        nc.vector.tensor_copy(out=r9[64:128, :].rearrange("p (i j) -> p i j", j=3),
-                              in_=rel_sb[64:128, :].unsqueeze(1).to_broadcast([64, 3, 3]))
-        r9_ps = psum.tile([P, WIN], F32, name="r9_ps", tag="mx", bufs=MX_BUFS) if AUX_TAG == "mx" else psum.tile([P, WIN], F32, name="r9_ps", tag="aux")
-        nc.tensor.matmul(out=r9_ps[:], lhsT=chperm[:], rhs=r9[:], start=True, stop=True)
-        r9p = const.tile([P, WIN], F32, name="r9p")
-        nc.vector.tensor_copy(out=r9p[:], in_=r9_ps[:])
-        rmat = const.tile([P, WIN, NG], F32, name="rmat")
-        nc.vector.tensor_tensor(out=rmat[:], in0=r9p[:].unsqueeze(2).to_broadcast([P, WIN, NG]),
-                                in1=gmask[:].unsqueeze(1).to_broadcast([P, WIN, NG]), op=ALU.mult)
-        rmat_b = const.tile([P, WIN * NG], BF16, name="rmat_b")
-        nc.vector.tensor_copy(out=rmat_b[:], in_=rmat[:].rearrange("p n g -> p (n g)"))
         atts = []
-        for idx in range(2):
+        for idx in range(ATT_BUFS):
             t_att = const.tile([P, WIN, W + 2], F32, name="att%d" % idx)
             nc.gpsimd.memset(t_att[:, :, 0:W + 2:W + 1], 0.0)
             atts.append(t_att)
@@ -222,21 +255,47 @@ def tile_mutliheadattention2d_kernel(tc, x, Wq, Wk, Wv, rel_t, rel_f, out_0, out
         w_codes = []
         w_scales = []
         for idx in range(3):
+            w_c = const.tile([P, P], U32, name="w_c%d" % idx, align_bytes=64)
+            w_s = const.tile([P, P], U8, name="w_s%d" % idx, align_bytes=64)
+            w_codes.append(w_c)
+            w_scales.append(w_s)
+        w_pss = {}
+
+        def w_turn(n):
+            idx = W_ORDER[n]
             nc.scalar.copy(out=w_de[:, idx, :, :], in_=w_raw[:, idx, :].rearrange("o (p t) -> o t p", t=4))
             w_ps = psum.tile([P, 4, P], BF16, name="w_ps", tag="mx", bufs=MX_BUFS)
             for t in range(4):
                 nc.tensor.transpose(w_ps[:, t, :], w_de[:, idx, t, :], ident_b[:])
+            w_pss[idx] = w_ps
+
+        def w_quant(n):
+            idx = W_ORDER[n]
+            w_ps = w_pss[idx]
             if idx < 2:
                 nc.vector.tensor_copy(out=w_grp[:, idx, :, :].rearrange("p (c g) t -> p c g t", g=NG),
                                       in_=w_ps[:].rearrange("p t (g c) -> p c g t", c=CG))
             else:
                 nc.vector.tensor_copy(out=w_grp[:, idx, :, :], in_=w_ps[:].rearrange("p t o -> p o t"))
-            w_c = const.tile([P, P], U32, name="w_c%d" % idx, align_bytes=64)
-            w_s = const.tile([P, P], U8, name="w_s%d" % idx, align_bytes=64)
-            nc.vector.quantize_mx(out=w_c[:].bitcast(FP8X4), scales=w_s[:],
+            nc.vector.quantize_mx(out=w_codes[idx][:].bitcast(FP8X4), scales=w_scales[idx][:],
                                   in_=w_grp[:, idx, :, :].rearrange("p o t -> p (o t)"))
-            w_codes.append(w_c)
-            w_scales.append(w_s)
+
+        r9 = const.tile([P, WIN], F32, name="r9")
+        r9p = const.tile([P, WIN], F32, name="r9p")
+        rmat = const.tile([P, WIN, NG], F32, name="rmat")
+        rmat_b = const.tile([P, WIN * NG], BF16, name="rmat_b")
+
+        def rel_mat(n):
+            nc.vector.tensor_copy(out=r9[0:64, :].rearrange("p (i j) -> p i j", j=3),
+                                  in_=rel_sb[0:64, :].unsqueeze(2).to_broadcast([64, 3, 3]))
+            nc.vector.tensor_copy(out=r9[64:128, :].rearrange("p (i j) -> p i j", j=3),
+                                  in_=rel_sb[64:128, :].unsqueeze(1).to_broadcast([64, 3, 3]))
+            r9_ps = psum.tile([P, WIN], F32, name="r9_ps", tag="mx", bufs=MX_BUFS) if AUX_TAG == "mx" else psum.tile([P, WIN], F32, name="r9_ps", tag="aux")
+            nc.tensor.matmul(out=r9_ps[:], lhsT=chperm[:], rhs=r9[:], start=True, stop=True)
+            nc.vector.tensor_copy(out=r9p[:], in_=r9_ps[:])
+            nc.vector.tensor_tensor(out=rmat[:], in0=r9p[:].unsqueeze(2).to_broadcast([P, WIN, NG]),
+                                    in1=gmask[:].unsqueeze(1).to_broadcast([P, WIN, NG]), op=ALU.mult)
+            nc.vector.tensor_copy(out=rmat_b[:], in_=rmat[:].rearrange("p n g -> p (n g)"))
 
         grp = {}
         xc = {}
@@ -260,9 +319,14 @@ def tile_mutliheadattention2d_kernel(tc, x, Wq, Wk, Wv, rel_t, rel_f, out_0, out
                 t_new = grpp.tile([P, PIX, 4], BF16, name="grp", align_bytes=64)
                 grp[q] = t_new
             cols = slice(first * W, (first + count) * W)
-            eng_copy = nc.vector.tensor_copy if q in V_RG else nc.scalar.copy
-            eng_copy(out=grp[q][:, cols, :].rearrange("p (c i) t -> p c t i", i=4),
-                     in_=raw[q][:, :, cols].rearrange("p t (c i) -> p c t i", i=4))
+            dst = grp[q][:, cols, :].rearrange("p (c i) t -> p c t i", i=4)
+            src = raw[q][:, :, cols].rearrange("p t (c i) -> p c t i", i=4)
+            if q in G_RG:
+                nc.gpsimd.tensor_scalar(out=dst, in0=src, scalar1=1.0, scalar2=0.0, op0=ALU.mult, op1=ALU.add)
+            elif q in V_RG:
+                nc.vector.tensor_copy(out=dst, in_=src)
+            else:
+                nc.scalar.copy(out=dst, in_=src)
             if first + count == R and q + RAW_BUFS < NQ:
                 load(q + RAW_BUFS, True)
 
@@ -409,12 +473,12 @@ def tile_mutliheadattention2d_kernel(tc, x, Wq, Wk, Wv, rel_t, rel_f, out_0, out
             j = JS[jj]
             t_e = psum.tile([P, 3, W], F32, name="e_ps", tag="eps")
             pending = []
-            for i in [i for i in range(3) if 3 * i + j not in RED_N] + [i for i in range(3) if 3 * i + j in RED_N]:
+            for i in E_ROWS:
                 n = 3 * i + j
                 if n in RED_N:
                     pending.append((t_e[:, i, :], ered[(m, n)][:], perms[j], True, False))
                 else:
-                    for c in range(CG // 2 if m < EADD_MB else CG):
+                    for c in range(CG // 2 if (m in EADD_MS and i in EADD_I) else CG):
                         pending.append((t_e[:, i, :], prod[(m, n)][:, c, :], perms[j], c == 0, False))
                 pending.append((t_e[:, i, :], qr9[m][:, n, :], ident_f, False, True))
             ework["todo"] = pending
@@ -451,64 +515,94 @@ def tile_mutliheadattention2d_kernel(tc, x, Wq, Wk, Wv, rel_t, rel_f, out_0, out
 
         def v_sub(m):
             flat = esb[m][:].rearrange("p i j w -> p (i j) w")
-            (nc.vector if SUB_ON_V else sm_eng).tensor_tensor(out=flat, in0=flat, in1=tops[m][:].unsqueeze(1).to_broadcast([P, WIN, W]), op=ALU.subtract)
+            for c in range(SM_SPLIT):
+                n = WIN // SM_SPLIT
+                (nc.vector if m >= SM_V_M else sm_eng).tensor_tensor(out=flat[:, c * n:(c + 1) * n, :], in0=flat[:, c * n:(c + 1) * n, :], in1=tops[m][:].unsqueeze(1).to_broadcast([P, n, W]), op=ALU.subtract)
 
         def s_exp(m):
             flat = esb[m][:].rearrange("p i j w -> p (i j) w")
             nc.scalar.activation(out=flat, in_=flat, func=ACT.Exp)
 
         def v_sum(m):
-            t_s = smallp.tile([P, W], F32, name="ssum")
-            nc.vector.tensor_reduce(out=t_s[:], in_=esb[m][:].rearrange("p i j w -> p w (i j)"), axis=AX.X, op=ALU.add)
+            if SUM_ON_G:
+                t_s = sums[m]
+            else:
+                t_s = smallp.tile([P, W], F32, name="ssum")
+                nc.vector.tensor_reduce(out=t_s[:], in_=esb[m][:].rearrange("p i j w -> p w (i j)"), axis=AX.X, op=ALU.add)
             t_r = smallp.tile([P, W], F32, name="rsum")
             nc.vector.reciprocal(out=t_r[:], in_=t_s[:])
             sums[m] = t_r
 
+        def g_sum(m):
+            if SUM_ON_G:
+                flat = esb[m][:].rearrange("p i j w -> p (i j) w")
+                t_f = foldp.tile([P, 4, W], F32, name="fold")
+                nc.gpsimd.tensor_tensor(out=t_f[:], in0=flat[:, 0:4, :], in1=flat[:, 4:8, :], op=ALU.add)
+                nc.gpsimd.tensor_tensor(out=t_f[:, 0:2, :], in0=t_f[:, 0:2, :], in1=t_f[:, 2:4, :], op=ALU.add)
+                nc.gpsimd.tensor_tensor(out=t_f[:, 0, :], in0=t_f[:, 0, :], in1=t_f[:, 1, :], op=ALU.add)
+                t_s = smallp.tile([P, W], F32, name="ssum")
+                nc.gpsimd.tensor_tensor(out=t_s[:], in0=t_f[:, 0, :], in1=flat[:, 8, :], op=ALU.add)
+                sums[m] = t_s
+
         def v_mul(m):
-            (nc.vector if MUL_ON_V else sm_eng).tensor_tensor(out=atts[m % 2][:, :, 1:W + 1], in0=esb[m][:].rearrange("p i j w -> p (i j) w"),
-                                 in1=sums[m][:].unsqueeze(1).to_broadcast([P, WIN, W]), op=ALU.mult)
+            flat = esb[m][:].rearrange("p i j w -> p (i j) w")
+            for c in range(SM_SPLIT):
+                n = WIN // SM_SPLIT
+                (nc.vector if m >= SM_V_M else sm_eng).tensor_tensor(out=atts[m % ATT_BUFS][:, c * n:(c + 1) * n, 1:W + 1], in0=flat[:, c * n:(c + 1) * n, :],
+                                     in1=sums[m][:].unsqueeze(1).to_broadcast([P, n, W]), op=ALU.mult)
 
         def s_tout(m):
             t_t = attp.tile([P, W, WIN], F32, name="t_out")
-            nc.scalar.copy(out=t_t[:], in_=atts[m % 2][:, :, 1:W + 1].rearrange("p n w -> p w n"))
+            nc.scalar.copy(out=t_t[:], in_=atts[m % ATT_BUFS][:, :, 1:W + 1].rearrange("p n w -> p w n"))
             for r in range(MBR):
                 {"sync": nc.sync, "scalar": nc.scalar, "gpsimd": nc.gpsimd}[T_QUEUE].dma_start(out=o1[:, m * MBR + r, :], in_=t_t[r * NG:(r + 1) * NG, :, :].rearrange("p w n -> p (w n)"))
 
         def tail(m):
             return m >= TAIL_MB
 
-        def on_vector(m, i, j):
-            return i == 1 or (i == 2 and (tail(m) or (V_EXTRA and j == 1)))
+        def plan(m):
+            return TAIL_PLAN if tail(m) else PLAN
+
+        def shv_banks(m):
+            return plan(m)["banks"]
+
+        def pe_shv(m, b):
+            banks = shv_banks(m)
+            if b >= len(banks):
+                return
+            tag = ("shv", "shw")[b]
+            if b == 1 and W_TAG == "qj":
+                t_ps = psum.tile([P, len(banks[b]), P], F32, name="sh_ps", tag="qj", bufs=QJ_BUFS)
+            else:
+                t_ps = psum.tile([P, len(banks[b]), P], F32, name="sh_ps", tag=tag)
+            for slot, (i, j) in enumerate(banks[b]):
+                nc.tensor.transpose(t_ps[:, slot, :], atts[m % ATT_BUFS][:, 3 * i + j, 2 - j:2 - j + W], ident_f[:])
+                sh[(m, i, j)] = (t_ps, slot)
 
         def pe_shift(m, i):
-            if i == 1:
-                t_ps = psum.tile([P, 4, P], F32, name="sh_ps", tag="shv")
-                todo = [(1, 0, 0), (1, 1, 1), (1, 2, 2)] + ([(2, 1, 3)] if ((V_EXTRA and not S_21) or tail(m)) else [])
-                sh[(m, "v")] = t_ps
-            elif i == 2 and tail(m):
-                t_ps = psum.tile([P, 2, P], F32, name="sh_ps", tag="qj", bufs=QJ_BUFS)
-                todo = [(2, 0, 0), (2, 2, 1)]
-                sh[(m, "t")] = t_ps
-            elif i == 2 and V_EXTRA and not S_21:
-                t_ps = aux_tile([P, 2, P], "sh_ps")
-                todo = [(2, 0, 0), (2, 2, 1)]
+            js = plan(m)["stage"].get(i, ())
+            if js:
+                t_ps = aux_tile([P, len(js), P], "sh_ps")
+                for slot, j in enumerate(js):
+                    nc.tensor.transpose(t_ps[:, slot, :], atts[m % ATT_BUFS][:, 3 * i + j, 2 - j:2 - j + W], ident_f[:])
                 sh[(m, i)] = t_ps
-            else:
-                t_ps = aux_tile([P, 3, P], "sh_ps")
-                todo = [(i, 0, 0), (i, 1, 1), (i, 2, 2)]
-                sh[(m, i)] = t_ps
-            for ii, j, slot in todo:
-                nc.tensor.transpose(t_ps[:, slot, :], atts[m % 2][:, 3 * ii + j, 2 - j:2 - j + W], ident_f[:])
 
         def s_shift(m, i):
-            t_sb = shp.tile([P, 3, P], F32, name="sh_sb")
-            n = sh[(m, i)].shape[1]
-            nc.scalar.copy(out=t_sb[:, 0:n, :], in_=sh[(m, i)][:])
-            sh[(m, i)] = t_sb
+            js = plan(m)["stage"].get(i, ())
+            if js:
+                t_sb = shp.tile([P, 3, P], F32, name="sh_sb")
+                nc.scalar.copy(out=t_sb[:, 0:len(js), :], in_=sh[(m, i)][:])
+                for slot, j in enumerate(js):
+                    sh[(m, i, j)] = (t_sb, slot)
 
-        def av_mul(eng, m, a, i, j0, nj, jstep, src, s0, sstep=1):
+        def av_mul(eng, m, a, i, js):
             h0 = m * MBR + a * R
             t_q = pv[(m, a, i)]
+            nj = len(js)
+            j0 = js[0]
+            jstep = js[1] - js[0] if nj > 1 else 1
+            src, s0 = sh[(m, i, j0)]
+            sstep = sh[(m, i, js[1])][1] - s0 if nj > 1 else 1
             lo = max(0, 1 - i - h0)
             hi = min(R, H + 1 - i - h0)
             for off, slot, cnt in ring_runs(h0 + lo + i - 1, hi - lo, RV):
@@ -520,85 +614,57 @@ def tile_mutliheadattention2d_kernel(tc, x, Wq, Wk, Wv, rel_t, rel_f, out_0, out
                     in1=src[:, s0:s0 + (nj - 1) * sstep + 1:sstep, x0:x0 + cnt * NG].unsqueeze(3).to_broadcast([P, nj, cnt * NG, CG]),
                     op=ALU.mult)
 
-        def summed(k):
-            return AV_ADD and 0 < k < NQ - 1 and not tail(k // QPM) and k % ADD_MOD == 0
+        def inner(k):
+            return 0 < k < NQ - 1
 
         def av(idx):
             k, s = divmod(idx, 3)
             m, a = divmod(k, QPM)
             if s == 0:
                 for i in range(3):
-                    t_new = pvp.tile([P, 3, R, P], F32, name="pv")
+                    t_new = pvp.tile([P, 3, R, P], F32, name="pv%d" % i, tag="pv%d" % i, bufs=PV_BUFS[i])
                     pv[(m, a, i)] = t_new
-            if s == G_WHEN[0]:
-                if S_00 and not tail(m):
-                    av_mul(nc.gpsimd, m, a, 0, 2, 1, 1, sh[(m, 0)], 2)
-                elif S_01 and not tail(m):
-                    av_mul(nc.gpsimd, m, a, 0, 0, 2, 2, sh[(m, 0)], 0, 2)
-                else:
-                    av_mul(nc.gpsimd, m, a, 0, 0, 3, 1, sh[(m, 0)], 0)
-            if s == V_WHEN[0]:
-                av_mul(nc.vector, m, a, 1, 0, 3, 1, sh[(m, "v")], 0)
-            if tail(m):
-                if s == V_WHEN[1]:
-                    av_mul(nc.vector, m, a, 2, 1, 1, 1, sh[(m, "v")], 3)
-                if s == V_WHEN[2]:
-                    av_mul(nc.vector, m, a, 2, 0, 2, 2, sh[(m, "t")], 0)
-            elif V_EXTRA:
-                if s == V_WHEN[1] and not S_21:
-                    av_mul(nc.vector, m, a, 2, 1, 1, 1, sh[(m, "v")], 3)
-                if s == G_WHEN[2]:
-                    av_mul(nc.gpsimd, m, a, 2, 0, 2, 2, sh[(m, 2)], 0, 2 if S_21 else 1)
-            elif s == G_WHEN[2]:
-                av_mul(nc.gpsimd, m, a, 2, 0, 3, 1, sh[(m, 2)], 0)
-            if s == ADD_WHEN and summed(k):
-                step = 2 if (V_EXTRA and not S_00) else 1
-                nc.gpsimd.tensor_tensor(out=pv[(m, a, 0)][:, 0:3:step], in0=pv[(m, a, 0)][:, 0:3:step], in1=pv[(m, a, 2)][:, 0:3:step], op=ALU.add)
+            for eng, step, i, js in plan(m)["mul"]:
+                if step == s:
+                    for part in (([(j,) for j in js]) if (eng == "g" and G_SPLIT) else [js]):
+                        av_mul(nc.gpsimd if eng == "g" else nc.vector, m, a, i, part)
+
+        def av_add(idx):
+            k, s = divmod(idx, 3)
+            m, a = divmod(k, QPM)
+            if inner(k):
+                for eng, step, i, i2, js in plan(m)["add"]:
+                    for part in ([(j,) for j in js] if G_SPLIT else [js]) if (eng == "g" and step == s) else ():
+                        jj = slice(part[0], part[-1] + 1, part[1] - part[0] if len(part) > 1 else 1)
+                        (nc.gpsimd if eng == "g" else nc.vector).tensor_tensor(out=pv[(m, a, i)][:, jj], in0=pv[(m, a, i)][:, jj], in1=pv[(m, a, i2)][:, jj], op=ALU.add)
+
+        def av_vadd(idx):
+            k, s = divmod(idx, 3)
+            m, a = divmod(k, QPM)
+            if inner(k):
+                for eng, step, i, i2, js in plan(m)["add"]:
+                    if eng == "v" and step == s:
+                        jj = slice(js[0], js[-1] + 1, js[1] - js[0] if len(js) > 1 else 1)
+                        nc.vector.tensor_tensor(out=pv[(m, a, i)][:, jj], in0=pv[(m, a, i)][:, jj], in1=pv[(m, a, i2)][:, jj], op=ALU.add)
 
         def s_av(idx):
             k, s = divmod(idx, 3)
             m, a = divmod(k, QPM)
             h0 = m * MBR + a * R
-            if S_01 and not tail(m):
+            for i, j in plan(m)["short"]:
+                src, sl = sh[(m, i, j)]
                 for r in S_ROWS[s]:
-                    if h0 + r - 1 >= 0:
-                        slot = (h0 + r - 1) % RV
-                        for j in ((0, 1) if S_00 else (1,)):
-                            for g in range(NG):
-                                x = (a * R + r) * NG + g
-                                nc.scalar.activation(out=pv[(m, a, 0)][:, j, r, g * CG:(g + 1) * CG], in_=v_ring[:, slot, g * CG:(g + 1) * CG],
-                                                     func=ACT.Copy, scale=sh[(m, 0)][:, j, x:x + 1])
-
-        def s_av2(idx):
-            k, s = divmod(idx, 3)
-            m, a = divmod(k, QPM)
-            h0 = m * MBR + a * R
-            if S_21 and not tail(m):
-                for r in S_ROWS[s]:
-                    if h0 + r + 1 < H:
-                        slot = (h0 + r + 1) % RV
+                    if 0 <= h0 + r + i - 1 < H:
+                        slot = (h0 + r + i - 1) % RV
                         for g in range(NG):
                             x = (a * R + r) * NG + g
-                            nc.scalar.activation(out=pv[(m, a, 2)][:, 1, r, g * CG:(g + 1) * CG], in_=v_ring[:, slot, g * CG:(g + 1) * CG],
-                                                 func=ACT.Copy, scale=sh[(m, 2)][:, 1, x:x + 1])
-
-        def vsummed(k):
-            return V_ADD and 0 < k < NQ - 1
-
-        def tsummed(k):
-            return VT_ADD and tail(k // QPM) and k < NQ - 1
-
-        def v_add(k):
-            m, a = divmod(k, QPM)
-            if tsummed(k):
-                nc.vector.tensor_tensor(out=pv[(m, a, 1)][:], in0=pv[(m, a, 1)][:], in1=pv[(m, a, 2)][:], op=ALU.add)
-            if vsummed(k):
-                nc.vector.tensor_tensor(out=pv[(m, a, 1)][:], in0=pv[(m, a, 1)][:], in1=pv[(m, a, 0)][:], op=ALU.add)
+                            nc.scalar.activation(out=pv[(m, a, i)][:, j, r, g * CG:(g + 1) * CG], in_=v_ring[:, slot, g * CG:(g + 1) * CG],
+                                                 func=ACT.Copy, scale=src[:, sl, x:x + 1])
 
         def g_eadd(u):
             m, j, a = decode(u)
             cols = slice(a * R * NG, (a + 1) * R * NG)
-            for i in range(3):
+            for i in EADD_I if m in EADD_MS else ():
                 t_p = prod[(m, 3 * i + j)]
                 nc.gpsimd.tensor_tensor(out=t_p[:, 0:CG // 2, cols], in0=t_p[:, 0:CG // 2, cols], in1=t_p[:, CG // 2:CG, cols], op=ALU.add)
 
@@ -616,7 +682,8 @@ def tile_mutliheadattention2d_kernel(tc, x, Wq, Wk, Wv, rel_t, rel_f, out_0, out
                     q_pass(NQ - 1, t_o)
             pending = []
             for r in range(R):
-                terms = [(i, j) for i in range(3) for j in range(3) if 0 <= h0 + r + i - 1 < H and not (i == 2 and summed(k) and not (V_EXTRA and not S_00 and j == 1)) and not (i == 0 and vsummed(k)) and not (i == 2 and tsummed(k))]
+                gone = [(i2, j) for eng, step, i, i2, js in plan(m)["add"] for j in js] if inner(k) else []
+                terms = [(i, j) for i in A_ROWS for j in range(3) if 0 <= h0 + r + i - 1 < H and (i, j) not in gone]
                 for idx, (i, j) in enumerate(terms):
                     pending.append((t_o[:, r, :], pv[(m, a, i)][:, j, r, :], perms[j], idx == 0, idx == len(terms) - 1))
             awork["todo"] = pending
@@ -644,26 +711,26 @@ def tile_mutliheadattention2d_kernel(tc, x, Wq, Wk, Wv, rel_t, rel_f, out_0, out
             return lambda m: fn(m) if cond(m) else None
 
         calls = {
+            "w_turn": w_turn, "w_quant": w_quant, "rel_mat": rel_mat,
             "pe_mxq": pe_mxq, "pe_mxk": pe_mxk, "pe_mxv": pe_mxv, "s_q": s_q, "g_qlo": g_qlo, "s_k": s_k, "s_v": s_v,
             "pe_qrel": pe_qrel, "s_qr": s_qr,
             "pe_sh0": lambda m: pe_shift(m, 0), "s_sh0": lambda m: s_shift(m, 0),
-            "pe_sh2": only(lambda m: not tail(m), lambda m: pe_shift(m, 2)),
-            "s_sh2": only(lambda m: not tail(m), lambda m: s_shift(m, 2)),
-            "pe_sh1": lambda m: pe_shift(m, 1), "pe_sh2t": only(tail, lambda m: pe_shift(m, 2)),
-            "g_eadd": g_eadd, "s_av": s_av, "s_av2": s_av2, "v_qlo": v_qlo, "v_red": v_red, "v_add": v_add, "pe_ebegin_h": pe_ebegin,
+            "pe_sh2": lambda m: pe_shift(m, 2), "s_sh2": lambda m: s_shift(m, 2),
+            "pe_sh1": lambda m: pe_shv(m, 0), "pe_sh2t": lambda m: pe_shv(m, 1), "av_add": av_add, "av_vadd": av_vadd,
+            "g_eadd": g_eadd, "s_av": s_av, "v_qlo": v_qlo, "v_red": v_red,
             "pe_abegin": pe_abegin, "pe_asteps": pe_asteps, "pe_asteps0": pe_asteps, "pe_asteps1": pe_asteps, "pe_asteps2": pe_asteps, "pe_aend": pe_aend, "s_osb": s_osb,
-            "pe_qshift": pe_qshift, "pe_ebegin": lambda idx: pe_ebegin(idx + 3 * EADD_MB), "pe_esteps": pe_esteps, "pe_eend": pe_eend, "s_esb": s_esb,
+            "pe_qshift": pe_qshift, "pe_ebegin": pe_ebegin, "pe_esteps": pe_esteps, "pe_eend": pe_eend, "s_esb": s_esb,
             "v_qk": v_qk, "av": av, "v_quant": v_quant, "v_quant1": lambda q: v_quant(q, 1),
             "s_rg0": lambda q: s_rg(q, 0), "s_rg1": lambda q: s_rg(q, 1), "s_rg2": lambda q: s_rg(q, 2), "s_rg3": lambda q: s_rg(q, 3),
-            "pe_warm": pe_warm, "v_max": v_max, "v_sub": v_sub, "s_exp": s_exp, "v_sum": v_sum, "v_mul": v_mul, "s_tout": s_tout,
+            "pe_warm": pe_warm, "v_max": v_max, "v_sub": v_sub, "s_exp": s_exp, "v_sum": v_sum, "g_sum": g_sum, "v_mul": v_mul, "s_tout": s_tout,
         }
-        first_u = min([OFF[name][0] for name in ORDER if name in OFF])
-        last_u = max([OFF[name][0] + OFF[name][1] * (OFF[name][2] - 1) for name in ORDER if name in OFF])
-        with tc.manual_schedule():
-            for u in range(first_u, last_u + 1):
-                for name in ORDER:
-                    if name in OFF:
-                        base, period, count = OFF[name]
-                        idx, rem = divmod(u - base, period)
-                        if rem == 0 and 0 <= idx < count:
-                            calls[name](idx)
+        due = {}
+        for name in ORDER:
+            base, period, count = OFF[name]
+            for idx in range(count):
+                head = HEAD.get(name, ())
+                u = head[idx] if idx < len(head) else base + period * idx
+                due.setdefault(u, []).append((name, idx))
+        for u in sorted(due):
+            for name, idx in due[u]:
+                calls[name](idx)

from contextlib import ExitStack

import concourse.masks as masks
import concourse.mybir as mybir

F32 = mybir.dt.float32
BF16 = mybir.dt.bfloat16
U32 = mybir.dt.uint32
U8 = mybir.dt.uint8
FP8X4 = mybir.dt.float8_e4m3fn_x4
ALU = mybir.AluOpType
ACT = mybir.ActivationFunctionType
AX = mybir.AxisListType

P = 128
H = 128
W = 128
NG = 8
CG = 16
WIN = 9
R = 4
NQ = H // R
PIX = R * W
MBR = 16
QPM = MBR // R
NMB = H // MBR
SUB = 3 * QPM
RQ = 32
RK = 36
RV = 52
RAW_BUFS = 4
LAG = 24
ESTEP = 13
ASTEP = 12
TAIL_MB = 6
QJ_BUFS = 2
MX_BUFS = 3
AUX_TAG = "mx"
LOAD_ON_SCALAR = False
SM_ON_G = True
MUL_ON_V = False
SUB_ON_V = False
G_PIECES = 1
RG_PIECES = ((0, 4),)
WARM_N = 1
WARM_K0 = NQ
MX_PRE = 0
PRE_Q = 0
PRE_V = 0
V_SPLIT = False
AV_ADD = True
VT_ADD = False
S_01 = True
S_00 = False
S_21 = False
S_ROWS = ((0, 1), (2,), (3,))
ADD_MOD = 1
V_EXTRA = True
V_WHEN = (1, 1, 2)
EADD_MS = ()
E_ROWS = (0, 1, 2)
EADD_I = (0, 1, 2)
RED_N = ()
V_ADD = False
OPS_MX_K0 = 22
ADD_WHEN = 2
G_WHEN = (0, 1, 2)
QN_PIECES = 1
QR_F32 = False
V_RG = (2, 3, 4,)
OUT_BUFS = 2
COD_BUFS = 5
O_QUEUE = "sync"
T_QUEUE = "sync"
JS = (1, 0, 2)
QPIX = True
QR_COLS = 72
SUM_ON_G = False
G_SPLIT = False
SM_SPLIT = 3
SM_V_M = 8
PV_BUFS = (2, 2, 2)
ATT_BUFS = 2
HALF_BUFS = 3
G_RG = ()
LOADS = ("w0", "w1", "w2", "x0", "rel", "x1", "x2", "x3")
W_ORDER = (0, 1, 2)
HEAD = {}
W_TAG = "qj"
A_ROWS = (0, 1, 2)
PLAN = {
    "banks": [[(1, 0), (1, 1), (1, 2)]],
    "stage": {0: (0, 1, 2), 2: (0, 1, 2)},
    "mul": [("g", 0, 0, (0, 2)), ("v", 1, 1, (0, 1, 2)), ("g", 2, 2, (0, 1, 2))],
    "short": [(0, 1)],
    "add": [("g", 2, 0, 2, (0,))],
}
TAIL_PLAN = {
    "banks": [[(1, 0), (1, 1), (1, 2), (2, 1)], [(2, 0), (2, 2)]],
    "stage": {0: (0, 1, 2)},
    "mul": [("g", 0, 0, (0, 1, 2)), ("v", 1, 1, (0, 1, 2)), ("v", 1, 2, (1,)), ("v", 2, 2, (0, 2))],
    "short": [],
    "add": [],
}

OFF = {
    "w_turn": (-18, 0, 3),
    "w_quant": (-18, 0, 3),
    "rel_mat": (-18, 0, 1),
    "pe_mxq": (-10, 3, 32),
    "pe_mxk": (-10, 3, 32),
    "s_q": (-10, 3, 32),
    "g_qlo": (-9, 3, 32),
    "s_k": (-10, 3, 32),
    "pe_mxv": (-9, 3, 32),
    "s_v": (-9, 3, 32),
    "pe_qrel": (-6, 3, 32),
    "s_qr": (-5, 3, 32),
    "pe_sh0": (22, 12, 8),
    "s_sh0": (22, 12, 8),
    "pe_sh2": (23, 12, 8),
    "s_sh2": (23, 12, 8),
    "pe_sh1": (23, 12, 8),
    "pe_sh2t": (24, 12, 8),
    "pe_abegin": (27, 3, 32),
    "pe_aend": (29, 3, 32),
    "s_osb": (29, 3, 32),
    "pe_qshift": (-1, 1, 96),
    "pe_ebegin": (4, 4, 24),
    "pe_esteps": (4, 1, 96),
    "pe_eend": (7, 4, 24),
    "s_esb": (7, 4, 24),
    "v_qk": (0, 1, 96),
    "g_eadd": (0, 1, 96),
    "av": (24, 1, 96),
    "s_rg0": (-16, 3, 32),
    "v_quant": (-13, 3, 32),
    "v_max": (16, 12, 8),
    "v_sub": (17, 12, 8),
    "s_exp": (17, 12, 8),
    "v_sum": (19, 12, 8),
    "g_sum": (19, 12, 8),
    "v_mul": (20, 12, 8),
    "s_tout": (21, 12, 8),
    "pe_asteps0": (27, 3, 32),
    "pe_asteps1": (28, 3, 32),
    "pe_asteps2": (29, 3, 32),
    "s_av": (24, 1, 96),
    "av_add": (24, 1, 96),
    "av_vadd": (25, 1, 96),
}
ORDER = (
    "w_turn", "w_quant", "rel_mat",
    "pe_qshift", "pe_mxq", "pe_mxk", "s_q", "g_qlo", "s_k", "pe_mxv", "s_v",
    "pe_qrel", "s_qr", "pe_sh0", "s_sh0", "pe_sh2", "s_sh2", "pe_sh1", "pe_sh2t",
    "pe_asteps1", "pe_asteps2", "pe_aend", "s_osb", "pe_ebegin", "pe_esteps", "pe_eend", "s_esb",
    "pe_abegin", "pe_asteps0", "v_qk", "g_eadd", "av", "s_av", "av_add", "av_vadd", "s_rg0",
    "v_quant", "v_max", "v_sub", "s_exp", "g_sum", "v_sum", "v_mul", "s_tout",
)

FLOPS = 2 * 3 * 128 * 512 * H * W + 2 * 2 * WIN * 128 * H * W


def ring_runs(first, count, ring):
    runs = []
    done = 0
    while done < count:
        slot = (first + done) % ring
        n = min(count - done, ring - slot)
        runs.append((done, slot, n))
        done += n
    return runs


def tile_mutliheadattention2d_kernel(tc, x, Wq, Wk, Wv, rel_t, rel_f, out_0, out_1):
    nc = tc.nc
    with ExitStack() as ctx:
        ctx.enter_context(tc.manual_schedule())
        const = ctx.enter_context(tc.tile_pool(name="const", bufs=1))
        rawp = ctx.enter_context(tc.tile_pool(name="rawp", bufs=RAW_BUFS))
        grpp = ctx.enter_context(tc.tile_pool(name="grpp", bufs=2))
        codp = ctx.enter_context(tc.tile_pool(name="codp", bufs=COD_BUFS))
        pp = ctx.enter_context(tc.tile_pool(name="pp", bufs=6))
        qrp = ctx.enter_context(tc.tile_pool(name="qrp", bufs=2))
        esp = ctx.enter_context(tc.tile_pool(name="esp", bufs=2))
        shp = ctx.enter_context(tc.tile_pool(name="shp", bufs=4))
        pvp = ctx.enter_context(tc.tile_pool(name="pvp", bufs=1))
        outp = ctx.enter_context(tc.tile_pool(name="outp", bufs=OUT_BUFS))
        attp = ctx.enter_context(tc.tile_pool(name="attp", bufs=1))
        smallp = ctx.enter_context(tc.tile_pool(name="smallp", bufs=2))
        foldp = ctx.enter_context(tc.tile_pool(name="foldp", bufs=1))
        redp = ctx.enter_context(tc.tile_pool(name="redp", bufs=2))
        halfp = ctx.enter_context(tc.tile_pool(name="halfp", bufs=HALF_BUFS))
        psum = ctx.enter_context(tc.psum_pool(name="psum", bufs=1))

        xv = x.rearrange("b (p j) h w -> p (b j) (h w)", j=4)
        o0 = out_0.rearrange("b o h w -> (b o) (h w)")
        o1 = out_1.rearrange("b g h w n -> (b g) h (w n)")

        raw = {}

        def load(q, late=False):
            t_raw = rawp.tile([P, 4, PIX], BF16, name="raw")
            queue = nc.scalar if (late and LOAD_ON_SCALAR) else nc.sync
            queue.dma_start(out=t_raw[:], in_=xv[:, :, q * PIX:(q + 1) * PIX])
            raw[q] = t_raw

        w_raw = pp.tile([P, 3, 512], BF16, name="w_raw", tag="big", align_bytes=64)
        rel_sb = const.tile([P, 3], BF16, name="rel_sb")

        def load_w(idx):
            nc.sync.dma_start(out=w_raw[:, idx, :], in_=(Wq, Wk, Wv)[idx])

        def load_rel():
            nc.sync.dma_start(out=rel_sb[0:64, :], in_=rel_t)
            nc.sync.dma_start(out=rel_sb[64:128, :], in_=rel_f)

        for item in LOADS:
            if item == "rel":
                load_rel()
            elif item[0] == "w":
                load_w(int(item[1]))
            else:
                load(int(item[1]))

        ident_f = const.tile([P, P], F32, name="ident_f")
        masks.make_identity(nc, ident_f[:])
        ident_b = const.tile([P, P], BF16, name="ident_b")
        masks.make_identity(nc, ident_b[:])
        perm0 = const.tile([P, P], F32, name="perm0")
        perm2 = const.tile([P, P], F32, name="perm2")
        nc.vector.tensor_copy(out=perm0[:, 1:P], in_=ident_f[:, 0:P - 1])
        nc.vector.tensor_copy(out=perm0[:, 0:1], in_=ident_f[:, P - 1:P])
        nc.vector.tensor_copy(out=perm2[:, 0:P - 1], in_=ident_f[:, 1:P])
        nc.vector.tensor_copy(out=perm2[:, P - 1:P], in_=ident_f[:, 0:1])
        perms = (perm0, ident_f, perm2)
        chperm = const.tile([P, P], F32, name="chperm")
        nc.vector.tensor_copy(out=chperm[:].rearrange("p (c g) -> p c g", g=NG),
                              in_=ident_f[:].rearrange("p (g c) -> p c g", c=CG))
        gmask = const.tile([P, NG], F32, name="gmask")
        nc.vector.tensor_reduce(out=gmask[:], in_=ident_f[:].rearrange("p (c g) -> p g c", g=NG), axis=AX.X, op=ALU.add)
        atts = []
        for idx in range(ATT_BUFS):
            t_att = const.tile([P, WIN, W + 2], F32, name="att%d" % idx)
            nc.gpsimd.memset(t_att[:, :, 0:W + 2:W + 1], 0.0)
            atts.append(t_att)
        q_ring = const.tile([P, RQ, W + 2], F32, name="q_ring")
        nc.gpsimd.memset(q_ring[:, :, 0:W + 2:W + 1], 0.0)
        k_ring = const.tile([P, RK, P], F32, name="k_ring")
        nc.gpsimd.memset(k_ring[:, RK - 1, :], 0.0)
        v_ring = const.tile([P, RV, P], F32, name="v_ring")

        w_de = pp.tile([P, 3, 4, P], BF16, name="w_de", tag="big", align_bytes=64)
        w_grp = pp.tile([P, 3, P, 4], BF16, name="w_grp", tag="big", align_bytes=64)
        w_codes = []
        w_scales = []
        for idx in range(3):
            w_c = const.tile([P, P], U32, name="w_c%d" % idx, align_bytes=64)
            w_s = const.tile([P, P], U8, name="w_s%d" % idx, align_bytes=64)
            w_codes.append(w_c)
            w_scales.append(w_s)
        w_pss = {}

        def w_turn(n):
            idx = W_ORDER[n]
            nc.scalar.copy(out=w_de[:, idx, :, :], in_=w_raw[:, idx, :].rearrange("o (p t) -> o t p", t=4))
            w_ps = psum.tile([P, 4, P], BF16, name="w_ps", tag="mx", bufs=MX_BUFS)
            for t in range(4):
                nc.tensor.transpose(w_ps[:, t, :], w_de[:, idx, t, :], ident_b[:])
            w_pss[idx] = w_ps

        def w_quant(n):
            idx = W_ORDER[n]
            w_ps = w_pss[idx]
            if idx < 2:
                nc.vector.tensor_copy(out=w_grp[:, idx, :, :].rearrange("p (c g) t -> p c g t", g=NG),
                                      in_=w_ps[:].rearrange("p t (g c) -> p c g t", c=CG))
            else:
                nc.vector.tensor_copy(out=w_grp[:, idx, :, :], in_=w_ps[:].rearrange("p t o -> p o t"))
            nc.vector.quantize_mx(out=w_codes[idx][:].bitcast(FP8X4), scales=w_scales[idx][:],
                                  in_=w_grp[:, idx, :, :].rearrange("p o t -> p (o t)"))

        r9 = const.tile([P, WIN], F32, name="r9")
        r9p = const.tile([P, WIN], F32, name="r9p")
        rmat = const.tile([P, WIN, NG], F32, name="rmat")
        rmat_b = const.tile([P, WIN * NG], BF16, name="rmat_b")

        def rel_mat(n):
            nc.vector.tensor_copy(out=r9[0:64, :].rearrange("p (i j) -> p i j", j=3),
                                  in_=rel_sb[0:64, :].unsqueeze(2).to_broadcast([64, 3, 3]))
            nc.vector.tensor_copy(out=r9[64:128, :].rearrange("p (i j) -> p i j", j=3),
                                  in_=rel_sb[64:128, :].unsqueeze(1).to_broadcast([64, 3, 3]))
            r9_ps = psum.tile([P, WIN], F32, name="r9_ps", tag="mx", bufs=MX_BUFS) if AUX_TAG == "mx" else psum.tile([P, WIN], F32, name="r9_ps", tag="aux")
            nc.tensor.matmul(out=r9_ps[:], lhsT=chperm[:], rhs=r9[:], start=True, stop=True)
            nc.vector.tensor_copy(out=r9p[:], in_=r9_ps[:])
            nc.vector.tensor_tensor(out=rmat[:], in0=r9p[:].unsqueeze(2).to_broadcast([P, WIN, NG]),
                                    in1=gmask[:].unsqueeze(1).to_broadcast([P, WIN, NG]), op=ALU.mult)
            nc.vector.tensor_copy(out=rmat_b[:], in_=rmat[:].rearrange("p n g -> p (n g)"))

        grp = {}
        xc = {}
        xs = {}
        q_hi = {}
        q_lo = {}
        qr9 = {}
        qjt = {}
        prod = {}
        esb = {}
        tops = {}
        sums = {}
        sh = {}
        pv = {}

        ps = {}

        def s_rg(q, piece):
            first, count = RG_PIECES[piece]
            if first == 0:
                t_new = grpp.tile([P, PIX, 4], BF16, name="grp", align_bytes=64)
                grp[q] = t_new
            cols = slice(first * W, (first + count) * W)
            dst = grp[q][:, cols, :].rearrange("p (c i) t -> p c t i", i=4)
            src = raw[q][:, :, cols].rearrange("p t (c i) -> p c t i", i=4)
            if q in G_RG:
                nc.gpsimd.tensor_scalar(out=dst, in0=src, scalar1=1.0, scalar2=0.0, op0=ALU.mult, op1=ALU.add)
            elif q in V_RG:
                nc.vector.tensor_copy(out=dst, in_=src)
            else:
                nc.scalar.copy(out=dst, in_=src)
            if first + count == R and q + RAW_BUFS < NQ:
                load(q + RAW_BUFS, True)

        def v_quant(q, piece=0):
            if piece == 0:
                t_c = codp.tile([P, PIX], U32, name="xc", align_bytes=64)
                t_s = codp.tile([P, PIX], U8, name="xs", align_bytes=64)
                xc[q] = t_c
                xs[q] = t_s
            n = PIX // QN_PIECES
            cols = slice(piece * n, (piece + 1) * n)
            nc.vector.quantize_mx(out=xc[q][:, cols].bitcast(FP8X4), scales=xs[q][:, cols],
                                  in_=grp[q][:, cols, :].rearrange("p c t -> p (c t)"))

        def q_pass(q, t_ps):
            nc.tensor.matmul_mx(out=t_ps[:].rearrange("p r w -> p (r w)"), lhsT=w_codes[0][:].bitcast(FP8X4),
                                lhsT_scale=w_scales[0][:], rhs=xc[q][:].bitcast(FP8X4), rhs_scale=xs[q][:],
                                start=True, stop=True)

        def mx_pixel(q, widx, name, extra=0):
            t_ps = psum.tile([P, R, P], F32, name=name, tag="mx", bufs=MX_BUFS)
            for rep in range(MX_PRE + extra):
                q_pass(q, t_ps)
            for r in range(R):
                cols = slice(r * W, (r + 1) * W)
                nc.tensor.matmul_mx(out=t_ps[:, r, :], lhsT=xc[q][:, cols].bitcast(FP8X4), lhsT_scale=xs[q][:, cols],
                                    rhs=w_codes[widx][:].bitcast(FP8X4), rhs_scale=w_scales[widx][:], start=True, stop=True)
            return t_ps

        def pe_mxq(q):
            q_ps = psum.tile([P, R, W], F32, name="q_ps", tag="mx", bufs=MX_BUFS)
            for rep in range(MX_PRE + PRE_Q + 1):
                q_pass(q, q_ps)
            ps[("q", q)] = q_ps

        def pe_mxk(q):
            ps[("k", q)] = mx_pixel(q, 1, "k_ps")

        def pe_mxv(q):
            ps[("v", q)] = mx_pixel(q, 2, "v_ps", PRE_V)

        def s_q(q):
            qs = (q * R) % RQ
            nc.scalar.copy(out=q_ring[:, qs:qs + R, 1:W + 1], in_=ps[("q", q)][:])
            if not QR_F32:
                t_hi = halfp.tile([P, R, W], BF16, name="q_hi")
                nc.scalar.copy(out=t_hi[:], in_=ps[("q", q)][:])
                q_hi[q] = t_hi

        def g_qlo(q):
            qs = (q * R) % RQ
            t_lo = halfp.tile([P, R, W], BF16, name="q_lo")
            nc.gpsimd.tensor_tensor(out=t_lo[:], in0=q_ring[:, qs:qs + R, 1:W + 1], in1=q_hi[q][:], op=ALU.subtract)
            q_lo[q] = t_lo

        def v_qlo(q):
            t_lo = halfp.tile([P, R, W], BF16, name="q_lo")
            nc.vector.tensor_tensor(out=t_lo[:], in0=ps[("q", q)][:], in1=q_hi[q][:], op=ALU.subtract)
            q_lo[q] = t_lo

        def s_k(q):
            ks = (q * R) % RK
            nc.scalar.copy(out=k_ring[:, ks:ks + R, :], in_=ps[("k", q)][:])

        def s_v(q):
            vs = (q * R) % RV
            nc.scalar.copy(out=v_ring[:, vs:vs + R, :], in_=ps[("v", q)][:])

        def aux_tile(shape, name):
            if AUX_TAG == "mx":
                return psum.tile(shape, F32, name=name, tag="mx", bufs=MX_BUFS)
            return psum.tile(shape, F32, name=name, tag="aux")

        def pe_qrel(q):
            t_ps = aux_tile([P, R, WIN * NG], "qr_ps")
            qs = (q * R) % RQ
            for r in range(R):
                if QR_F32:
                    nc.tensor.matmul(out=t_ps[:, r, :], lhsT=q_ring[:, qs + r, 1:W + 1],
                                     rhs=rmat[:].rearrange("p n g -> p (n g)"), start=True, stop=True)
                else:
                    nc.tensor.matmul(out=t_ps[:, r, :], lhsT=q_hi[q][:, r, :], rhs=rmat_b[:], start=True, stop=False)
                    nc.tensor.matmul(out=t_ps[:, r, :], lhsT=q_lo[q][:, r, :], rhs=rmat_b[:], start=False, stop=True)
            ps[("qr", q)] = t_ps

        def s_qr(q):
            m, a = divmod(q, QPM)
            if a == 0:
                t_new = qrp.tile([P, WIN, P], F32, name="qr9")
                qr9[m] = t_new
            nc.scalar.copy(out=qr9[m][:, :, a * R * NG:(a + 1) * R * NG].rearrange("p n (r g) -> p n r g", g=NG),
                           in_=ps[("qr", q)][:].rearrange("p r (n g) -> p n r g", g=NG))

        def decode(u):
            m, rem = divmod(u, SUB)
            j, a = divmod(rem, QPM)
            return m, JS[j], a

        def pe_qshift(u):
            m, j, a = decode(u)
            qs = ((m * QPM + a) * R) % RQ
            t_ps = psum.tile([P, R, P], F32, name="qj", tag="qj", bufs=QJ_BUFS)
            q = m * QPM + a
            for r in range(R):
                if QPIX and j == 1:
                    cols = slice(r * W, (r + 1) * W)
                    nc.tensor.matmul_mx(out=t_ps[:, r, :], lhsT=xc[q][:, cols].bitcast(FP8X4), lhsT_scale=xs[q][:, cols],
                                        rhs=w_codes[0][:].bitcast(FP8X4), rhs_scale=w_scales[0][:], start=True, stop=True)
                else:
                    nc.tensor.transpose(t_ps[:, r, :], q_ring[:, qs + r, 2 - j:2 - j + W], ident_f[:])
            qjt[u] = t_ps

        def v_qk(u):
            m, j, a = decode(u)
            h0 = m * MBR + a * R
            if u == (NMB - 1) * SUB:
                nc.gpsimd.memset(k_ring[:, H % RK, :], 0.0)
            for i in range(3):
                n = 3 * i + j
                if a == 0:
                    t_new = pp.tile([P, CG, P], F32, name="prod", tag="big", align_bytes=64)
                    prod[(m, n)] = t_new
                t_p = prod[(m, n)]
                for off, slot, cnt in ring_runs(h0 + i - 1, R, RK):
                    c0 = (a * R + off) * NG
                    nc.vector.tensor_tensor(
                        out=t_p[:, :, c0:c0 + cnt * NG].rearrange("p c (r g) -> p c r g", g=NG),
                        in0=k_ring[:, slot:slot + cnt, :].rearrange("p r (c g) -> p c r g", g=NG),
                        in1=qjt[u][:, off:off + cnt, :].rearrange("p r (c g) -> p c r g", g=NG), op=ALU.mult)

        ework = {"todo": [], "pos": 0, "tile": None}
        ered = {}

        def v_red(f):
            m, jj = divmod(f, 3)
            j = JS[jj]
            for i in [i for i in range(3) if 3 * i + j in RED_N]:
                t_r = redp.tile([P, P], F32, name="ered")
                nc.vector.tensor_reduce(out=t_r[:], in_=prod[(m, 3 * i + j)][:].rearrange("p c x -> p x c"), axis=AX.X, op=ALU.add)
                ered[(m, 3 * i + j)] = t_r

        def pe_ebegin(f):
            m, jj = divmod(f, 3)
            j = JS[jj]
            t_e = psum.tile([P, 3, W], F32, name="e_ps", tag="eps")
            pending = []
            for i in E_ROWS:
                n = 3 * i + j
                if n in RED_N:
                    pending.append((t_e[:, i, :], ered[(m, n)][:], perms[j], True, False))
                else:
                    for c in range(CG // 2 if (m in EADD_MS and i in EADD_I) else CG):
                        pending.append((t_e[:, i, :], prod[(m, n)][:, c, :], perms[j], c == 0, False))
                pending.append((t_e[:, i, :], qr9[m][:, n, :], ident_f, False, True))
            ework["todo"] = pending
            ework["pos"] = 0
            ps[("e", f)] = t_e

        def work_step(work, count):
            todo = work["todo"]
            for step in range(work["pos"], min(work["pos"] + count, len(todo))):
                dst, lhs, perm, first, last = todo[step]
                nc.tensor.matmul(out=dst, lhsT=lhs, rhs=perm[:], start=first, stop=last, is_transpose=True)
            work["pos"] = min(work["pos"] + count, len(todo))

        def pe_esteps(idx):
            work_step(ework, ESTEP)

        def pe_eend(f):
            work_step(ework, len(ework["todo"]))

        def s_esb(f):
            m, jj = divmod(f, 3)
            j = JS[jj]
            if jj == 0:
                t_new = esp.tile([P, 3, 3, W], F32, name="esb")
                esb[m] = t_new
            nc.scalar.copy(out=esb[m][:, :, j, :], in_=ps[("e", f)][:])

        def v_max(m):
            t_m = smallp.tile([P, W], F32, name="mx")
            nc.vector.tensor_reduce(out=t_m[:], in_=esb[m][:].rearrange("p i j w -> p w (i j)"), axis=AX.X, op=ALU.max)
            tops[m] = t_m

        sm_eng = nc.gpsimd if SM_ON_G else nc.vector

        def v_sub(m):
            flat = esb[m][:].rearrange("p i j w -> p (i j) w")
            for c in range(SM_SPLIT):
                n = WIN // SM_SPLIT
                (nc.vector if m >= SM_V_M else sm_eng).tensor_tensor(out=flat[:, c * n:(c + 1) * n, :], in0=flat[:, c * n:(c + 1) * n, :], in1=tops[m][:].unsqueeze(1).to_broadcast([P, n, W]), op=ALU.subtract)

        def s_exp(m):
            flat = esb[m][:].rearrange("p i j w -> p (i j) w")
            nc.scalar.activation(out=flat, in_=flat, func=ACT.Exp)

        def v_sum(m):
            if SUM_ON_G:
                t_s = sums[m]
            else:
                t_s = smallp.tile([P, W], F32, name="ssum")
                nc.vector.tensor_reduce(out=t_s[:], in_=esb[m][:].rearrange("p i j w -> p w (i j)"), axis=AX.X, op=ALU.add)
            t_r = smallp.tile([P, W], F32, name="rsum")
            nc.vector.reciprocal(out=t_r[:], in_=t_s[:])
            sums[m] = t_r

        def g_sum(m):
            if SUM_ON_G:
                flat = esb[m][:].rearrange("p i j w -> p (i j) w")
                t_f = foldp.tile([P, 4, W], F32, name="fold")
                nc.gpsimd.tensor_tensor(out=t_f[:], in0=flat[:, 0:4, :], in1=flat[:, 4:8, :], op=ALU.add)
                nc.gpsimd.tensor_tensor(out=t_f[:, 0:2, :], in0=t_f[:, 0:2, :], in1=t_f[:, 2:4, :], op=ALU.add)
                nc.gpsimd.tensor_tensor(out=t_f[:, 0, :], in0=t_f[:, 0, :], in1=t_f[:, 1, :], op=ALU.add)
                t_s = smallp.tile([P, W], F32, name="ssum")
                nc.gpsimd.tensor_tensor(out=t_s[:], in0=t_f[:, 0, :], in1=flat[:, 8, :], op=ALU.add)
                sums[m] = t_s

        def v_mul(m):
            flat = esb[m][:].rearrange("p i j w -> p (i j) w")
            for c in range(SM_SPLIT):
                n = WIN // SM_SPLIT
                (nc.vector if m >= SM_V_M else sm_eng).tensor_tensor(out=atts[m % ATT_BUFS][:, c * n:(c + 1) * n, 1:W + 1], in0=flat[:, c * n:(c + 1) * n, :],
                                     in1=sums[m][:].unsqueeze(1).to_broadcast([P, n, W]), op=ALU.mult)

        def s_tout(m):
            t_t = attp.tile([P, W, WIN], F32, name="t_out")
            nc.scalar.copy(out=t_t[:], in_=atts[m % ATT_BUFS][:, :, 1:W + 1].rearrange("p n w -> p w n"))
            for r in range(MBR):
                {"sync": nc.sync, "scalar": nc.scalar, "gpsimd": nc.gpsimd}[T_QUEUE].dma_start(out=o1[:, m * MBR + r, :], in_=t_t[r * NG:(r + 1) * NG, :, :].rearrange("p w n -> p (w n)"))

        def tail(m):
            return m >= TAIL_MB

        def plan(m):
            return TAIL_PLAN if tail(m) else PLAN

        def shv_banks(m):
            return plan(m)["banks"]

        def pe_shv(m, b):
            banks = shv_banks(m)
            if b >= len(banks):
                return
            tag = ("shv", "shw")[b]
            if b == 1 and W_TAG == "qj":
                t_ps = psum.tile([P, len(banks[b]), P], F32, name="sh_ps", tag="qj", bufs=QJ_BUFS)
            else:
                t_ps = psum.tile([P, len(banks[b]), P], F32, name="sh_ps", tag=tag)
            for slot, (i, j) in enumerate(banks[b]):
                nc.tensor.transpose(t_ps[:, slot, :], atts[m % ATT_BUFS][:, 3 * i + j, 2 - j:2 - j + W], ident_f[:])
                sh[(m, i, j)] = (t_ps, slot)

        def pe_shift(m, i):
            js = plan(m)["stage"].get(i, ())
            if js:
                t_ps = aux_tile([P, len(js), P], "sh_ps")
                for slot, j in enumerate(js):
                    nc.tensor.transpose(t_ps[:, slot, :], atts[m % ATT_BUFS][:, 3 * i + j, 2 - j:2 - j + W], ident_f[:])
                sh[(m, i)] = t_ps

        def s_shift(m, i):
            js = plan(m)["stage"].get(i, ())
            if js:
                t_sb = shp.tile([P, 3, P], F32, name="sh_sb")
                nc.scalar.copy(out=t_sb[:, 0:len(js), :], in_=sh[(m, i)][:])
                for slot, j in enumerate(js):
                    sh[(m, i, j)] = (t_sb, slot)

        def av_mul(eng, m, a, i, js):
            h0 = m * MBR + a * R
            t_q = pv[(m, a, i)]
            nj = len(js)
            j0 = js[0]
            jstep = js[1] - js[0] if nj > 1 else 1
            src, s0 = sh[(m, i, j0)]
            sstep = sh[(m, i, js[1])][1] - s0 if nj > 1 else 1
            lo = max(0, 1 - i - h0)
            hi = min(R, H + 1 - i - h0)
            for off, slot, cnt in ring_runs(h0 + lo + i - 1, hi - lo, RV):
                b = lo + off
                x0 = (a * R + b) * NG
                eng.tensor_tensor(
                    out=t_q[:, j0:j0 + (nj - 1) * jstep + 1:jstep, b:b + cnt, :].rearrange("p j r (g c) -> p j (r g) c", c=CG),
                    in0=v_ring[:, slot:slot + cnt, :].rearrange("p r (g c) -> p (r g) c", c=CG).unsqueeze(1).to_broadcast([P, nj, cnt * NG, CG]),
                    in1=src[:, s0:s0 + (nj - 1) * sstep + 1:sstep, x0:x0 + cnt * NG].unsqueeze(3).to_broadcast([P, nj, cnt * NG, CG]),
                    op=ALU.mult)

        def inner(k):
            return 0 < k < NQ - 1

        def av(idx):
            k, s = divmod(idx, 3)
            m, a = divmod(k, QPM)
            if s == 0:
                for i in range(3):
                    t_new = pvp.tile([P, 3, R, P], F32, name="pv%d" % i, tag="pv%d" % i, bufs=PV_BUFS[i])
                    pv[(m, a, i)] = t_new
            for eng, step, i, js in plan(m)["mul"]:
                if step == s:
                    for part in (([(j,) for j in js]) if (eng == "g" and G_SPLIT) else [js]):
                        av_mul(nc.gpsimd if eng == "g" else nc.vector, m, a, i, part)

        def av_add(idx):
            k, s = divmod(idx, 3)
            m, a = divmod(k, QPM)
            if inner(k):
                for eng, step, i, i2, js in plan(m)["add"]:
                    for part in ([(j,) for j in js] if G_SPLIT else [js]) if (eng == "g" and step == s) else ():
                        jj = slice(part[0], part[-1] + 1, part[1] - part[0] if len(part) > 1 else 1)
                        (nc.gpsimd if eng == "g" else nc.vector).tensor_tensor(out=pv[(m, a, i)][:, jj], in0=pv[(m, a, i)][:, jj], in1=pv[(m, a, i2)][:, jj], op=ALU.add)

        def av_vadd(idx):
            k, s = divmod(idx, 3)
            m, a = divmod(k, QPM)
            if inner(k):
                for eng, step, i, i2, js in plan(m)["add"]:
                    if eng == "v" and step == s:
                        jj = slice(js[0], js[-1] + 1, js[1] - js[0] if len(js) > 1 else 1)
                        nc.vector.tensor_tensor(out=pv[(m, a, i)][:, jj], in0=pv[(m, a, i)][:, jj], in1=pv[(m, a, i2)][:, jj], op=ALU.add)

        def s_av(idx):
            k, s = divmod(idx, 3)
            m, a = divmod(k, QPM)
            h0 = m * MBR + a * R
            for i, j in plan(m)["short"]:
                src, sl = sh[(m, i, j)]
                for r in S_ROWS[s]:
                    if 0 <= h0 + r + i - 1 < H:
                        slot = (h0 + r + i - 1) % RV
                        for g in range(NG):
                            x = (a * R + r) * NG + g
                            nc.scalar.activation(out=pv[(m, a, i)][:, j, r, g * CG:(g + 1) * CG], in_=v_ring[:, slot, g * CG:(g + 1) * CG],
                                                 func=ACT.Copy, scale=src[:, sl, x:x + 1])

        def g_eadd(u):
            m, j, a = decode(u)
            cols = slice(a * R * NG, (a + 1) * R * NG)
            for i in EADD_I if m in EADD_MS else ():
                t_p = prod[(m, 3 * i + j)]
                nc.gpsimd.tensor_tensor(out=t_p[:, 0:CG // 2, cols], in0=t_p[:, 0:CG // 2, cols], in1=t_p[:, CG // 2:CG, cols], op=ALU.add)

        awork = {"todo": [], "pos": 0, "tile": None}

        def pe_abegin(k):
            m, a = divmod(k, QPM)
            h0 = m * MBR + a * R
            if k >= OPS_MX_K0:
                t_o = psum.tile([P, R, W], F32, name="o_ps", tag="mx", bufs=MX_BUFS)
            else:
                t_o = psum.tile([P, R, W], F32, name="o_ps", tag="ops")
            if k >= WARM_K0:
                for rep in range(WARM_N):
                    q_pass(NQ - 1, t_o)
            pending = []
            for r in range(R):
                gone = [(i2, j) for eng, step, i, i2, js in plan(m)["add"] for j in js] if inner(k) else []
                terms = [(i, j) for i in A_ROWS for j in range(3) if 0 <= h0 + r + i - 1 < H and (i, j) not in gone]
                for idx, (i, j) in enumerate(terms):
                    pending.append((t_o[:, r, :], pv[(m, a, i)][:, j, r, :], perms[j], idx == 0, idx == len(terms) - 1))
            awork["todo"] = pending
            awork["pos"] = 0
            ps[("o", k)] = t_o

        def pe_asteps(idx):
            work_step(awork, ASTEP)

        def pe_aend(k):
            work_step(awork, len(awork["todo"]))

        def s_osb(k):
            t_sb = outp.tile([P, PIX], F32, name="o_sb")
            nc.scalar.copy(out=t_sb[:], in_=ps[("o", k)][:].rearrange("p r w -> p (r w)"))
            {"sync": nc.sync, "scalar": nc.scalar, "gpsimd": nc.gpsimd}[O_QUEUE].dma_start(out=o0[:, k * PIX:(k + 1) * PIX], in_=t_sb[:])

        def pe_warm(idx):
            t_ps = psum.tile([P, PIX], F32, name="warm_ps", tag="mx", bufs=MX_BUFS)
            for rep in range(WARM_N):
                nc.tensor.matmul_mx(out=t_ps[:], lhsT=w_codes[0][:].bitcast(FP8X4), lhsT_scale=w_scales[0][:],
                                    rhs=xc[NQ - 1][:].bitcast(FP8X4), rhs_scale=xs[NQ - 1][:], start=True, stop=True)

        def only(cond, fn):
            return lambda m: fn(m) if cond(m) else None

        calls = {
            "w_turn": w_turn, "w_quant": w_quant, "rel_mat": rel_mat,
            "pe_mxq": pe_mxq, "pe_mxk": pe_mxk, "pe_mxv": pe_mxv, "s_q": s_q, "g_qlo": g_qlo, "s_k": s_k, "s_v": s_v,
            "pe_qrel": pe_qrel, "s_qr": s_qr,
            "pe_sh0": lambda m: pe_shift(m, 0), "s_sh0": lambda m: s_shift(m, 0),
            "pe_sh2": lambda m: pe_shift(m, 2), "s_sh2": lambda m: s_shift(m, 2),
            "pe_sh1": lambda m: pe_shv(m, 0), "pe_sh2t": lambda m: pe_shv(m, 1), "av_add": av_add, "av_vadd": av_vadd,
            "g_eadd": g_eadd, "s_av": s_av, "v_qlo": v_qlo, "v_red": v_red,
            "pe_abegin": pe_abegin, "pe_asteps": pe_asteps, "pe_asteps0": pe_asteps, "pe_asteps1": pe_asteps, "pe_asteps2": pe_asteps, "pe_aend": pe_aend, "s_osb": s_osb,
            "pe_qshift": pe_qshift, "pe_ebegin": pe_ebegin, "pe_esteps": pe_esteps, "pe_eend": pe_eend, "s_esb": s_esb,
            "v_qk": v_qk, "av": av, "v_quant": v_quant, "v_quant1": lambda q: v_quant(q, 1),
            "s_rg0": lambda q: s_rg(q, 0), "s_rg1": lambda q: s_rg(q, 1), "s_rg2": lambda q: s_rg(q, 2), "s_rg3": lambda q: s_rg(q, 3),
            "pe_warm": pe_warm, "v_max": v_max, "v_sub": v_sub, "s_exp": s_exp, "v_sum": v_sum, "g_sum": g_sum, "v_mul": v_mul, "s_tout": s_tout,
        }
        due = {}
        for name in ORDER:
            base, period, count = OFF[name]
            for idx in range(count):
                head = HEAD.get(name, ())
                u = head[idx] if idx < len(head) else base + period * idx
                due.setdefault(u, []).append((name, idx))
        for u in sorted(due):
            for name, idx in due[u]:
                calls[name](idx)
